import numpy as np
import ml_dtypes


def mxq(x, axis, fmt="e4m3"):
    dtype, down = {"e4m3": (ml_dtypes.float8_e4m3fn, 7), "e5m2": (ml_dtypes.float8_e5m2, 14)}[fmt]
    v = np.moveaxis(np.asarray(x, np.float32).astype(ml_dtypes.bfloat16).astype(np.float64), axis, -1)
    blocks = v.reshape(v.shape[:-1] + (-1, 32))
    amax = np.abs(blocks).max(-1, keepdims=True)
    byte = np.maximum(np.where(amax > 0, np.frexp(amax)[1] - 1 + 127, 0) - down, 1)
    scale = np.exp2(byte - 127.0)
    codes = (blocks / scale).astype(np.float32).astype(dtype).astype(np.float64)
    return np.moveaxis((codes * scale).reshape(v.shape), -1, axis)


WIDE = False


def mx_kscale(k):
    if not WIDE:
        return np.ones(k)
    levels = np.array([10, -10, 5, -5, 0])
    if k % 512:
        return np.exp2(np.random.permutation(np.resize(levels, k // 32))).repeat(32)
    a = np.empty((k // 512, 16))
    for p in range(k // 512):
        a[p, :8] = np.random.permutation(np.resize(levels, 8))
        for g in range(8):
            far = levels[np.abs(levels - a[p, g]) >= 10]
            a[p, g + 8] = far[np.random.randint(len(far))]
    return np.exp2(a.ravel()).repeat(32)


BF16 = ml_dtypes.bfloat16


def bf(x):
    return np.asarray(x, np.float32).astype(BF16)


def f64(x):
    return np.asarray(x).astype(np.float64)


B, T, E, H, DC, KB, DFF = 2, 1024, 1024, 16, 2, 512, 4096
HD = E // H
HALF = H // 2


def mix_matrices(mix_w, decay):
    i = np.arange(T)[:, None]
    j = np.arange(T)[None, :]
    d = np.clip(decay, 0.9, 1.0)
    expo = (j - i) / DC
    dec = d[:, None, None] ** expo
    causal = j >= i
    mcol = np.where(causal, mix_w[:HALF, None, :] * dec[:HALF], 0.0)
    mrow = np.where(causal, mix_w[HALF:, :, None] * dec[HALF:], 0.0)
    return np.concatenate([mcol, mrow], axis=0)


def setup_inputs():
    s = mx_kscale(T)
    u = mx_kscale(E)[::HD]
    st = np.concatenate([np.ones((HALF, T)), np.tile(s, (HALF, 1))], axis=0)
    return {"p": bf(np.random.standard_normal((B, H, T, HD)) / st[None, :, :, None]),
            "mix_w": bf(np.random.standard_normal((H, T)) * 3.0 / np.sqrt(T) * st * u[:, None]),
            "mix_b": bf(np.random.standard_normal((H, T)) * 0.2 * u[:, None]),
            "decay": bf(np.random.permutation(np.linspace(0.8, 1.04, H))),
            "out_w": bf(np.random.standard_normal((E, E)) / np.sqrt(E) / np.repeat(u, HD)[:, None]),
            "out_b": bf(np.random.standard_normal(E) * 0.2),
            "x": bf(np.random.standard_normal((B, T, E)))}


def reference(p, mix_w, mix_b, decay, out_w, out_b, x):
    m = mix_matrices(f64(mix_w), f64(decay))
    pq = mxq(f64(p), 2, "e4m3")
    cols = []
    for s0 in range(0, T, KB):
        s1 = s0 + KB
        mq = mxq(m[:, :s1, s0:s1], 1, "e4m3")
        cols.append(mq.transpose(0, 2, 1) @ pq[:, :, :s1, :])
    mixed = np.concatenate(cols, axis=2) + f64(mix_b)[None, :, :, None]
    c = mixed.transpose(0, 2, 1, 3).reshape(B, T, E)
    y = (mxq(c, 2, "e4m3") @ mxq(f64(out_w), 0, "e4m3")) + f64(out_b)
    return y + f64(x)

@@ -1,0 +1,513 @@
+from contextlib import ExitStack
+
+import concourse.mybir as mybir
+from concourse.masks import make_identity
+
+F32 = mybir.dt.float32
+BF16 = mybir.dt.bfloat16
+I32 = mybir.dt.int32
+U32 = mybir.dt.uint32
+U8 = mybir.dt.uint8
+FP8X4 = mybir.dt.float8_e4m3fn_x4
+ALU = mybir.AluOpType
+ACT = mybir.ActivationFunctionType
+AX = mybir.AxisListType
+
+P = 128
+PACK = 4
+K_PASS = P * PACK
+B, H, T, HD = 2, 16, 1024, 64
+E = H * HD
+HALF_H = H // 2
+CHUNKS = T // P
+PAIRS = H // 2
+N_TILE = 512
+SWEEPS = T // N_TILE
+BLOCKS = N_TILE // P
+UNITS = SWEEPS * H
+GROUPS = E // K_PASS
+GROUP_H = H // GROUPS
+ITEMS = SWEEPS * B * (E // N_TILE) * BLOCKS
+DIAG_ROW = N_TILE + HD
+DIAG_TILES = 3
+
+FLOPS = 2 * B * H * HD * (K_PASS * N_TILE + T * N_TILE) + 2 * B * T * E * E
+
+
+def tile_mixerblock_pa_kernel(tc, p, mix_w, mix_b, decay, out_w, out_b, x, out):
+    nc = tc.nc
+    with ExitStack() as stack:
+        def pool(name, bufs):
+            return stack.enter_context(tc.tile_pool(name=name, bufs=bufs))
+
+        const = pool("const", 1)
+        big_pool = pool("big", 3)
+        p_raw_pool = pool("p_raw", 3)
+        p_grouped_pool = pool("p_grouped", 2)
+        left_pool = pool("left_rows", 4)
+        full_pool = pool("m_full", 3)
+        grouped_pool = pool("grouped", 4)
+        m_pool = pool("m_words", 5)
+        c_pool = pool("c_rows", 2)
+        x_pool = pool("x_stage", 5)
+        y_pool = pool("y_stage", 3)
+        psum_m = stack.enter_context(tc.psum_pool(name="psum_m", bufs=3))
+        psum_mix = stack.enter_context(tc.psum_pool(name="psum_mix", bufs=2))
+        psum_misc = stack.enter_context(tc.psum_pool(name="psum_misc", bufs=3))
+
+        p_raw, p_grouped, w_raw, left_rows, m_full, m_psum = {}, {}, {}, {}, {}, {}
+        m_grouped, m_words, m_scales, mixed, c_rows, c_psum, c_grouped = {}, {}, {}, {}, {}, {}, {}
+        projected, y_turned, turned_back, x_raw = {}, {}, {}, {}
+
+        def load_p(pair):
+            if not 0 <= pair < PAIRS:
+                return
+            p_raw[pair] = p_raw_pool.tile([P, B, 2 * 2, PACK, HD], BF16, name="p_raw")
+            for b in range(B):
+                nc.sync.dma_start(
+                    out=p_raw[pair][:, b, :, :, :].rearrange("q g j f -> q g (j f)"),
+                    in_=p[b, 2 * pair : 2 * pair + 2, :, :].rearrange(
+                        "h (c q j) f -> q (h c) (j f)", q=P, j=PACK
+                    ),
+                )
+
+        def regroup_p(pair, b, engine_copy):
+            if not 0 <= pair < PAIRS:
+                return
+            if b == 0:
+                p_grouped[pair] = p_grouped_pool.tile(
+                    [P, 2 * 2, B, HD, PACK], BF16, name="p_grouped", align_bytes=64
+                )
+            engine_copy(
+                out=p_grouped[pair][:, :, b, :, :],
+                in_=p_raw[pair][:, b, :, :, :].rearrange("q g j f -> q g f j"),
+            )
+
+        def quantise_p(pair):
+            if not 0 <= pair < PAIRS:
+                return
+            nc.vector.quantize_mx(
+                out=p_words[:, pair, :].bitcast(FP8X4),
+                scales=p_scales[:, pair, :],
+                in_=p_grouped[pair][:].rearrange("q g b f j -> q (g b f j)"),
+            )
+
+        def load_out_w(g):
+            w_raw[g] = big_pool.tile([P, PACK, E], BF16, name="w_raw", tag="big", align_bytes=64)
+            nc.sync.dma_start(
+                out=w_raw[g][:],
+                in_=out_w[g * K_PASS : (g + 1) * K_PASS, :].rearrange("(q j) n -> q j n", j=PACK),
+            )
+
+        def quantise_out_w(g):
+            w_grouped = big_pool.tile([P, E, PACK], BF16, name="w_grouped", tag="big", align_bytes=64)
+            nc.vector.tensor_copy(
+                out=w_grouped[:].rearrange("q (c i) j -> q c j i", i=4),
+                in_=w_raw[g][:].rearrange("q j (c i) -> q c j i", i=4),
+            )
+            nc.vector.quantize_mx(
+                out=w_words[:, g, :].bitcast(FP8X4),
+                scales=w_scales[:, g, :],
+                in_=w_grouped[:].rearrange("q n j -> q (n j)"),
+            )
+
+        decay_rows = const.tile([P, H], BF16)
+        nc.sync.dma_start(out=decay_rows[:], in_=decay.partition_broadcast(P))
+        mix_w_rows = const.tile([H, T], BF16)
+        nc.sync.dma_start(out=mix_w_rows[:], in_=mix_w[:, :])
+        w_rows = const.tile([P, P], BF16)
+        nc.sync.dma_start(out=w_rows[:], in_=mix_w.rearrange("h (a q) -> (h a) q", q=P))
+        b_rows = const.tile([P, P], BF16)
+        nc.sync.dma_start(out=b_rows[:], in_=mix_b.rearrange("h (a q) -> (h a) q", q=P))
+        load_out_w(0)
+        load_p(0)
+        load_out_w(1)
+        load_p(1)
+
+        t_int = const.tile([P, CHUNKS], I32)
+        nc.gpsimd.iota(t_int[:], pattern=[[P, CHUNKS]], base=0, channel_multiplier=1)
+        t_index = const.tile([P, CHUNKS], F32)
+        nc.vector.tensor_copy(out=t_index[:], in_=t_int[:])
+        t_row_int = const.tile([P, T], I32)
+        for c in range(2):
+            nc.gpsimd.iota(
+                t_row_int[:, c * K_PASS : (c + 1) * K_PASS].rearrange("p (u q e) -> p u q e", u=2, e=2),
+                pattern=[[2, 2], [PACK, P], [1, 2]],
+                base=c * K_PASS,
+                channel_multiplier=0,
+            )
+        t_row = const.tile([P, T], F32)
+        nc.vector.tensor_copy(out=t_row[:], in_=t_row_int[:])
+        identity_bf16 = const.tile([P, P], BF16)
+        make_identity(nc, identity_bf16[:])
+        identity_f32 = const.tile([P, P], F32)
+        make_identity(nc, identity_f32[:])
+        own_head = identity_f32[0:H, 0:H]
+        late_head = const.tile([H, 1], F32)
+        nc.vector.tensor_reduce(out=late_head[:], in_=own_head[:, HALF_H:H], op=ALU.add, axis=AX.X)
+        early_head = const.tile([H, 1], F32)
+        nc.vector.tensor_reduce(out=early_head[:], in_=own_head[:, 0:HALF_H], op=ALU.add, axis=AX.X)
+        triangle = const.tile([P, 2, HD], BF16)
+        nc.vector.tensor_scalar(
+            out=triangle[:],
+            in0=t_row[:, 0:K_PASS].rearrange("p (u r) -> p u r", u=2)[:, :, 0:HD],
+            scalar1=t_index[:, 0:1],
+            scalar2=None,
+            op0=ALU.is_le,
+        )
+
+        diag_tiles = []
+        for n in range(DIAG_TILES):
+            flat = const.tile([P, BLOCKS * DIAG_ROW], BF16, name="diag_tile%d" % n)
+            nc.vector.memset(flat[:], 0.0)
+            diag_tiles.append(flat[:])
+
+        d_clipped = const.tile([P, H], F32)
+        nc.vector.tensor_scalar(
+            out=d_clipped[:], in0=decay_rows[:], scalar1=0.9, scalar2=1.0, op0=ALU.max, op1=ALU.min
+        )
+        log_d = const.tile([P, H], F32)
+        nc.scalar.activation(out=log_d[:], in_=d_clipped[:], func=ACT.Ln)
+
+        own_product = const.tile([H, H], F32)
+        nc.vector.tensor_tensor(out=own_product[:], in0=log_d[0:H, :], in1=own_head, op=ALU.mult)
+        own_log = const.tile([H, 1], F32)
+        nc.vector.tensor_reduce(out=own_log[:], in_=own_product[:], op=ALU.add, axis=AX.X)
+        own_rate = const.tile([H, 1], F32)
+        nc.vector.tensor_scalar(out=own_rate[:], in0=own_log[:], scalar1=-0.5, scalar2=None, op0=ALU.mult)
+        left_decay = const.tile([H, T], F32)
+        nc.scalar.activation(out=left_decay[:], in_=t_row[0:H, :], func=ACT.Exp, scale=own_rate[:, 0:1])
+        left_factor = const.tile([H, 2, 2, P, 2], F32)
+        for c in range(2):
+            for u in range(2):
+                nc.vector.tensor_scalar(
+                    out=left_factor[:, c, u, :, :],
+                    in0=mix_w_rows[:, c * K_PASS : (c + 1) * K_PASS].rearrange(
+                        "p (q u e) -> p u q e", u=2, e=2
+                    )[:, u, :, :],
+                    scalar1=late_head[:, 0:1],
+                    scalar2=early_head[:, 0:1],
+                    op0=ALU.mult,
+                    op1=ALU.add,
+                )
+        left_all = const.tile([H, T], F32)
+        nc.vector.tensor_tensor(
+            out=left_all[:],
+            in0=left_decay[:],
+            in1=left_factor[:].rearrange("p c u q e -> p (c u q e)"),
+            op=ALU.mult,
+        )
+        parked = [out[b, T - H : T, :] for b in range(SWEEPS)]
+        for sweep in range(SWEEPS):
+            width = (sweep + 1) * K_PASS
+            nc.scalar.dma_start(out=parked[sweep][:, 0:width], in_=left_all[:, 0:width])
+
+        w_turned = psum_misc.tile([P, P], BF16, name="w_turned", tag="misc")
+        nc.tensor.transpose(out=w_turned[:], in_=w_rows[:], identity=identity_bf16[:])
+        w_by_s = const.tile([P, H, CHUNKS], F32)
+        nc.vector.tensor_copy(out=w_by_s[:].rearrange("q h i -> q (h i)"), in_=w_turned[:])
+        b_turned = psum_misc.tile([P, P], BF16, name="b_turned", tag="misc")
+        nc.tensor.transpose(out=b_turned[:], in_=b_rows[:], identity=identity_bf16[:])
+        bias_by_s = const.tile([P, H, CHUNKS], F32)
+        nc.vector.tensor_copy(out=bias_by_s[:].rearrange("q h i -> q (h i)"), in_=b_turned[:])
+
+        exponent = const.tile([P, H, CHUNKS], F32)
+        nc.vector.tensor_tensor(
+            out=exponent[:],
+            in0=t_index[:].unsqueeze(1).to_broadcast([P, H, CHUNKS]),
+            in1=log_d[:].unsqueeze(2).to_broadcast([P, H, CHUNKS]),
+            op=ALU.mult,
+        )
+        right = const.tile([P, H, CHUNKS], F32)
+        nc.scalar.activation(out=right[:], in_=exponent[:], func=ACT.Exp, scale=0.5)
+        nc.vector.tensor_tensor(
+            out=right[:, 0:HALF_H, :], in0=right[:, 0:HALF_H, :], in1=w_by_s[:, 0:HALF_H, :], op=ALU.mult
+        )
+
+        out_b_rows = const.tile([P, P], BF16)
+        nc.vector.memset(out_b_rows[:], 0.0)
+        nc.sync.dma_start(out=out_b_rows[0 : E // P, :], in_=out_b.rearrange("(i q) -> i q", q=P))
+        out_b_turned = psum_misc.tile([P, P], BF16, name="out_b_turned", tag="misc")
+        nc.tensor.transpose(out=out_b_turned[:], in_=out_b_rows[:], identity=identity_bf16[:])
+        out_b_column = const.tile([P, E // P], F32)
+        nc.vector.tensor_copy(out=out_b_column[:], in_=out_b_turned[:, 0 : E // P])
+
+        p_words = const.tile([P, PAIRS, 2 * 2 * B * HD], U32, align_bytes=64)
+        p_scales = const.tile([P, PAIRS, 2 * 2 * B * HD], U8, align_bytes=64)
+        c_words = const.tile([P, B, GROUPS, T], U32, align_bytes=64)
+        c_scales = const.tile([P, B, GROUPS, T], U8, align_bytes=64)
+        w_words = const.tile([P, GROUPS, E], U32, align_bytes=64)
+        w_scales = const.tile([P, GROUPS, E], U8, align_bytes=64)
+
+        def load_left(unit):
+            if not 0 <= unit < UNITS:
+                return
+            sweep, h = divmod(unit, H)
+            width = (sweep + 1) * K_PASS
+            left_rows[unit] = left_pool.tile([P, T], F32, name="left_rows")
+            nc.sync.dma_start(
+                out=left_rows[unit][:, 0:width], in_=parked[sweep][h, 0:width].partition_broadcast(P)
+            )
+
+        def scale_left(on_scalar, dst, src, scale):
+            if on_scalar:
+                nc.scalar.activation(out=dst, in_=src, func=ACT.Copy, scale=scale)
+            else:
+                nc.vector.tensor_scalar(out=dst, in0=src, scalar1=scale, scalar2=None, op0=ALU.mult)
+
+        def chunk_of(unit, c, i):
+            if c == unit // H:
+                return diag_tiles[unit % DIAG_TILES][:, i * N_TILE : (i + 1) * N_TILE]
+            return m_full[unit][:, i, :]
+
+        def make_m(unit):
+            if not 0 <= unit < UNITS:
+                return
+            sweep, h = divmod(unit, H)
+            if sweep > 0:
+                m_full[unit] = full_pool.tile([P, BLOCKS, K_PASS], BF16, name="m_full")
+            for i in range(BLOCKS):
+                scale = right[:, h, sweep * BLOCKS + i : sweep * BLOCKS + i + 1]
+                if sweep > 0:
+                    scale_left(i < 2, chunk_of(unit, 0, i), left_rows[unit][:, 0:K_PASS], scale)
+                width = HD * (i + 1)
+                scale_left(
+                    sweep == 0 and i == 3,
+                    chunk_of(unit, sweep, i).rearrange("p (u r) -> p u r", u=2)[:, :, 0:width],
+                    left_rows[unit][:, sweep * K_PASS : (sweep + 1) * K_PASS].rearrange(
+                        "p (u r) -> p u r", u=2
+                    )[:, :, 0:width],
+                    scale,
+                )
+
+        def mask_m(unit):
+            if not 0 <= unit < UNITS:
+                return
+            blocks = (
+                diag_tiles[unit % DIAG_TILES]
+                .rearrange("p (i r) -> p i r", i=BLOCKS)[:, :, 0:K_PASS]
+                .rearrange("p i (u r) -> p i u r", u=2)[:, :, :, 0:HD]
+            )
+            nc.vector.tensor_tensor(
+                out=blocks,
+                in0=blocks,
+                in1=triangle[:].unsqueeze(1).to_broadcast([P, BLOCKS, 2, HD]),
+                op=ALU.mult,
+            )
+
+        def transpose_m(unit):
+            if not 0 <= unit < UNITS:
+                return
+            for c in range(unit // H + 1):
+                m_grouped[(unit, c)] = grouped_pool.tile(
+                    [P, N_TILE, PACK], BF16, name="m_grouped", tag="grouped", align_bytes=64
+                )
+                for half in range(2):
+                    bank = psum_m.tile([P, 2, 2, P], F32, name="m_psum", tag="m_psum")
+                    for i in range(2):
+                        words = chunk_of(unit, c, 2 * half + i).bitcast(F32)
+                        for u in range(2):
+                            nc.tensor.transpose(
+                                out=bank[:, i, u, :],
+                                in_=words[:, u * P : (u + 1) * P],
+                                identity=identity_f32[:],
+                            )
+                    nc.scalar.copy(
+                        out=m_grouped[(unit, c)][:]
+                        .rearrange("q s j -> q (s j)")
+                        .bitcast(F32)[:, half * N_TILE : (half + 1) * N_TILE]
+                        .rearrange("q (i s u) -> q i s u", i=2, u=2),
+                        in_=bank[:].rearrange("q i u s -> q i s u"),
+                    )
+
+        def quantise_m(unit):
+            if not 0 <= unit < UNITS:
+                return
+            for c in range(unit // H + 1):
+                m_words[(unit, c)] = m_pool.tile([P, N_TILE], U32, name="m_words", align_bytes=64)
+                m_scales[(unit, c)] = m_pool.tile([P, N_TILE], U8, name="m_scales", align_bytes=64)
+                nc.vector.quantize_mx(
+                    out=m_words[(unit, c)][:].bitcast(FP8X4),
+                    scales=m_scales[(unit, c)][:],
+                    in_=m_grouped[(unit, c)][:].rearrange("q s j -> q (s j)"),
+                )
+
+        def multiply(unit):
+            if not 0 <= unit < UNITS:
+                return
+            sweep, h = divmod(unit, H)
+            mixed[unit] = psum_mix.tile([P, N_TILE], F32, name="mixed")
+            for i in range(BLOCKS):
+                steps = slice(i * P, (i + 1) * P)
+                for c in range(sweep + 1):
+                    first = ((h % 2) * 2 + c) * B * HD
+                    cols = slice(first, first + B * HD)
+                    nc.tensor.matmul_mx(
+                        out=mixed[unit][:, steps],
+                        lhsT=m_words[(unit, c)][:, steps].bitcast(FP8X4),
+                        lhsT_scale=m_scales[(unit, c)][:, steps],
+                        rhs=p_words[:, h // 2, cols].bitcast(FP8X4),
+                        rhs_scale=p_scales[:, h // 2, cols],
+                        start=(c == 0),
+                        stop=(c == sweep),
+                    )
+
+        def add_bias(unit):
+            if not 0 <= unit < UNITS:
+                return
+            sweep, h = divmod(unit, H)
+            g, h_in_group = divmod(h, GROUP_H)
+            if h_in_group == 0:
+                c_rows[(sweep, g)] = c_pool.tile([P, BLOCKS, B, K_PASS], BF16, name="c_rows")
+            nc.vector.tensor_tensor(
+                out=c_rows[(sweep, g)][:, :, :, h_in_group * HD : (h_in_group + 1) * HD],
+                in0=mixed[unit][:].rearrange("p (i b f) -> p i b f", i=BLOCKS, b=B),
+                in1=bias_by_s[:, h, sweep * BLOCKS : (sweep + 1) * BLOCKS]
+                .unsqueeze(2)
+                .unsqueeze(3)
+                .to_broadcast([P, BLOCKS, B, HD]),
+                op=ALU.add,
+            )
+
+        def transpose_c(bank):
+            if not 0 <= bank < SWEEPS * GROUPS * B * 2:
+                return
+            sweep, g, b, half = bank // 8, bank // 4 % 2, bank // 2 % 2, bank % 2
+            if half == 0:
+                c_grouped[bank] = grouped_pool.tile(
+                    [P, N_TILE, PACK], BF16, name="c_grouped", tag="grouped", align_bytes=64
+                )
+                c_grouped[bank + 1] = c_grouped[bank]
+            turned = psum_misc.tile([P, 2, 2, P], F32, name="c_turned", tag="misc")
+            for i in range(2):
+                words = c_rows[(sweep, g)][:, 2 * half + i, b, :].bitcast(F32)
+                for u in range(2):
+                    nc.tensor.transpose(
+                        out=turned[:, i, u, :], in_=words[:, u : 2 * P : 2], identity=identity_f32[:]
+                    )
+            nc.scalar.copy(
+                out=c_grouped[bank][:]
+                .rearrange("q s j -> q (s j)")
+                .bitcast(F32)[:, half * N_TILE : (half + 1) * N_TILE]
+                .rearrange("q (i s u) -> q i s u", i=2, u=2),
+                in_=turned[:].rearrange("q i u s -> q i s u"),
+            )
+
+        def quantise_c(bank):
+            if not (0 <= bank < SWEEPS * GROUPS * B * 2 and bank % 2 == 1):
+                return
+            sweep, g, b = bank // 8, bank // 4 % 2, bank // 2 % 2
+            cols = slice(sweep * N_TILE, (sweep + 1) * N_TILE)
+            nc.vector.quantize_mx(
+                out=c_words[:, b, g, cols].bitcast(FP8X4),
+                scales=c_scales[:, b, g, cols],
+                in_=c_grouped[bank][:].rearrange("q s j -> q (s j)"),
+            )
+
+        def patch_of(item):
+            sweep, rest = divmod(item // BLOCKS, B * 2)
+            return sweep, rest // 2, rest % 2
+
+        def project(item):
+            if not 0 <= item < ITEMS:
+                return
+            sweep, b, n_half = patch_of(item)
+            n_block = n_half * BLOCKS + item % BLOCKS
+            cols = slice(n_block * P, (n_block + 1) * P)
+            steps = slice(sweep * N_TILE, (sweep + 1) * N_TILE)
+            projected[item] = psum_misc.tile([P, N_TILE], F32, name="projected", tag="misc")
+            for g in range(GROUPS):
+                nc.tensor.matmul_mx(
+                    out=projected[item][:],
+                    lhsT=w_words[:, g, cols].bitcast(FP8X4),
+                    lhsT_scale=w_scales[:, g, cols],
+                    rhs=c_words[:, b, g, steps].bitcast(FP8X4),
+                    rhs_scale=c_scales[:, b, g, steps],
+                    start=(g == 0),
+                    stop=(g == GROUPS - 1),
+                )
+
+        def add_out_b(item):
+            if not 0 <= item < ITEMS:
+                return
+            patch, i = divmod(item, BLOCKS)
+            n_block = patch_of(item)[2] * BLOCKS + i
+            if i == 0:
+                y_turned[patch] = big_pool.tile(
+                    [P, BLOCKS, N_TILE], F32, name="y_turned", tag="big", align_bytes=64
+                )
+            nc.scalar.activation(
+                out=y_turned[patch][:, i, :],
+                in_=projected[item][:],
+                func=ACT.Identity,
+                bias=out_b_column[:, n_block : n_block + 1],
+            )
+
+        def rows_and_cols(item):
+            sweep, b, n_half = patch_of(item)
+            first = sweep * N_TILE + (item % BLOCKS) * P
+            return b, slice(first, first + P), slice(n_half * N_TILE, (n_half + 1) * N_TILE)
+
+        def load_x(item):
+            if not 0 <= item < ITEMS:
+                return
+            b, rows, cols = rows_and_cols(item)
+            x_raw[item] = x_pool.tile([P, N_TILE], BF16, name="x_raw")
+            nc.sync.dma_start(out=x_raw[item][:], in_=x[b, rows, cols])
+
+        def turn_back(item):
+            if not 0 <= item < ITEMS:
+                return
+            patch, block = divmod(item, BLOCKS)
+            turned_back[item] = psum_misc.tile([P, N_TILE], F32, name="turned_back", tag="misc")
+            for i in range(BLOCKS):
+                nc.tensor.transpose(
+                    out=turned_back[item][:, i * P : (i + 1) * P],
+                    in_=y_turned[patch][:, i, block * P : (block + 1) * P],
+                    identity=identity_f32[:],
+                )
+
+        def add_x_and_store(item):
+            if not 0 <= item < ITEMS:
+                return
+            b, rows, cols = rows_and_cols(item)
+            y = y_pool.tile([P, N_TILE], F32)
+            nc.vector.tensor_tensor(out=y[:], in0=turned_back[item][:], in1=x_raw[item][:], op=ALU.add)
+            nc.sync.dma_start(out=out[b, rows, cols], in_=y[:])
+
+        last_bank = -2
+        with tc.manual_schedule():
+            quantise_out_w(0)
+            load_left(0)
+            load_left(1)
+            regroup_p(0, 0, nc.vector.tensor_copy)
+            regroup_p(0, 1, nc.vector.tensor_copy)
+            load_left(2)
+            quantise_p(0)
+            quantise_out_w(1)
+            for step in range(-2, UNITS + 26):
+                item = step - 20
+                pair, odd = divmod(step + 3, 2)
+                turn, bank = divmod(step - 9, 8)
+                bank = 4 * turn + bank if bank < 4 else -2
+                load_left(step + 5)
+                load_x(item - 3)
+                if odd:
+                    load_p(pair + 2)
+                if pair > 0:
+                    regroup_p(pair, odd, nc.scalar.copy if odd else nc.vector.tensor_copy)
+                make_m(step + 2)
+                mask_m(step + 2)
+                transpose_m(step + 1)
+                transpose_c(bank)
+                turn_back(item - 5)
+                quantise_m(step)
+                if pair > 1 and not odd:
+                    quantise_p(pair - 1)
+                quantise_c(last_bank)
+                last_bank = bank
+                add_bias(step - 1)
+                multiply(step)
+                project(item)
+                add_out_b(item - 1)
+                add_x_and_store(item - 6)

@@ -24,12 +24,22 @@ PAIRS = H // 2
 N_TILE = 512
 SWEEPS = T // N_TILE
 BLOCKS = N_TILE // P
-UNITS = SWEEPS * H
 GROUPS = E // K_PASS
 GROUP_H = H // GROUPS
 ITEMS = SWEEPS * B * (E // N_TILE) * BLOCKS
-DIAG_ROW = N_TILE + HD
-DIAG_TILES = 3
+HALVES = 2
+STEPS = SWEEPS * H
+VARIANT_TILES = 3
+
+MAX_BLOCKS = 7
+CHUNKS_OF = ((0, 1, 1, 2), (2, 3, 0, 3))
+ROW_WIDTH = ((256, 512), (768, 1024))
+M_ROWS = 4608
+ON_SCALAR = (((0, 3), (0, 1), (1, 0)), ((0, 0), (1, 1), (1, 0)))
+
+
+def DRAIN_ON_VECTOR(sweep, half, n):
+    return False
 
 FLOPS = 2 * B * H * HD * (K_PASS * N_TILE + T * N_TILE) + 2 * B * T * E * E
 
@@ -42,12 +52,12 @@ def tile_mixerblock_pa_kernel(tc, p, mix_w, mix_b, decay, out_w, out_b, x, out):
 
         const = pool("const", 1)
         big_pool = pool("big", 3)
-        p_raw_pool = pool("p_raw", 3)
+        p_raw_pool = pool("p_raw", 2)
         p_grouped_pool = pool("p_grouped", 2)
-        left_pool = pool("left_rows", 4)
-        full_pool = pool("m_full", 3)
-        grouped_pool = pool("grouped", 4)
-        m_pool = pool("m_words", 5)
+        left_pool = pool("left_rows", 6)
+        rows_pool = pool("m_rows", 4)
+        grouped_pool = pool("m_grouped", 3)
+        m_pool = pool("m_words", 3)
         c_pool = pool("c_rows", 2)
         x_pool = pool("x_stage", 5)
         y_pool = pool("y_stage", 3)
@@ -55,32 +65,47 @@ def tile_mixerblock_pa_kernel(tc, p, mix_w, mix_b, decay, out_w, out_b, x, out):
         psum_mix = stack.enter_context(tc.psum_pool(name="psum_mix", bufs=2))
         psum_misc = stack.enter_context(tc.psum_pool(name="psum_misc", bufs=3))
 
-        p_raw, p_grouped, w_raw, left_rows, m_full, m_psum = {}, {}, {}, {}, {}, {}
-        m_grouped, m_words, m_scales, mixed, c_rows, c_psum, c_grouped = {}, {}, {}, {}, {}, {}, {}
+        p_raw, p_grouped, w_raw, w_grouped, left_rows, m_rows, blocks = {}, {}, {}, {}, {}, {}, {}
+        m_grouped, m_words, m_scales, mixed, c_rows, c_grouped = {}, {}, {}, {}, {}, {}
         projected, y_turned, turned_back, x_raw = {}, {}, {}, {}
+
+        p_words = const.tile([P, PAIRS, 2 * 2 * B * HD], U32, align_bytes=64)
+        p_scales = const.tile([P, PAIRS, 2 * 2 * B * HD], U8, align_bytes=64)
+        c_words = const.tile([P, B, GROUPS, T], U32, align_bytes=64)
+        c_scales = const.tile([P, B, GROUPS, T], U8, align_bytes=64)
+        w_words = const.tile([P, GROUPS, E], U32, align_bytes=64)
+        w_scales = const.tile([P, GROUPS, E], U8, align_bytes=64)
+        variants = [
+            const.tile([P, 3, 2, B * HD], U32, name="variants%d" % n, align_bytes=64)
+            for n in range(VARIANT_TILES)
+        ]
 
         def load_p(pair):
             if not 0 <= pair < PAIRS:
                 return
-            p_raw[pair] = p_raw_pool.tile([P, B, 2 * 2, PACK, HD], BF16, name="p_raw")
+            p_raw[pair] = p_raw_pool.tile([P, B, 2, 2, PACK * HD], BF16, name="p_raw")
             for b in range(B):
                 nc.sync.dma_start(
-                    out=p_raw[pair][:, b, :, :, :].rearrange("q g j f -> q g (j f)"),
-                    in_=p[b, 2 * pair : 2 * pair + 2, :, :].rearrange(
-                        "h (c q j) f -> q (h c) (j f)", q=P, j=PACK
-                    ),
+                    out=p_raw[pair][:, b, 0, :, :],
+                    in_=p[b, 2 * pair, :, :].rearrange("(c q j) f -> q c (j f)", q=P, j=PACK),
                 )
+            for b in range(B):
+                source = p[b, 2 * pair + 1, :, :].rearrange("(c a r j) f -> a r c (j f)", a=4, r=32, j=PACK)
+                for a in range(4):
+                    nc.sync.dma_start(
+                        out=p_raw[pair][32 * (3 - a) : 32 * (4 - a), b, 1, :, :], in_=source[a]
+                    )
 
         def regroup_p(pair, b, engine_copy):
             if not 0 <= pair < PAIRS:
                 return
             if b == 0:
                 p_grouped[pair] = p_grouped_pool.tile(
-                    [P, 2 * 2, B, HD, PACK], BF16, name="p_grouped", align_bytes=64
+                    [P, 2 * 2, B, HD, PACK], BF16, name="p_grouped", tag="p_grouped", align_bytes=64
                 )
             engine_copy(
                 out=p_grouped[pair][:, :, b, :, :],
-                in_=p_raw[pair][:, b, :, :, :].rearrange("q g j f -> q g f j"),
+                in_=p_raw[pair][:, b, :, :, :].rearrange("q h c (j f) -> q (h c) f j", j=PACK),
             )
 
         def quantise_p(pair):
@@ -92,6 +117,23 @@ def tile_mixerblock_pa_kernel(tc, p, mix_w, mix_b, decay, out_w, out_b, x, out):
                 in_=p_grouped[pair][:].rearrange("q g b f j -> q (g b f j)"),
             )
 
+        def p_cols(odd, c):
+            first = (2 * odd + c) * B * HD
+            return slice(first, first + B * HD)
+
+        def copy_variants(unit):
+            if not 0 <= unit < SWEEPS * PAIRS:
+                return
+            sweep, pair = divmod(unit, PAIRS)
+            tile = variants[unit % VARIANT_TILES]
+            for v in range(3):
+                for odd in range(2):
+                    rows = slice(32 * (v + 1), P) if odd else slice(0, 32 * (v + 1))
+                    nc.sync.dma_start(
+                        out=tile[rows, v, odd, :].bitcast(I32),
+                        in_=p_words[rows, pair, p_cols(odd, sweep)].bitcast(I32),
+                    )
+
         def load_out_w(g):
             w_raw[g] = big_pool.tile([P, PACK, E], BF16, name="w_raw", tag="big", align_bytes=64)
             nc.sync.dma_start(
@@ -99,286 +141,215 @@ def tile_mixerblock_pa_kernel(tc, p, mix_w, mix_b, decay, out_w, out_b, x, out):
                 in_=out_w[g * K_PASS : (g + 1) * K_PASS, :].rearrange("(q j) n -> q j n", j=PACK),
             )
 
-        def quantise_out_w(g):
-            w_grouped = big_pool.tile([P, E, PACK], BF16, name="w_grouped", tag="big", align_bytes=64)
-            nc.vector.tensor_copy(
-                out=w_grouped[:].rearrange("q (c i) j -> q c j i", i=4),
+        def regroup_out_w(g, engine_copy):
+            w_grouped[g] = big_pool.tile([P, E, PACK], BF16, name="w_grouped", tag="big", align_bytes=64)
+            engine_copy(
+                out=w_grouped[g][:].rearrange("q (c i) j -> q c j i", i=4),
                 in_=w_raw[g][:].rearrange("q j (c i) -> q c j i", i=4),
             )
+
+        def quantise_out_w(g):
             nc.vector.quantize_mx(
                 out=w_words[:, g, :].bitcast(FP8X4),
                 scales=w_scales[:, g, :],
-                in_=w_grouped[:].rearrange("q n j -> q (n j)"),
+                in_=w_grouped[g][:].rearrange("q n j -> q (n j)"),
             )
 
-        decay_rows = const.tile([P, H], BF16)
-        nc.sync.dma_start(out=decay_rows[:], in_=decay.partition_broadcast(P))
-        mix_w_rows = const.tile([H, T], BF16)
-        nc.sync.dma_start(out=mix_w_rows[:], in_=mix_w[:, :])
-        w_rows = const.tile([P, P], BF16)
-        nc.sync.dma_start(out=w_rows[:], in_=mix_w.rearrange("h (a q) -> (h a) q", q=P))
-        b_rows = const.tile([P, P], BF16)
-        nc.sync.dma_start(out=b_rows[:], in_=mix_b.rearrange("h (a q) -> (h a) q", q=P))
-        load_out_w(0)
-        load_p(0)
-        load_out_w(1)
-        load_p(1)
-
-        t_int = const.tile([P, CHUNKS], I32)
-        nc.gpsimd.iota(t_int[:], pattern=[[P, CHUNKS]], base=0, channel_multiplier=1)
-        t_index = const.tile([P, CHUNKS], F32)
-        nc.vector.tensor_copy(out=t_index[:], in_=t_int[:])
-        t_row_int = const.tile([P, T], I32)
-        for c in range(2):
-            nc.gpsimd.iota(
-                t_row_int[:, c * K_PASS : (c + 1) * K_PASS].rearrange("p (u q e) -> p u q e", u=2, e=2),
-                pattern=[[2, 2], [PACK, P], [1, 2]],
-                base=c * K_PASS,
-                channel_multiplier=0,
-            )
-        t_row = const.tile([P, T], F32)
-        nc.vector.tensor_copy(out=t_row[:], in_=t_row_int[:])
-        identity_bf16 = const.tile([P, P], BF16)
-        make_identity(nc, identity_bf16[:])
-        identity_f32 = const.tile([P, P], F32)
-        make_identity(nc, identity_f32[:])
-        own_head = identity_f32[0:H, 0:H]
-        late_head = const.tile([H, 1], F32)
-        nc.vector.tensor_reduce(out=late_head[:], in_=own_head[:, HALF_H:H], op=ALU.add, axis=AX.X)
-        early_head = const.tile([H, 1], F32)
-        nc.vector.tensor_reduce(out=early_head[:], in_=own_head[:, 0:HALF_H], op=ALU.add, axis=AX.X)
-        triangle = const.tile([P, 2, HD], BF16)
-        nc.vector.tensor_scalar(
-            out=triangle[:],
-            in0=t_row[:, 0:K_PASS].rearrange("p (u r) -> p u r", u=2)[:, :, 0:HD],
-            scalar1=t_index[:, 0:1],
-            scalar2=None,
-            op0=ALU.is_le,
-        )
-
-        diag_tiles = []
-        for n in range(DIAG_TILES):
-            flat = const.tile([P, BLOCKS * DIAG_ROW], BF16, name="diag_tile%d" % n)
-            nc.vector.memset(flat[:], 0.0)
-            diag_tiles.append(flat[:])
-
-        d_clipped = const.tile([P, H], F32)
-        nc.vector.tensor_scalar(
-            out=d_clipped[:], in0=decay_rows[:], scalar1=0.9, scalar2=1.0, op0=ALU.max, op1=ALU.min
-        )
-        log_d = const.tile([P, H], F32)
-        nc.scalar.activation(out=log_d[:], in_=d_clipped[:], func=ACT.Ln)
-
-        own_product = const.tile([H, H], F32)
-        nc.vector.tensor_tensor(out=own_product[:], in0=log_d[0:H, :], in1=own_head, op=ALU.mult)
-        own_log = const.tile([H, 1], F32)
-        nc.vector.tensor_reduce(out=own_log[:], in_=own_product[:], op=ALU.add, axis=AX.X)
-        own_rate = const.tile([H, 1], F32)
-        nc.vector.tensor_scalar(out=own_rate[:], in0=own_log[:], scalar1=-0.5, scalar2=None, op0=ALU.mult)
-        left_decay = const.tile([H, T], F32)
-        nc.scalar.activation(out=left_decay[:], in_=t_row[0:H, :], func=ACT.Exp, scale=own_rate[:, 0:1])
-        left_factor = const.tile([H, 2, 2, P, 2], F32)
-        for c in range(2):
-            for u in range(2):
-                nc.vector.tensor_scalar(
-                    out=left_factor[:, c, u, :, :],
-                    in0=mix_w_rows[:, c * K_PASS : (c + 1) * K_PASS].rearrange(
-                        "p (q u e) -> p u q e", u=2, e=2
-                    )[:, u, :, :],
-                    scalar1=late_head[:, 0:1],
-                    scalar2=early_head[:, 0:1],
-                    op0=ALU.mult,
-                    op1=ALU.add,
-                )
-        left_all = const.tile([H, T], F32)
-        nc.vector.tensor_tensor(
-            out=left_all[:],
-            in0=left_decay[:],
-            in1=left_factor[:].rearrange("p c u q e -> p (c u q e)"),
-            op=ALU.mult,
-        )
-        parked = [out[b, T - H : T, :] for b in range(SWEEPS)]
-        for sweep in range(SWEEPS):
-            width = (sweep + 1) * K_PASS
-            nc.scalar.dma_start(out=parked[sweep][:, 0:width], in_=left_all[:, 0:width])
-
-        w_turned = psum_misc.tile([P, P], BF16, name="w_turned", tag="misc")
-        nc.tensor.transpose(out=w_turned[:], in_=w_rows[:], identity=identity_bf16[:])
-        w_by_s = const.tile([P, H, CHUNKS], F32)
-        nc.vector.tensor_copy(out=w_by_s[:].rearrange("q h i -> q (h i)"), in_=w_turned[:])
-        b_turned = psum_misc.tile([P, P], BF16, name="b_turned", tag="misc")
-        nc.tensor.transpose(out=b_turned[:], in_=b_rows[:], identity=identity_bf16[:])
-        bias_by_s = const.tile([P, H, CHUNKS], F32)
-        nc.vector.tensor_copy(out=bias_by_s[:].rearrange("q h i -> q (h i)"), in_=b_turned[:])
-
-        exponent = const.tile([P, H, CHUNKS], F32)
-        nc.vector.tensor_tensor(
-            out=exponent[:],
-            in0=t_index[:].unsqueeze(1).to_broadcast([P, H, CHUNKS]),
-            in1=log_d[:].unsqueeze(2).to_broadcast([P, H, CHUNKS]),
-            op=ALU.mult,
-        )
-        right = const.tile([P, H, CHUNKS], F32)
-        nc.scalar.activation(out=right[:], in_=exponent[:], func=ACT.Exp, scale=0.5)
-        nc.vector.tensor_tensor(
-            out=right[:, 0:HALF_H, :], in0=right[:, 0:HALF_H, :], in1=w_by_s[:, 0:HALF_H, :], op=ALU.mult
-        )
-
-        out_b_rows = const.tile([P, P], BF16)
-        nc.vector.memset(out_b_rows[:], 0.0)
-        nc.sync.dma_start(out=out_b_rows[0 : E // P, :], in_=out_b.rearrange("(i q) -> i q", q=P))
-        out_b_turned = psum_misc.tile([P, P], BF16, name="out_b_turned", tag="misc")
-        nc.tensor.transpose(out=out_b_turned[:], in_=out_b_rows[:], identity=identity_bf16[:])
-        out_b_column = const.tile([P, E // P], F32)
-        nc.vector.tensor_copy(out=out_b_column[:], in_=out_b_turned[:, 0 : E // P])
-
-        p_words = const.tile([P, PAIRS, 2 * 2 * B * HD], U32, align_bytes=64)
-        p_scales = const.tile([P, PAIRS, 2 * 2 * B * HD], U8, align_bytes=64)
-        c_words = const.tile([P, B, GROUPS, T], U32, align_bytes=64)
-        c_scales = const.tile([P, B, GROUPS, T], U8, align_bytes=64)
-        w_words = const.tile([P, GROUPS, E], U32, align_bytes=64)
-        w_scales = const.tile([P, GROUPS, E], U8, align_bytes=64)
+        def unit_of(step):
+            return step // H, step % H // 2, step % 2
 
         def load_left(unit):
-            if not 0 <= unit < UNITS:
+            if not 0 <= unit < SWEEPS * PAIRS:
                 return
-            sweep, h = divmod(unit, H)
-            width = (sweep + 1) * K_PASS
-            left_rows[unit] = left_pool.tile([P, T], F32, name="left_rows")
-            nc.sync.dma_start(
-                out=left_rows[unit][:, 0:width], in_=parked[sweep][h, 0:width].partition_broadcast(P)
-            )
-
-        def scale_left(on_scalar, dst, src, scale):
-            if on_scalar:
-                nc.scalar.activation(out=dst, in_=src, func=ACT.Copy, scale=scale)
-            else:
-                nc.vector.tensor_scalar(out=dst, in0=src, scalar1=scale, scalar2=None, op0=ALU.mult)
-
-        def chunk_of(unit, c, i):
-            if c == unit // H:
-                return diag_tiles[unit % DIAG_TILES][:, i * N_TILE : (i + 1) * N_TILE]
-            return m_full[unit][:, i, :]
-
-        def make_m(unit):
-            if not 0 <= unit < UNITS:
-                return
-            sweep, h = divmod(unit, H)
-            if sweep > 0:
-                m_full[unit] = full_pool.tile([P, BLOCKS, K_PASS], BF16, name="m_full")
-            for i in range(BLOCKS):
-                scale = right[:, h, sweep * BLOCKS + i : sweep * BLOCKS + i + 1]
-                if sweep > 0:
-                    scale_left(i < 2, chunk_of(unit, 0, i), left_rows[unit][:, 0:K_PASS], scale)
-                width = HD * (i + 1)
-                scale_left(
-                    sweep == 0 and i == 3,
-                    chunk_of(unit, sweep, i).rearrange("p (u r) -> p u r", u=2)[:, :, 0:width],
-                    left_rows[unit][:, sweep * K_PASS : (sweep + 1) * K_PASS].rearrange(
-                        "p (u r) -> p u r", u=2
-                    )[:, :, 0:width],
-                    scale,
+            sweep, pair = divmod(unit, PAIRS)
+            for odd in range(2):
+                h = 2 * pair + odd
+                first, last = (0, 2 * 256) if sweep else ((256, 512) if odd else (0, 256))
+                left_rows[(unit, odd)] = left_pool.tile([P, 2, 2 * 256], F32, name="left_rows")
+                nc.sync.dma_start(
+                    out=left_rows[(unit, odd)][:, :, first:last],
+                    in_=parked[sweep][h].rearrange("(u v) -> u v", u=2)[:, first:last].partition_broadcast(P),
                 )
 
-        def mask_m(unit):
-            if not 0 <= unit < UNITS:
+        def make_m(step):
+            if not 0 <= step < STEPS:
                 return
-            blocks = (
-                diag_tiles[unit % DIAG_TILES]
-                .rearrange("p (i r) -> p i r", i=BLOCKS)[:, :, 0:K_PASS]
-                .rearrange("p i (u r) -> p i u r", u=2)[:, :, :, 0:HD]
+            sweep, pair, half = unit_of(step)
+            tile = rows_pool.tile([P, M_ROWS], BF16, name="m_rows", align_bytes=64)
+            m_rows[step] = tile
+            width = ROW_WIDTH[sweep][half]
+
+            def part(row, first, last):
+                base = (row - 2 * half) * 2 * width
+                return tile[:, base : base + 2 * width].rearrange("p (u v) -> p u v", u=2)[:, :, first:last]
+
+            def scale_left(odd, chunk, dst, first, last):
+                h = 2 * pair + odd
+                i = sweep * BLOCKS + chunk
+                src = left_rows[(step // 2, odd)][:, :, first:last]
+                scale = right[:, h, i : i + 1]
+                if (odd, chunk) in ON_SCALAR[sweep]:
+                    nc.scalar.activation(out=dst, in_=src, func=ACT.Copy, scale=scale)
+                else:
+                    nc.vector.tensor_scalar(out=dst, in0=src, scalar1=scale, scalar2=None, op0=ALU.mult)
+
+            for row in (2 * half, 2 * half + 1):
+                edge = HD * (row + 1)
+                if sweep == 0 and row < 3:
+                    scale_left(0, row, part(row, 0, edge), 0, edge)
+                    scale_left(1, 2 - row, part(row, edge, 256), 256 + edge, 512)
+                elif sweep == 0:
+                    scale_left(0, 3, part(3, 0, 256), 0, 256)
+                    scale_left(1, 3, part(3, 256, 512), 256, 512)
+                elif row < 3:
+                    scale_left(0, row, part(row, 0, 256 + edge), 0, 256 + edge)
+                    scale_left(1, 2 - row, part(row, 256 + edge, 768), edge, 512)
+                else:
+                    scale_left(0, 3, part(3, 0, 512), 0, 512)
+                    scale_left(1, 3, part(3, 512, 1024), 0, 512)
+
+        def mask_m(step):
+            if not 0 <= step < STEPS:
+                return
+            sweep, pair, half = unit_of(step)
+            width = ROW_WIDTH[sweep][half]
+            first = 256 * sweep + 2 * half * HD
+            pieces = (
+                m_rows[step][:, first : first + 2 * (2 * width + HD)]
+                .rearrange("p (r v) -> p r v", r=2)[:, :, 0 : 2 * width]
+                .rearrange("p r (u v) -> p r u v", u=2)[:, :, :, 0 : 2 * HD]
             )
             nc.vector.tensor_tensor(
-                out=blocks,
-                in0=blocks,
-                in1=triangle[:].unsqueeze(1).to_broadcast([P, BLOCKS, 2, HD]),
+                out=pieces,
+                in0=pieces,
+                in1=triangles[:].unsqueeze(1).to_broadcast([P, 2, 2, 2 * HD]),
                 op=ALU.mult,
             )
 
-        def transpose_m(unit):
-            if not 0 <= unit < UNITS:
-                return
-            for c in range(unit // H + 1):
-                m_grouped[(unit, c)] = grouped_pool.tile(
-                    [P, N_TILE, PACK], BF16, name="m_grouped", tag="grouped", align_bytes=64
-                )
-                for half in range(2):
-                    bank = psum_m.tile([P, 2, 2, P], F32, name="m_psum", tag="m_psum")
-                    for i in range(2):
-                        words = chunk_of(unit, c, 2 * half + i).bitcast(F32)
-                        for u in range(2):
-                            nc.tensor.transpose(
-                                out=bank[:, i, u, :],
-                                in_=words[:, u * P : (u + 1) * P],
-                                identity=identity_f32[:],
-                            )
-                    nc.scalar.copy(
-                        out=m_grouped[(unit, c)][:]
-                        .rearrange("q s j -> q (s j)")
-                        .bitcast(F32)[:, half * N_TILE : (half + 1) * N_TILE]
-                        .rearrange("q (i s u) -> q i s u", i=2, u=2),
-                        in_=bank[:].rearrange("q i u s -> q i s u"),
-                    )
+        def block_list(sweep, half):
+            if sweep == 0:
+                if half == 0:
+                    return [("X", 0, 0, 0), ("X", 1, 1, 0)]
+                return [("X", 2, 2, 0), ("A", 3, 3, 0), ("B", 3, 3, 256)]
+            if half == 0:
+                rows, tail = (0, 1), []
+            else:
+                rows = (2,)
+                tail = [("A full", 3, 3, 0), ("A", 3, 3, 256), ("B", 3, 3, 512), ("B full", 3, 3, 768)]
+            found = []
+            for row in rows:
+                found += [("A full", row, row, 0), ("X", row, row, 256), ("B full", 2 - row, row, 512)]
+            return found + tail
 
-        def quantise_m(unit):
-            if not 0 <= unit < UNITS:
+        def transpose_m(step):
+            if not 0 <= step < STEPS:
                 return
-            for c in range(unit // H + 1):
-                m_words[(unit, c)] = m_pool.tile([P, N_TILE], U32, name="m_words", align_bytes=64)
-                m_scales[(unit, c)] = m_pool.tile([P, N_TILE], U8, name="m_scales", align_bytes=64)
-                nc.vector.quantize_mx(
-                    out=m_words[(unit, c)][:].bitcast(FP8X4),
-                    scales=m_scales[(unit, c)][:],
-                    in_=m_grouped[(unit, c)][:].rearrange("q s j -> q (s j)"),
-                )
-
-        def multiply(unit):
-            if not 0 <= unit < UNITS:
-                return
-            sweep, h = divmod(unit, H)
-            mixed[unit] = psum_mix.tile([P, N_TILE], F32, name="mixed")
-            for i in range(BLOCKS):
-                steps = slice(i * P, (i + 1) * P)
-                for c in range(sweep + 1):
-                    first = ((h % 2) * 2 + c) * B * HD
-                    cols = slice(first, first + B * HD)
-                    nc.tensor.matmul_mx(
-                        out=mixed[unit][:, steps],
-                        lhsT=m_words[(unit, c)][:, steps].bitcast(FP8X4),
-                        lhsT_scale=m_scales[(unit, c)][:, steps],
-                        rhs=p_words[:, h // 2, cols].bitcast(FP8X4),
-                        rhs_scale=p_scales[:, h // 2, cols],
-                        start=(c == 0),
-                        stop=(c == sweep),
-                    )
-
-        def add_bias(unit):
-            if not 0 <= unit < UNITS:
-                return
-            sweep, h = divmod(unit, H)
-            g, h_in_group = divmod(h, GROUP_H)
-            if h_in_group == 0:
-                c_rows[(sweep, g)] = c_pool.tile([P, BLOCKS, B, K_PASS], BF16, name="c_rows")
-            nc.vector.tensor_tensor(
-                out=c_rows[(sweep, g)][:, :, :, h_in_group * HD : (h_in_group + 1) * HD],
-                in0=mixed[unit][:].rearrange("p (i b f) -> p i b f", i=BLOCKS, b=B),
-                in1=bias_by_s[:, h, sweep * BLOCKS : (sweep + 1) * BLOCKS]
-                .unsqueeze(2)
-                .unsqueeze(3)
-                .to_broadcast([P, BLOCKS, B, HD]),
-                op=ALU.add,
+            sweep, pair, half = unit_of(step)
+            width = ROW_WIDTH[sweep][half]
+            found = block_list(sweep, half)
+            words = m_rows[step][:].bitcast(F32)
+            m_grouped[step] = grouped_pool.tile(
+                [P, MAX_BLOCKS * P, PACK], BF16, name="m_grouped", align_bytes=64
             )
+            out_words = m_grouped[step][:].rearrange("q s j -> q (s j)").bitcast(F32)
+            for n in range(0, len(found), 2):
+                count = min(2, len(found) - n)
+                bank = psum_m.tile([P, 2, 2, P], F32, name="m_psum", tag="m_psum")
+                for i in range(count):
+                    what, chunk, row, first = found[n + i]
+                    for u in range(2):
+                        start = ((row - 2 * half) * 2 * width + u * width + first) // 2
+                        nc.tensor.transpose(
+                            out=bank[:, i, u, :], in_=words[:, start : start + P], identity=identity_f32[:]
+                        )
+                drain = nc.vector.tensor_copy if DRAIN_ON_VECTOR(sweep, half, n) else nc.scalar.copy
+                drain(
+                    out=out_words[:, 256 * n : 256 * (n + count)].rearrange(
+                        "q (i s u) -> q i s u", i=count, u=2
+                    ),
+                    in_=bank[:, 0:count, :, :].rearrange("q i u s -> q i s u"),
+                )
+
+        def quantise_m(step):
+            if not 0 <= step < STEPS:
+                return
+            sweep, pair, half = unit_of(step)
+            found = block_list(sweep, half)
+            m_words[step] = m_pool.tile([P, MAX_BLOCKS * P], U32, name="m_words", align_bytes=64)
+            m_scales[step] = m_pool.tile([P, MAX_BLOCKS * P], U8, name="m_scales", align_bytes=64)
+            source = m_grouped[step][:].rearrange("q s j -> q (s j)")
+            first = 0
+            for count in (4, 2, 1):
+                if len(found) & count:
+                    cols = slice(first * P, (first + count) * P)
+                    nc.vector.quantize_mx(
+                        out=m_words[step][:, cols].bitcast(FP8X4),
+                        scales=m_scales[step][:, cols],
+                        in_=source[:, first * K_PASS : (first + count) * K_PASS],
+                    )
+                    first += count
+
+        def multiply(step):
+            if not 0 <= step < STEPS:
+                return
+            sweep, pair, half = unit_of(step)
+            slots = {(what, chunk): n for n, (what, chunk, row, first) in enumerate(block_list(sweep, half))}
+            tile = variants[(step // 2) % VARIANT_TILES]
+            mixed[step] = psum_mix.tile([P, BLOCKS, B * HD], F32, name="mixed")
+            for n in range(BLOCKS):
+                odd, chunk = n // 2, CHUNKS_OF[half][n]
+                own = "AB"[odd]
+                passes = []
+                if sweep > 0:
+                    passes.append((slots[(own + " full", chunk)], p_words[:, pair, p_cols(odd, 0)], p_cols(odd, 0)))
+                if chunk == 3:
+                    passes.append((slots[(own, 3)], p_words[:, pair, p_cols(odd, sweep)], p_cols(odd, sweep)))
+                else:
+                    v = 2 - chunk if odd else chunk
+                    passes.append((slots[("X", v)], tile[:, v, odd, :], p_cols(odd, sweep)))
+                for k, (slot, moving, scale_cols) in enumerate(passes):
+                    cols = slice(slot * P, (slot + 1) * P)
+                    nc.tensor.matmul_mx(
+                        out=mixed[step][:, n, :],
+                        lhsT=m_words[step][:, cols].bitcast(FP8X4),
+                        lhsT_scale=m_scales[step][:, cols],
+                        rhs=moving.bitcast(FP8X4),
+                        rhs_scale=p_scales[:, pair, scale_cols],
+                        start=(k == 0),
+                        stop=(k == len(passes) - 1),
+                    )
+
+        def add_bias(step):
+            if not 0 <= step < STEPS:
+                return
+            sweep, pair, half = unit_of(step)
+            g, pair_in_group = divmod(pair, PAIRS // GROUPS)
+            if half == 0 and pair_in_group == 0:
+                c_rows[(sweep, g)] = c_pool.tile([P, BLOCKS, B, K_PASS], BF16, name="c_rows")
+            for odd in range(2):
+                first, second = CHUNKS_OF[half][2 * odd : 2 * odd + 2]
+                picked = slice(first, second + 1, second - first)
+                cols = slice((2 * pair_in_group + odd) * HD, (2 * pair_in_group + odd + 1) * HD)
+                nc.vector.tensor_tensor(
+                    out=c_rows[(sweep, g)][:, picked, :, cols],
+                    in0=mixed[step][:, 2 * odd : 2 * odd + 2, :].rearrange("p i (b f) -> p i b f", b=B),
+                    in1=bias_by_s[:, 2 * pair + odd, sweep * BLOCKS : (sweep + 1) * BLOCKS][:, picked]
+                    .unsqueeze(2)
+                    .unsqueeze(3)
+                    .to_broadcast([P, 2, B, HD]),
+                    op=ALU.add,
+                )
 
         def transpose_c(bank):
             if not 0 <= bank < SWEEPS * GROUPS * B * 2:
                 return
             sweep, g, b, half = bank // 8, bank // 4 % 2, bank // 2 % 2, bank % 2
             if half == 0:
-                c_grouped[bank] = grouped_pool.tile(
-                    [P, N_TILE, PACK], BF16, name="c_grouped", tag="grouped", align_bytes=64
+                c_grouped[bank] = p_grouped_pool.tile(
+                    [P, N_TILE, PACK], BF16, name="c_grouped", tag="p_grouped", align_bytes=64
                 )
                 c_grouped[bank + 1] = c_grouped[bank]
-            turned = psum_misc.tile([P, 2, 2, P], F32, name="c_turned", tag="misc")
+            turned = psum_m.tile([P, 2, 2, P], F32, name="c_turned", tag="m_psum")
             for i in range(2):
                 words = c_rows[(sweep, g)][:, 2 * half + i, b, :].bitcast(F32)
                 for u in range(2):
@@ -475,35 +446,183 @@ def tile_mixerblock_pa_kernel(tc, p, mix_w, mix_b, decay, out_w, out_b, x, out):
             nc.vector.tensor_tensor(out=y[:], in0=turned_back[item][:], in1=x_raw[item][:], op=ALU.add)
             nc.sync.dma_start(out=out[b, rows, cols], in_=y[:])
 
-        last_bank = -2
+
         with tc.manual_schedule():
-            quantise_out_w(0)
+            warm = const.tile([P, 1], F32)
+            nc.vector.memset(warm[:], 1.0)
+            nc.scalar.activation(out=warm[:], in_=warm[:], func=ACT.Ln)
+
+            own_decay = const.tile([H, 1], BF16)
+            nc.sync.dma_start(out=own_decay[:], in_=decay.rearrange("(h o) -> h o", o=1))
+            decay_rows = const.tile([P, H], BF16)
+            nc.sync.dma_start(out=decay_rows[:], in_=decay.partition_broadcast(P))
+            mix_w_rows = const.tile([H, T], BF16)
+            nc.sync.dma_start(out=mix_w_rows[:], in_=mix_w[:, :])
+            load_out_w(0)
+            load_p(0)
+            w_rows = const.tile([P, P], BF16)
+            nc.sync.dma_start(out=w_rows[:], in_=mix_w.rearrange("h (a q) -> (h a) q", q=P))
+            b_rows = const.tile([P, P], BF16)
+            nc.sync.dma_start(out=b_rows[:], in_=mix_b.rearrange("h (a q) -> (h a) q", q=P))
+            load_out_w(1)
+            load_p(1)
+
+            t_int = left_pool.tile([H, T], I32, name="t_int", tag="left_rows")
+            nc.gpsimd.iota(t_int[:], pattern=[[1, T]], base=0, channel_multiplier=0)
+            head_int = const.tile([H, 1], I32)
+            nc.gpsimd.iota(head_int[:], pattern=[[0, 1]], base=0, channel_multiplier=1)
+            s_int = const.tile([P, CHUNKS], I32)
+            nc.gpsimd.iota(s_int[:], pattern=[[P, CHUNKS]], base=0, channel_multiplier=1)
+            t_in_block_int = const.tile([P, 2, HD // 2, 2], I32)
+            nc.gpsimd.iota(t_in_block_int[:], pattern=[[2, 2], [PACK, HD // 2], [1, 2]], base=0, channel_multiplier=0)
+            identity_f32 = const.tile([P, P], F32)
+            make_identity(nc, identity_f32[:])
+            identity_bf16 = const.tile([P, P], BF16)
+            make_identity(nc, identity_bf16[:])
+            for tile in variants:
+                nc.gpsimd.memset(tile[:].rearrange("q v h n -> q (v h n)").bitcast(I32), 0)
+
+            own_clipped = const.tile([H, 1], F32)
+            nc.vector.tensor_scalar(
+                out=own_clipped[:], in0=own_decay[:], scalar1=0.9, scalar2=1.0, op0=ALU.max, op1=ALU.min
+            )
+            own_log = const.tile([H, 1], F32)
+            nc.scalar.activation(out=own_log[:], in_=own_clipped[:], func=ACT.Ln)
+            d_clipped = const.tile([P, H], F32)
+            nc.vector.tensor_scalar(
+                out=d_clipped[:], in0=decay_rows[:], scalar1=0.9, scalar2=1.0, op0=ALU.max, op1=ALU.min
+            )
+            log_d = const.tile([P, H], F32)
+            nc.scalar.activation(out=log_d[:], in_=d_clipped[:], func=ACT.Ln)
+
+            t_row = left_pool.tile([H, T], F32, name="t_row", tag="left_rows")
+            nc.vector.tensor_copy(out=t_row[:], in_=t_int[:])
+            own_rate = const.tile([H, 1], F32)
+            nc.vector.tensor_scalar(out=own_rate[:], in0=own_log[:], scalar1=-0.5, scalar2=None, op0=ALU.mult)
+            nc.scalar.activation(out=t_row[:], in_=t_row[:], func=ACT.Exp, scale=own_rate[:, 0:1])
+            late_head = const.tile([H, 1], F32)
+            nc.vector.tensor_scalar(
+                out=late_head[:], in0=head_int[:], scalar1=float(HALF_H), scalar2=None, op0=ALU.is_ge
+            )
+            early_head = const.tile([H, 1], F32)
+            nc.vector.tensor_scalar(
+                out=early_head[:], in0=head_int[:], scalar1=float(HALF_H), scalar2=None, op0=ALU.is_lt
+            )
+            factor = left_pool.tile([H, T], F32, name="factor", tag="left_rows")
+            nc.vector.tensor_scalar(
+                out=factor[:],
+                in0=mix_w_rows[:],
+                scalar1=late_head[:, 0:1],
+                scalar2=early_head[:, 0:1],
+                op0=ALU.mult,
+                op1=ALU.add,
+            )
+            left_even = left_pool.tile([H, 2, 2 * 256], F32, name="left_even", tag="left_rows")
+            left_odd = left_pool.tile([H, 2, 2 * 256], F32, name="left_odd", tag="left_rows")
+            parked = [out[b, T - H : T, :] for b in range(SWEEPS)]
+            for c in range(2):
+                for odd in range(2):
+                    first = 256 * (1 - c) if odd else 256 * c
+                    for u in range(2):
+                        dst = (left_odd if odd else left_even)[:, u, first : first + 256]
+                        views = [
+                            source[:, c * K_PASS : (c + 1) * K_PASS].rearrange(
+                                "h (a r u e) -> h u a r e", a=4, u=2, e=2
+                            )[:, u, :: (-1 if odd else 1), :, :]
+                            for source in (t_row, factor)
+                        ]
+                        nc.vector.tensor_tensor(
+                            out=dst.rearrange("h (a r e) -> h a r e", a=4, e=2),
+                            in0=views[0],
+                            in1=views[1],
+                            op=ALU.mult,
+                        )
+                for odd in range(2):
+                    first = (256 * (1 - c) if odd else 256 * c) if c == 0 else 0
+                    last = first + 256 if c == 0 else 512
+                    nc.scalar.dma_start(
+                        out=parked[c].rearrange("h (u v) -> h u v", u=2)[odd:H:2, :, first:last],
+                        in_=(left_odd if odd else left_even)[odd:H:2, :, first:last],
+                    )
+
+            s_index = const.tile([P, CHUNKS], F32)
+            nc.vector.tensor_copy(out=s_index[:], in_=s_int[:])
+            w_turned = psum_misc.tile([P, P], BF16, name="w_turned", tag="misc")
+            nc.tensor.transpose(out=w_turned[:], in_=w_rows[:], identity=identity_bf16[:])
+            b_turned = psum_misc.tile([P, P], BF16, name="b_turned", tag="misc")
+            nc.tensor.transpose(out=b_turned[:], in_=b_rows[:], identity=identity_bf16[:])
+
+            exponent = const.tile([P, H, CHUNKS], F32)
+            nc.vector.tensor_tensor(
+                out=exponent[:],
+                in0=s_index[:].unsqueeze(1).to_broadcast([P, H, CHUNKS]),
+                in1=log_d[:].unsqueeze(2).to_broadcast([P, H, CHUNKS]),
+                op=ALU.mult,
+            )
+            right = const.tile([P, H, CHUNKS], F32)
+            nc.scalar.activation(out=right[:], in_=exponent[:], func=ACT.Exp, scale=0.5)
             load_left(0)
             load_left(1)
+
+            t_in_block = const.tile([P, 2, HD], F32)
+            nc.vector.tensor_copy(out=t_in_block[:], in_=t_in_block_int[:].rearrange("q u r e -> q u (r e)"))
+            triangles = const.tile([P, 2, 2 * HD], BF16)
+            for n in range(2):
+                nc.vector.tensor_scalar(
+                    out=triangles[:, :, n * HD : (n + 1) * HD],
+                    in0=t_in_block[:],
+                    scalar1=s_index[:, 0:1],
+                    scalar2=None,
+                    op0=ALU.is_le,
+                )
+
+            w_by_s = const.tile([P, H, CHUNKS], F32)
+            nc.vector.tensor_copy(out=w_by_s[:].rearrange("q h i -> q (h i)"), in_=w_turned[:])
+            nc.vector.tensor_tensor(
+                out=right[:, 0:HALF_H, :], in0=right[:, 0:HALF_H, :], in1=w_by_s[:, 0:HALF_H, :], op=ALU.mult
+            )
+            bias_by_s = const.tile([P, H, CHUNKS], F32)
+            nc.vector.tensor_copy(out=bias_by_s[:].rearrange("q h i -> q (h i)"), in_=b_turned[:])
+
             regroup_p(0, 0, nc.vector.tensor_copy)
             regroup_p(0, 1, nc.vector.tensor_copy)
-            load_left(2)
             quantise_p(0)
-            quantise_out_w(1)
-            for step in range(-2, UNITS + 26):
+            copy_variants(0)
+            regroup_out_w(0, nc.vector.tensor_copy)
+            quantise_out_w(0)
+            regroup_out_w(1, nc.scalar.copy)
+
+            out_b_rows = const.tile([P, P], BF16)
+            nc.gpsimd.memset(out_b_rows[:], 0.0)
+            nc.sync.dma_start(out=out_b_rows[0 : E // P, :], in_=out_b.rearrange("(i q) -> i q", q=P))
+            out_b_turned = psum_misc.tile([P, P], BF16, name="out_b_turned", tag="misc")
+            nc.tensor.transpose(out=out_b_turned[:], in_=out_b_rows[:], identity=identity_bf16[:])
+            out_b_column = const.tile([P, E // P], F32)
+            nc.vector.tensor_copy(out=out_b_column[:], in_=out_b_turned[:, 0 : E // P])
+
+            last_bank = -2
+            for step in range(-3, STEPS + 26):
                 item = step - 20
                 pair, odd = divmod(step + 3, 2)
                 turn, bank = divmod(step - 9, 8)
                 bank = 4 * turn + bank if bank < 4 else -2
-                load_left(step + 5)
-                load_x(item - 3)
-                if odd:
+                if not odd:
+                    load_left(pair + 2)
                     load_p(pair + 2)
-                if pair > 0:
-                    regroup_p(pair, odd, nc.scalar.copy if odd else nc.vector.tensor_copy)
-                make_m(step + 2)
+                load_x(item - 3)
+                make_m(step + 3)
                 mask_m(step + 2)
+                regroup_p(pair + 1, odd, nc.scalar.copy if odd else nc.vector.tensor_copy)
                 transpose_m(step + 1)
                 transpose_c(bank)
                 turn_back(item - 5)
                 quantise_m(step)
-                if pair > 1 and not odd:
-                    quantise_p(pair - 1)
+                if step == -2:
+                    quantise_out_w(1)
+                if not odd and pair > 0:
+                    quantise_p(pair)
+                if not odd and pair > 0:
+                    copy_variants(pair)
                 quantise_c(last_bank)
                 last_bank = bank
                 add_bias(step - 1)

@@ -22,24 +22,22 @@ HALF_H = H // 2
 CHUNKS = T // P
 PAIRS = H // 2
 N_TILE = 512
-SWEEPS = T // N_TILE
-BLOCKS = N_TILE // P
+BLOCKS = K_PASS // P
+SWEEPS = 4
+STEPS = SWEEPS * PAIRS
 GROUPS = E // K_PASS
-GROUP_H = H // GROUPS
-ITEMS = SWEEPS * B * (E // N_TILE) * BLOCKS
-HALVES = 2
-STEPS = SWEEPS * H
-VARIANT_TILES = 3
-
+GROUP_PAIRS = PAIRS // GROUPS
+ITEMS = SWEEPS * (E // P)
 MAX_BLOCKS = 7
-CHUNKS_OF = ((0, 1, 1, 2), (2, 3, 0, 3))
 ROW_WIDTH = ((256, 512), (768, 1024))
-M_ROWS = 4608
-ON_SCALAR = (((0, 3), (0, 1), (1, 0)), ((0, 0), (1, 1), (1, 0)))
-
-
-def DRAIN_ON_VECTOR(sweep, half, n):
-    return False
+M_ROWS = 4672
+VARIANT_COPIES = (
+    (-2, 0, 0, 0, 2), (-2, 0, 2, 0, 2), (0, 0, 0, 2, 4), (0, 0, 2, 2, 4),
+    (2, 0, 0, 4, 6), (2, 0, 2, 4, 6), (4, 0, 0, 6, 8), (4, 0, 2, 6, 8),
+    (5, 0, 1, 0, 8), (12, 1, 0, 0, 4), (12, 1, 2, 0, 4), (16, 1, 0, 4, 8), (16, 1, 2, 4, 8), (17, 1, 1, 0, 8),
+)
+DRAIN_ON_VECTOR = ()
+ON_SCALAR = (((0, 2), (1, 2)), ((0, 3), (0, 1)), ((0, 0), (1, 0)), ((0, 3),))
 
 FLOPS = 2 * B * H * HD * (K_PASS * N_TILE + T * N_TILE) + 2 * B * T * E * E
 
@@ -51,15 +49,15 @@ def tile_mixerblock_pa_kernel(tc, p, mix_w, mix_b, decay, out_w, out_b, x, out):
             return stack.enter_context(tc.tile_pool(name=name, bufs=bufs))
 
         const = pool("const", 1)
-        big_pool = pool("big", 3)
-        p_raw_pool = pool("p_raw", 2)
+        big_pool = pool("big", 2)
+        p_raw_pool = pool("p_raw", 1)
         p_grouped_pool = pool("p_grouped", 2)
-        left_pool = pool("left_rows", 6)
-        rows_pool = pool("m_rows", 4)
+        left_pool = pool("left_rows", 3)
+        rows_pool = pool("m_rows", 3)
         grouped_pool = pool("m_grouped", 3)
         m_pool = pool("m_words", 3)
         c_pool = pool("c_rows", 2)
-        x_pool = pool("x_stage", 5)
+        x_pool = pool("x_stage", 4)
         y_pool = pool("y_stage", 3)
         psum_m = stack.enter_context(tc.psum_pool(name="psum_m", bufs=3))
         psum_mix = stack.enter_context(tc.psum_pool(name="psum_mix", bufs=2))
@@ -69,70 +67,56 @@ def tile_mixerblock_pa_kernel(tc, p, mix_w, mix_b, decay, out_w, out_b, x, out):
         m_grouped, m_words, m_scales, mixed, c_rows, c_grouped = {}, {}, {}, {}, {}, {}
         projected, y_turned, turned_back, x_raw = {}, {}, {}, {}
 
-        p_words = const.tile([P, PAIRS, 2 * 2 * B * HD], U32, align_bytes=64)
-        p_scales = const.tile([P, PAIRS, 2 * 2 * B * HD], U8, align_bytes=64)
-        c_words = const.tile([P, B, GROUPS, T], U32, align_bytes=64)
-        c_scales = const.tile([P, B, GROUPS, T], U8, align_bytes=64)
+        p_words = const.tile([P, 2 * PAIRS, 2 * B * HD], U32, align_bytes=64)
+        p_scales = const.tile([P, 2 * PAIRS, 2 * B * HD], U8, align_bytes=64)
+        c_words = const.tile([P, GROUPS, SWEEPS, N_TILE], U32, align_bytes=64)
+        c_scales = const.tile([P, GROUPS, SWEEPS, N_TILE], U8, align_bytes=64)
         w_words = const.tile([P, GROUPS, E], U32, align_bytes=64)
         w_scales = const.tile([P, GROUPS, E], U8, align_bytes=64)
-        variants = [
-            const.tile([P, 3, 2, B * HD], U32, name="variants%d" % n, align_bytes=64)
-            for n in range(VARIANT_TILES)
-        ]
+        variants = const.tile([P, 3, PAIRS, 2 * B * HD], U32, align_bytes=64)
 
-        def load_p(pair):
-            if not 0 <= pair < PAIRS:
-                return
-            p_raw[pair] = p_raw_pool.tile([P, B, 2, 2, PACK * HD], BF16, name="p_raw")
-            for b in range(B):
-                nc.sync.dma_start(
-                    out=p_raw[pair][:, b, 0, :, :],
-                    in_=p[b, 2 * pair, :, :].rearrange("(c q j) f -> q c (j f)", q=P, j=PACK),
-                )
-            for b in range(B):
-                source = p[b, 2 * pair + 1, :, :].rearrange("(c a r j) f -> a r c (j f)", a=4, r=32, j=PACK)
-                for a in range(4):
-                    nc.sync.dma_start(
-                        out=p_raw[pair][32 * (3 - a) : 32 * (4 - a), b, 1, :, :], in_=source[a]
-                    )
+        def load_p(c):
+            p_raw[c] = p_raw_pool.tile([P, 2, B * PAIRS, PACK * HD], BF16, name="p_raw")
+            steps = slice(c * K_PASS, (c + 1) * K_PASS)
+            heads = p.rearrange("b (r h) t f -> h (b r) t f", h=2)
+            nc.sync.dma_start(
+                out=p_raw[c][:, 0, :, :], in_=heads[0][:, steps, :].rearrange("n (q j) f -> q n (j f)", j=PACK)
+            )
+            source = heads[1][:, steps, :].rearrange("n (a r j) f -> a r n (j f)", a=BLOCKS, j=PACK)
+            for a in range(BLOCKS):
+                rows = slice(32 * (3 - a), 32 * (4 - a))
+                nc.sync.dma_start(out=p_raw[c][rows, 1, :, :], in_=source[a])
 
-        def regroup_p(pair, b, engine_copy):
-            if not 0 <= pair < PAIRS:
-                return
-            if b == 0:
-                p_grouped[pair] = p_grouped_pool.tile(
-                    [P, 2 * 2, B, HD, PACK], BF16, name="p_grouped", tag="p_grouped", align_bytes=64
+        def regroup_p(part, odd, engine_copy):
+            c, pair = divmod(part, PAIRS)
+            if odd == 0:
+                p_grouped[part] = p_grouped_pool.tile(
+                    [P, 2, B, HD, PACK], BF16, name="p_grouped", tag="p_grouped", align_bytes=64
                 )
             engine_copy(
-                out=p_grouped[pair][:, :, b, :, :],
-                in_=p_raw[pair][:, b, :, :, :].rearrange("q h c (j f) -> q (h c) f j", j=PACK),
+                out=p_grouped[part][:, odd, :, :, :],
+                in_=p_raw[c][:, odd, :, :]
+                .rearrange("q (b r) v -> q b r v", b=B)[:, :, pair, :]
+                .rearrange("q b (j f) -> q b f j", j=PACK),
             )
 
-        def quantise_p(pair):
-            if not 0 <= pair < PAIRS:
-                return
+        def quantise_p(part):
             nc.vector.quantize_mx(
-                out=p_words[:, pair, :].bitcast(FP8X4),
-                scales=p_scales[:, pair, :],
-                in_=p_grouped[pair][:].rearrange("q g b f j -> q (g b f j)"),
+                out=p_words[:, part, :].bitcast(FP8X4),
+                scales=p_scales[:, part, :],
+                in_=p_grouped[part][:].rearrange("q h b f j -> q (h b f j)"),
             )
 
-        def p_cols(odd, c):
-            first = (2 * odd + c) * B * HD
-            return slice(first, first + B * HD)
+        def p_cols(odd):
+            return slice(odd * B * HD, (odd + 1) * B * HD)
 
-        def copy_variants(unit):
-            if not 0 <= unit < SWEEPS * PAIRS:
-                return
-            sweep, pair = divmod(unit, PAIRS)
-            tile = variants[unit % VARIANT_TILES]
-            for v in range(3):
-                for odd in range(2):
-                    rows = slice(32 * (v + 1), P) if odd else slice(0, 32 * (v + 1))
-                    nc.sync.dma_start(
-                        out=tile[rows, v, odd, :].bitcast(I32),
-                        in_=p_words[rows, pair, p_cols(odd, sweep)].bitcast(I32),
-                    )
+        def copy_variants(c, v, pairs):
+            for odd in range(2):
+                rows = slice(32 * (v + 1), P) if odd else slice(0, 32 * (v + 1))
+                nc.sync.dma_start(
+                    out=variants[rows, v, pairs, p_cols(odd)].bitcast(I32),
+                    in_=p_words[rows, c * PAIRS + pairs.start : c * PAIRS + pairs.stop, p_cols(odd)].bitcast(I32),
+                )
 
         def load_out_w(g):
             w_raw[g] = big_pool.tile([P, PACK, E], BF16, name="w_raw", tag="big", align_bytes=64)
@@ -142,7 +126,7 @@ def tile_mixerblock_pa_kernel(tc, p, mix_w, mix_b, decay, out_w, out_b, x, out):
             )
 
         def regroup_out_w(g, engine_copy):
-            w_grouped[g] = big_pool.tile([P, E, PACK], BF16, name="w_grouped", tag="big", align_bytes=64)
+            w_grouped[g] = rows_pool.tile([P, E, PACK], BF16, name="w_grouped", tag="m_rows", align_bytes=64)
             engine_copy(
                 out=w_grouped[g][:].rearrange("q (c i) j -> q c j i", i=4),
                 in_=w_raw[g][:].rearrange("q j (c i) -> q c j i", i=4),
@@ -155,52 +139,51 @@ def tile_mixerblock_pa_kernel(tc, p, mix_w, mix_b, decay, out_w, out_b, x, out):
                 in_=w_grouped[g][:].rearrange("q n j -> q (n j)"),
             )
 
-        def unit_of(step):
-            return step // H, step % H // 2, step % 2
+        def place_of(step):
+            return step // PAIRS // 2, step // PAIRS % 2, step % PAIRS
 
-        def load_left(unit):
-            if not 0 <= unit < SWEEPS * PAIRS:
+        def load_left(step):
+            if not 0 <= step < STEPS:
                 return
-            sweep, pair = divmod(unit, PAIRS)
-            for odd in range(2):
-                h = 2 * pair + odd
-                first, last = (0, 2 * 256) if sweep else ((256, 512) if odd else (0, 256))
-                left_rows[(unit, odd)] = left_pool.tile([P, 2, 2 * 256], F32, name="left_rows")
-                nc.sync.dma_start(
-                    out=left_rows[(unit, odd)][:, :, first:last],
-                    in_=parked[sweep][h].rearrange("(u v) -> u v", u=2)[:, first:last].partition_broadcast(P),
-                )
+            c, half, pair = place_of(step)
+            width = 2 * K_PASS * (c + 1)
+            tile = left_pool.tile([P, 2 * T], F32, name="left_rows", tag="left_rows")
+            nc.sync.dma_start(
+                out=tile[:, 0:width],
+                in_=parked[step // PAIRS].rearrange("n v -> (n v)")[pair * width : (pair + 1) * width].partition_broadcast(P),
+            )
+            left_rows[step] = tile[:, 0:width].rearrange("p (h u v) -> p h u v", h=2, u=2)
 
         def make_m(step):
             if not 0 <= step < STEPS:
                 return
-            sweep, pair, half = unit_of(step)
-            tile = rows_pool.tile([P, M_ROWS], BF16, name="m_rows", align_bytes=64)
+            c, half, pair = place_of(step)
+            tile = rows_pool.tile([P, M_ROWS], BF16, name="m_rows", tag="m_rows", align_bytes=64)
             m_rows[step] = tile
-            width = ROW_WIDTH[sweep][half]
+            width = ROW_WIDTH[c][half]
 
             def part(row, first, last):
-                base = (row - 2 * half) * 2 * width
+                base = row // 2 * 2 * width
                 return tile[:, base : base + 2 * width].rearrange("p (u v) -> p u v", u=2)[:, :, first:last]
 
             def scale_left(odd, chunk, dst, first, last):
                 h = 2 * pair + odd
-                i = sweep * BLOCKS + chunk
-                src = left_rows[(step // 2, odd)][:, :, first:last]
+                i = c * BLOCKS + chunk
+                src = left_rows[step][:, odd, :, first:last]
                 scale = right[:, h, i : i + 1]
-                if (odd, chunk) in ON_SCALAR[sweep]:
+                if (odd, chunk) in ON_SCALAR[step // PAIRS]:
                     nc.scalar.activation(out=dst, in_=src, func=ACT.Copy, scale=scale)
                 else:
                     nc.vector.tensor_scalar(out=dst, in0=src, scalar1=scale, scalar2=None, op0=ALU.mult)
 
-            for row in (2 * half, 2 * half + 1):
+            for row in (half, half + 2):
                 edge = HD * (row + 1)
-                if sweep == 0 and row < 3:
+                if c == 0 and row < 3:
                     scale_left(0, row, part(row, 0, edge), 0, edge)
-                    scale_left(1, 2 - row, part(row, edge, 256), 256 + edge, 512)
-                elif sweep == 0:
+                    scale_left(1, 2 - row, part(row, edge, 256), edge, 256)
+                elif c == 0:
                     scale_left(0, 3, part(3, 0, 256), 0, 256)
-                    scale_left(1, 3, part(3, 256, 512), 256, 512)
+                    scale_left(1, 3, part(3, 256, 512), 0, 256)
                 elif row < 3:
                     scale_left(0, row, part(row, 0, 256 + edge), 0, 256 + edge)
                     scale_left(1, 2 - row, part(row, 256 + edge, 768), edge, 512)
@@ -211,11 +194,11 @@ def tile_mixerblock_pa_kernel(tc, p, mix_w, mix_b, decay, out_w, out_b, x, out):
         def mask_m(step):
             if not 0 <= step < STEPS:
                 return
-            sweep, pair, half = unit_of(step)
-            width = ROW_WIDTH[sweep][half]
-            first = 256 * sweep + 2 * half * HD
+            c, half, pair = place_of(step)
+            width = ROW_WIDTH[c][half]
+            first = 256 * c + half * HD
             pieces = (
-                m_rows[step][:, first : first + 2 * (2 * width + HD)]
+                m_rows[step][:, first : first + 2 * (2 * width + 2 * HD)]
                 .rearrange("p (r v) -> p r v", r=2)[:, :, 0 : 2 * width]
                 .rearrange("p r (u v) -> p r u v", u=2)[:, :, :, 0 : 2 * HD]
             )
@@ -226,27 +209,26 @@ def tile_mixerblock_pa_kernel(tc, p, mix_w, mix_b, decay, out_w, out_b, x, out):
                 op=ALU.mult,
             )
 
-        def block_list(sweep, half):
-            if sweep == 0:
-                if half == 0:
-                    return [("X", 0, 0, 0), ("X", 1, 1, 0)]
-                return [("X", 2, 2, 0), ("A", 3, 3, 0), ("B", 3, 3, 256)]
-            if half == 0:
-                rows, tail = (0, 1), []
-            else:
-                rows = (2,)
-                tail = [("A full", 3, 3, 0), ("A", 3, 3, 256), ("B", 3, 3, 512), ("B full", 3, 3, 768)]
+        def block_list(c, half):
+            rows = (half,) if half else (0, 2)
             found = []
             for row in rows:
-                found += [("A full", row, row, 0), ("X", row, row, 256), ("B full", 2 - row, row, 512)]
-            return found + tail
+                if c == 1:
+                    found.append(("A full", row, row, 0))
+                found.append(("X", row, row, 256 * c))
+                if c == 1:
+                    found.append(("B full", 2 - row, row, 512))
+            if half:
+                names = ("A full", "A", "B", "B full") if c == 1 else ("A", "B")
+                found += [(name, 3, 3, 256 * n) for n, name in enumerate(names)]
+            return found
 
         def transpose_m(step):
             if not 0 <= step < STEPS:
                 return
-            sweep, pair, half = unit_of(step)
-            width = ROW_WIDTH[sweep][half]
-            found = block_list(sweep, half)
+            c, half, pair = place_of(step)
+            width = ROW_WIDTH[c][half]
+            found = block_list(c, half)
             words = m_rows[step][:].bitcast(F32)
             m_grouped[step] = grouped_pool.tile(
                 [P, MAX_BLOCKS * P, PACK], BF16, name="m_grouped", align_bytes=64
@@ -258,11 +240,11 @@ def tile_mixerblock_pa_kernel(tc, p, mix_w, mix_b, decay, out_w, out_b, x, out):
                 for i in range(count):
                     what, chunk, row, first = found[n + i]
                     for u in range(2):
-                        start = ((row - 2 * half) * 2 * width + u * width + first) // 2
+                        start = (row // 2 * 2 * width + u * width + first) // 2
                         nc.tensor.transpose(
                             out=bank[:, i, u, :], in_=words[:, start : start + P], identity=identity_f32[:]
                         )
-                drain = nc.vector.tensor_copy if DRAIN_ON_VECTOR(sweep, half, n) else nc.scalar.copy
+                drain = nc.vector.tensor_copy if (c, half, n) in DRAIN_ON_VECTOR else nc.scalar.copy
                 drain(
                     out=out_words[:, 256 * n : 256 * (n + count)].rearrange(
                         "q (i s u) -> q i s u", i=count, u=2
@@ -273,8 +255,8 @@ def tile_mixerblock_pa_kernel(tc, p, mix_w, mix_b, decay, out_w, out_b, x, out):
         def quantise_m(step):
             if not 0 <= step < STEPS:
                 return
-            sweep, pair, half = unit_of(step)
-            found = block_list(sweep, half)
+            c, half, pair = place_of(step)
+            found = block_list(c, half)
             m_words[step] = m_pool.tile([P, MAX_BLOCKS * P], U32, name="m_words", align_bytes=64)
             m_scales[step] = m_pool.tile([P, MAX_BLOCKS * P], U8, name="m_scales", align_bytes=64)
             source = m_grouped[step][:].rearrange("q s j -> q (s j)")
@@ -292,108 +274,96 @@ def tile_mixerblock_pa_kernel(tc, p, mix_w, mix_b, decay, out_w, out_b, x, out):
         def multiply(step):
             if not 0 <= step < STEPS:
                 return
-            sweep, pair, half = unit_of(step)
-            slots = {(what, chunk): n for n, (what, chunk, row, first) in enumerate(block_list(sweep, half))}
-            tile = variants[(step // 2) % VARIANT_TILES]
-            mixed[step] = psum_mix.tile([P, BLOCKS, B * HD], F32, name="mixed")
-            for n in range(BLOCKS):
-                odd, chunk = n // 2, CHUNKS_OF[half][n]
-                own = "AB"[odd]
-                passes = []
-                if sweep > 0:
-                    passes.append((slots[(own + " full", chunk)], p_words[:, pair, p_cols(odd, 0)], p_cols(odd, 0)))
-                if chunk == 3:
-                    passes.append((slots[(own, 3)], p_words[:, pair, p_cols(odd, sweep)], p_cols(odd, sweep)))
-                else:
-                    v = 2 - chunk if odd else chunk
-                    passes.append((slots[("X", v)], tile[:, v, odd, :], p_cols(odd, sweep)))
-                for k, (slot, moving, scale_cols) in enumerate(passes):
-                    cols = slice(slot * P, (slot + 1) * P)
-                    nc.tensor.matmul_mx(
-                        out=mixed[step][:, n, :],
-                        lhsT=m_words[step][:, cols].bitcast(FP8X4),
-                        lhsT_scale=m_scales[step][:, cols],
-                        rhs=moving.bitcast(FP8X4),
-                        rhs_scale=p_scales[:, pair, scale_cols],
-                        start=(k == 0),
-                        stop=(k == len(passes) - 1),
-                    )
+            c, half, pair = place_of(step)
+            slots = {(what, chunk): n for n, (what, chunk, row, first) in enumerate(block_list(c, half))}
+            mixed[step] = psum_mix.tile([P, 2, 2, B * HD], F32, name="mixed")
+            for odd in range(2):
+                for n in range(2):
+                    chunk = half + 2 * n
+                    own = "AB"[odd]
+                    here = c * PAIRS + pair
+                    passes = []
+                    if c > 0:
+                        passes.append((slots[(own + " full", chunk)], p_words[:, pair, p_cols(odd)], pair))
+                    if chunk == 3:
+                        passes.append((slots[(own, 3)], p_words[:, here, p_cols(odd)], here))
+                    else:
+                        v = 2 - chunk if odd else chunk
+                        passes.append((slots[("X", v)], variants[:, v, pair, p_cols(odd)], here))
+                    for k, (slot, moving, part) in enumerate(passes):
+                        cols = slice(slot * P, (slot + 1) * P)
+                        nc.tensor.matmul_mx(
+                            out=mixed[step][:, odd, n, :],
+                            lhsT=m_words[step][:, cols].bitcast(FP8X4),
+                            lhsT_scale=m_scales[step][:, cols],
+                            rhs=moving.bitcast(FP8X4),
+                            rhs_scale=p_scales[:, part, p_cols(odd)],
+                            start=(k == 0),
+                            stop=(k == len(passes) - 1),
+                        )
 
         def add_bias(step):
             if not 0 <= step < STEPS:
                 return
-            sweep, pair, half = unit_of(step)
-            g, pair_in_group = divmod(pair, PAIRS // GROUPS)
-            if half == 0 and pair_in_group == 0:
-                c_rows[(sweep, g)] = c_pool.tile([P, BLOCKS, B, K_PASS], BF16, name="c_rows")
-            for odd in range(2):
-                first, second = CHUNKS_OF[half][2 * odd : 2 * odd + 2]
-                picked = slice(first, second + 1, second - first)
-                cols = slice((2 * pair_in_group + odd) * HD, (2 * pair_in_group + odd + 1) * HD)
-                nc.vector.tensor_tensor(
-                    out=c_rows[(sweep, g)][:, picked, :, cols],
-                    in0=mixed[step][:, 2 * odd : 2 * odd + 2, :].rearrange("p i (b f) -> p i b f", b=B),
-                    in1=bias_by_s[:, 2 * pair + odd, sweep * BLOCKS : (sweep + 1) * BLOCKS][:, picked]
-                    .unsqueeze(2)
-                    .unsqueeze(3)
-                    .to_broadcast([P, 2, B, HD]),
-                    op=ALU.add,
-                )
-
-        def transpose_c(bank):
-            if not 0 <= bank < SWEEPS * GROUPS * B * 2:
-                return
-            sweep, g, b, half = bank // 8, bank // 4 % 2, bank // 2 % 2, bank % 2
-            if half == 0:
-                c_grouped[bank] = p_grouped_pool.tile(
-                    [P, N_TILE, PACK], BF16, name="c_grouped", tag="p_grouped", align_bytes=64
-                )
-                c_grouped[bank + 1] = c_grouped[bank]
-            turned = psum_m.tile([P, 2, 2, P], F32, name="c_turned", tag="m_psum")
-            for i in range(2):
-                words = c_rows[(sweep, g)][:, 2 * half + i, b, :].bitcast(F32)
-                for u in range(2):
-                    nc.tensor.transpose(
-                        out=turned[:, i, u, :], in_=words[:, u : 2 * P : 2], identity=identity_f32[:]
-                    )
-            nc.scalar.copy(
-                out=c_grouped[bank][:]
-                .rearrange("q s j -> q (s j)")
-                .bitcast(F32)[:, half * N_TILE : (half + 1) * N_TILE]
-                .rearrange("q (i s u) -> q i s u", i=2, u=2),
-                in_=turned[:].rearrange("q i u s -> q i s u"),
+            c, half, pair = place_of(step)
+            g, pair_in_group = divmod(pair, GROUP_PAIRS)
+            where = (step // PAIRS, g)
+            if pair_in_group == 0:
+                c_rows[where] = c_pool.tile([P, 2, B, K_PASS], BF16, name="c_rows")
+            first = 2 * HD * pair_in_group
+            nc.vector.tensor_tensor(
+                out=c_rows[where][:, :, :, first : first + 2 * HD].rearrange("p n b (h f) -> p h (n b) f", h=2),
+                in0=mixed[step][:].rearrange("p h n (b f) -> p h (n b) f", b=B),
+                in1=bias_by_s[:, 2 * pair : 2 * pair + 2, step // PAIRS, :]
+                .unsqueeze(3)
+                .to_broadcast([P, 2, 2 * B, HD]),
+                op=ALU.add,
             )
 
-        def quantise_c(bank):
-            if not (0 <= bank < SWEEPS * GROUPS * B * 2 and bank % 2 == 1):
+        def transpose_c(turn):
+            if not 0 <= turn < SWEEPS * GROUPS:
                 return
-            sweep, g, b = bank // 8, bank // 4 % 2, bank // 2 % 2
-            cols = slice(sweep * N_TILE, (sweep + 1) * N_TILE)
+            rows = c_rows[divmod(turn, GROUPS)]
+            c_grouped[turn] = p_grouped_pool.tile(
+                [P, N_TILE, PACK], BF16, name="c_grouped", tag="c_grouped", align_bytes=64
+            )
+            out_words = c_grouped[turn][:].rearrange("q s j -> q (s j)").bitcast(F32)
+            for b in range(B):
+                turned = psum_m.tile([P, 2, 2, P], F32, name="c_turned", tag="m_psum")
+                for n in range(2):
+                    words = rows[:, n, b, :].bitcast(F32)
+                    for u in range(2):
+                        nc.tensor.transpose(
+                            out=turned[:, n, u, :], in_=words[:, u : 2 * P : 2], identity=identity_f32[:]
+                        )
+                (nc.scalar.copy if b == 0 or turn < SWEEPS * GROUPS - 1 else nc.vector.tensor_copy)(
+                    out=out_words[:, b * N_TILE : (b + 1) * N_TILE].rearrange("q (n s u) -> q n s u", n=2, u=2),
+                    in_=turned[:].rearrange("q n u s -> q n s u"),
+                )
+
+        def quantise_c(turn):
+            if not 0 <= turn < SWEEPS * GROUPS:
+                return
+            sweep, g = divmod(turn, GROUPS)
             nc.vector.quantize_mx(
-                out=c_words[:, b, g, cols].bitcast(FP8X4),
-                scales=c_scales[:, b, g, cols],
-                in_=c_grouped[bank][:].rearrange("q s j -> q (s j)"),
+                out=c_words[:, g, sweep, :].bitcast(FP8X4),
+                scales=c_scales[:, g, sweep, :],
+                in_=c_grouped[turn][:].rearrange("q s j -> q (s j)"),
             )
-
-        def patch_of(item):
-            sweep, rest = divmod(item // BLOCKS, B * 2)
-            return sweep, rest // 2, rest % 2
 
         def project(item):
             if not 0 <= item < ITEMS:
                 return
-            sweep, b, n_half = patch_of(item)
-            n_block = n_half * BLOCKS + item % BLOCKS
+            sweep, n_block = divmod(item, E // P)
             cols = slice(n_block * P, (n_block + 1) * P)
-            steps = slice(sweep * N_TILE, (sweep + 1) * N_TILE)
             projected[item] = psum_misc.tile([P, N_TILE], F32, name="projected", tag="misc")
             for g in range(GROUPS):
                 nc.tensor.matmul_mx(
                     out=projected[item][:],
                     lhsT=w_words[:, g, cols].bitcast(FP8X4),
                     lhsT_scale=w_scales[:, g, cols],
-                    rhs=c_words[:, b, g, steps].bitcast(FP8X4),
-                    rhs_scale=c_scales[:, b, g, steps],
+                    rhs=c_words[:, g, sweep, :].bitcast(FP8X4),
+                    rhs_scale=c_scales[:, g, sweep, :],
                     start=(g == 0),
                     stop=(g == GROUPS - 1),
                 )
@@ -401,12 +371,10 @@ def tile_mixerblock_pa_kernel(tc, p, mix_w, mix_b, decay, out_w, out_b, x, out):
         def add_out_b(item):
             if not 0 <= item < ITEMS:
                 return
-            patch, i = divmod(item, BLOCKS)
-            n_block = patch_of(item)[2] * BLOCKS + i
+            patch, i = divmod(item, 4)
             if i == 0:
-                y_turned[patch] = big_pool.tile(
-                    [P, BLOCKS, N_TILE], F32, name="y_turned", tag="big", align_bytes=64
-                )
+                y_turned[patch] = big_pool.tile([P, 4, N_TILE], F32, name="y_turned", tag="big", align_bytes=64)
+            n_block = item % (E // P)
             nc.scalar.activation(
                 out=y_turned[patch][:, i, :],
                 in_=projected[item][:],
@@ -415,23 +383,28 @@ def tile_mixerblock_pa_kernel(tc, p, mix_w, mix_b, decay, out_w, out_b, x, out):
             )
 
         def rows_and_cols(item):
-            sweep, b, n_half = patch_of(item)
-            first = sweep * N_TILE + (item % BLOCKS) * P
-            return b, slice(first, first + P), slice(n_half * N_TILE, (n_half + 1) * N_TILE)
+            patch, i = divmod(item, 4)
+            sweep, n_half = divmod(patch, 2)
+            b, n = divmod(i, 2)
+            chunk = sweep // 2 * BLOCKS + sweep % 2 + 2 * n
+            return b, slice(chunk * P, (chunk + 1) * P), slice(n_half * N_TILE, (n_half + 1) * N_TILE)
 
         def load_x(item):
-            if not 0 <= item < ITEMS:
+            if not 0 <= item < ITEMS or item % 2:
                 return
             b, rows, cols = rows_and_cols(item)
-            x_raw[item] = x_pool.tile([P, N_TILE], BF16, name="x_raw")
-            nc.sync.dma_start(out=x_raw[item][:], in_=x[b, rows, cols])
+            x_raw[item] = x_pool.tile([P, 2, N_TILE], BF16, name="x_raw")
+            nc.sync.dma_start(
+                out=x_raw[item][:],
+                in_=x[b, rows.start : rows.start + 3 * P, cols].rearrange("(n s) v -> s n v", s=P)[:, 0:3:2, :],
+            )
 
         def turn_back(item):
             if not 0 <= item < ITEMS:
                 return
-            patch, block = divmod(item, BLOCKS)
+            patch, block = divmod(item, 4)
             turned_back[item] = psum_misc.tile([P, N_TILE], F32, name="turned_back", tag="misc")
-            for i in range(BLOCKS):
+            for i in range(4):
                 nc.tensor.transpose(
                     out=turned_back[item][:, i * P : (i + 1) * P],
                     in_=y_turned[patch][:, i, block * P : (block + 1) * P],
@@ -443,9 +416,8 @@ def tile_mixerblock_pa_kernel(tc, p, mix_w, mix_b, decay, out_w, out_b, x, out):
                 return
             b, rows, cols = rows_and_cols(item)
             y = y_pool.tile([P, N_TILE], F32)
-            nc.vector.tensor_tensor(out=y[:], in0=turned_back[item][:], in1=x_raw[item][:], op=ALU.add)
+            nc.vector.tensor_tensor(out=y[:], in0=turned_back[item][:], in1=x_raw[item - item % 2][:, item % 2, :], op=ALU.add)
             nc.sync.dma_start(out=out[b, rows, cols], in_=y[:])
-
 
         with tc.manual_schedule():
             warm = const.tile([P, 1], F32)
@@ -458,17 +430,24 @@ def tile_mixerblock_pa_kernel(tc, p, mix_w, mix_b, decay, out_w, out_b, x, out):
             nc.sync.dma_start(out=decay_rows[:], in_=decay.partition_broadcast(P))
             mix_w_rows = const.tile([H, T], BF16)
             nc.sync.dma_start(out=mix_w_rows[:], in_=mix_w[:, :])
-            load_out_w(0)
             load_p(0)
+            load_out_w(0)
             w_rows = const.tile([P, P], BF16)
             nc.sync.dma_start(out=w_rows[:], in_=mix_w.rearrange("h (a q) -> (h a) q", q=P))
             b_rows = const.tile([P, P], BF16)
             nc.sync.dma_start(out=b_rows[:], in_=mix_b.rearrange("h (a q) -> (h a) q", q=P))
             load_out_w(1)
-            load_p(1)
 
-            t_int = left_pool.tile([H, T], I32, name="t_int", tag="left_rows")
-            nc.gpsimd.iota(t_int[:], pattern=[[1, T]], base=0, channel_multiplier=0)
+            left_work = [left_pool.tile([P, 2 * T], F32, name="left_work", tag="left_rows") for n in range(3)]
+            t_int = left_work[0][0:H, T : 2 * T].bitcast(I32)
+            t_row = left_work[0][0:H, 0:T]
+            factor = left_work[1][0:H, 0:T]
+            places = (left_work[1][0:H, T : 2 * T], left_work[2][0:H, 0:T])
+            left_parts = [
+                [place[:, odd * 512 : (odd + 1) * 512].rearrange("h (u v) -> h u v", u=2) for odd in range(2)]
+                for place in places
+            ]
+            nc.gpsimd.iota(t_int, pattern=[[1, T]], base=0, channel_multiplier=0)
             head_int = const.tile([H, 1], I32)
             nc.gpsimd.iota(head_int[:], pattern=[[0, 1]], base=0, channel_multiplier=1)
             s_int = const.tile([P, CHUNKS], I32)
@@ -479,8 +458,7 @@ def tile_mixerblock_pa_kernel(tc, p, mix_w, mix_b, decay, out_w, out_b, x, out):
             make_identity(nc, identity_f32[:])
             identity_bf16 = const.tile([P, P], BF16)
             make_identity(nc, identity_bf16[:])
-            for tile in variants:
-                nc.gpsimd.memset(tile[:].rearrange("q v h n -> q (v h n)").bitcast(I32), 0)
+            nc.gpsimd.memset(variants[:].rearrange("q v r n -> q (v r n)").bitcast(I32), 0)
 
             own_clipped = const.tile([H, 1], F32)
             nc.vector.tensor_scalar(
@@ -495,11 +473,10 @@ def tile_mixerblock_pa_kernel(tc, p, mix_w, mix_b, decay, out_w, out_b, x, out):
             log_d = const.tile([P, H], F32)
             nc.scalar.activation(out=log_d[:], in_=d_clipped[:], func=ACT.Ln)
 
-            t_row = left_pool.tile([H, T], F32, name="t_row", tag="left_rows")
-            nc.vector.tensor_copy(out=t_row[:], in_=t_int[:])
+            nc.vector.tensor_copy(out=t_row, in_=t_int)
             own_rate = const.tile([H, 1], F32)
             nc.vector.tensor_scalar(out=own_rate[:], in0=own_log[:], scalar1=-0.5, scalar2=None, op0=ALU.mult)
-            nc.scalar.activation(out=t_row[:], in_=t_row[:], func=ACT.Exp, scale=own_rate[:, 0:1])
+            nc.scalar.activation(out=t_row, in_=t_row, func=ACT.Exp, scale=own_rate[:, 0:1])
             late_head = const.tile([H, 1], F32)
             nc.vector.tensor_scalar(
                 out=late_head[:], in0=head_int[:], scalar1=float(HALF_H), scalar2=None, op0=ALU.is_ge
@@ -508,23 +485,33 @@ def tile_mixerblock_pa_kernel(tc, p, mix_w, mix_b, decay, out_w, out_b, x, out):
             nc.vector.tensor_scalar(
                 out=early_head[:], in0=head_int[:], scalar1=float(HALF_H), scalar2=None, op0=ALU.is_lt
             )
-            factor = left_pool.tile([H, T], F32, name="factor", tag="left_rows")
             nc.vector.tensor_scalar(
-                out=factor[:],
+                out=factor,
                 in0=mix_w_rows[:],
                 scalar1=late_head[:, 0:1],
                 scalar2=early_head[:, 0:1],
                 op0=ALU.mult,
                 op1=ALU.add,
             )
-            left_even = left_pool.tile([H, 2, 2 * 256], F32, name="left_even", tag="left_rows")
-            left_odd = left_pool.tile([H, 2, 2 * 256], F32, name="left_odd", tag="left_rows")
-            parked = [out[b, T - H : T, :] for b in range(SWEEPS)]
+            parked = [out[n % 2, T - PAIRS : T, :] for n in range(2)]
+            parked += [out[n % 2, T - PAIRS - H : T - PAIRS, :] for n in range(2)]
+
+            def park(sweep, queue):
+                for odd in range(2):
+                    heads = slice(odd, H, 2)
+                    if sweep < 2:
+                        rows = parked[sweep].rearrange("r (h u v) -> h r u v", h=2, u=2)
+                        queue.dma_start(out=rows[odd], in_=left_parts[0][odd][heads, :, :])
+                    else:
+                        rows = parked[sweep].rearrange("(r h) (u c v) -> h c r u v", h=2, u=2, c=2)
+                        for c in range(2):
+                            place = 1 - c if odd else c
+                            queue.dma_start(out=rows[odd][place], in_=left_parts[c][odd][heads, :, :])
+
             for c in range(2):
                 for odd in range(2):
-                    first = 256 * (1 - c) if odd else 256 * c
                     for u in range(2):
-                        dst = (left_odd if odd else left_even)[:, u, first : first + 256]
+                        dst = left_parts[c][odd][:, u, :]
                         views = [
                             source[:, c * K_PASS : (c + 1) * K_PASS].rearrange(
                                 "h (a r u e) -> h u a r e", a=4, u=2, e=2
@@ -537,13 +524,8 @@ def tile_mixerblock_pa_kernel(tc, p, mix_w, mix_b, decay, out_w, out_b, x, out):
                             in1=views[1],
                             op=ALU.mult,
                         )
-                for odd in range(2):
-                    first = (256 * (1 - c) if odd else 256 * c) if c == 0 else 0
-                    last = first + 256 if c == 0 else 512
-                    nc.scalar.dma_start(
-                        out=parked[c].rearrange("h (u v) -> h u v", u=2)[odd:H:2, :, first:last],
-                        in_=(left_odd if odd else left_even)[odd:H:2, :, first:last],
-                    )
+                if c == 0:
+                    park(0, nc.scalar)
 
             s_index = const.tile([P, CHUNKS], F32)
             nc.vector.tensor_copy(out=s_index[:], in_=s_int[:])
@@ -562,6 +544,8 @@ def tile_mixerblock_pa_kernel(tc, p, mix_w, mix_b, decay, out_w, out_b, x, out):
             right = const.tile([P, H, CHUNKS], F32)
             nc.scalar.activation(out=right[:], in_=exponent[:], func=ACT.Exp, scale=0.5)
             load_left(0)
+            for sweep in range(1, SWEEPS):
+                park(sweep, nc.sync)
             load_left(1)
 
             t_in_block = const.tile([P, 2, HD], F32)
@@ -581,16 +565,21 @@ def tile_mixerblock_pa_kernel(tc, p, mix_w, mix_b, decay, out_w, out_b, x, out):
             nc.vector.tensor_tensor(
                 out=right[:, 0:HALF_H, :], in0=right[:, 0:HALF_H, :], in1=w_by_s[:, 0:HALF_H, :], op=ALU.mult
             )
-            bias_by_s = const.tile([P, H, CHUNKS], F32)
-            nc.vector.tensor_copy(out=bias_by_s[:].rearrange("q h i -> q (h i)"), in_=b_turned[:])
+            bias_by_s = const.tile([P, H, SWEEPS, 2 * B], F32)
+            turned = b_turned[:].rearrange("q (h c n e) -> q h c n e", h=H, c=2, n=2)
+            for sweep in range(SWEEPS):
+                nc.vector.tensor_copy(
+                    out=bias_by_s[:, :, sweep, :].rearrange("q h (n b) -> q h n b", b=B),
+                    in_=turned[:, :, sweep // 2, :, sweep % 2].unsqueeze(3).to_broadcast([P, H, 2, B]),
+                )
 
             regroup_p(0, 0, nc.vector.tensor_copy)
             regroup_p(0, 1, nc.vector.tensor_copy)
             quantise_p(0)
-            copy_variants(0)
             regroup_out_w(0, nc.vector.tensor_copy)
             quantise_out_w(0)
             regroup_out_w(1, nc.scalar.copy)
+            last_turn = -1
 
             out_b_rows = const.tile([P, P], BF16)
             nc.gpsimd.memset(out_b_rows[:], 0.0)
@@ -600,33 +589,35 @@ def tile_mixerblock_pa_kernel(tc, p, mix_w, mix_b, decay, out_w, out_b, x, out):
             out_b_column = const.tile([P, E // P], F32)
             nc.vector.tensor_copy(out=out_b_column[:], in_=out_b_turned[:, 0 : E // P])
 
-            last_bank = -2
-            for step in range(-3, STEPS + 26):
-                item = step - 20
-                pair, odd = divmod(step + 3, 2)
-                turn, bank = divmod(step - 9, 8)
-                bank = 4 * turn + bank if bank < 4 else -2
-                if not odd:
-                    load_left(pair + 2)
-                    load_p(pair + 2)
+            for step in range(-3, STEPS + 17):
+                item = step - 11
+                turn = (step - 5) // 4 if step % 4 == 1 else -1
+                load_left(step + 5)
+                if step == 4:
+                    load_p(1)
                 load_x(item - 3)
                 make_m(step + 3)
                 mask_m(step + 2)
-                regroup_p(pair + 1, odd, nc.scalar.copy if odd else nc.vector.tensor_copy)
+                part = step + 4 if step < 4 else step
+                if step < 4 or 8 <= step < 16:
+                    regroup_p(part, 0, nc.vector.tensor_copy)
+                    regroup_p(part, 1, nc.scalar.copy)
                 transpose_m(step + 1)
-                transpose_c(bank)
+                transpose_c(turn)
                 turn_back(item - 5)
                 quantise_m(step)
                 if step == -2:
                     quantise_out_w(1)
-                if not odd and pair > 0:
-                    quantise_p(pair)
-                if not odd and pair > 0:
-                    copy_variants(pair)
-                quantise_c(last_bank)
-                last_bank = bank
+                if -3 < step <= 4 or 8 < step <= 16:
+                    quantise_p(last_part)
+                last_part = part
+                quantise_c(last_turn)
+                last_turn = turn
                 add_bias(step - 1)
                 multiply(step)
+                for when, c, v, first, last in VARIANT_COPIES:
+                    if when == step:
+                        copy_variants(c, v, slice(first, last))
                 project(item)
                 add_out_b(item - 1)
                 add_x_and_store(item - 6)

@@ -28,13 +28,14 @@ STEPS = SWEEPS * PAIRS
 GROUPS = E // K_PASS
 GROUP_PAIRS = PAIRS // GROUPS
 ITEMS = SWEEPS * (E // P)
+COPIES = 32
 MAX_BLOCKS = 7
 ROW_WIDTH = ((256, 512), (768, 1024))
 M_ROWS = 4672
 VARIANT_COPIES = (
-    (-2, 0, 0, 0, 2), (-2, 0, 2, 0, 2), (0, 0, 0, 2, 4), (0, 0, 2, 2, 4),
-    (2, 0, 0, 4, 6), (2, 0, 2, 4, 6), (4, 0, 0, 6, 8), (4, 0, 2, 6, 8),
-    (5, 0, 1, 0, 8), (12, 1, 0, 0, 4), (12, 1, 2, 0, 4), (16, 1, 0, 4, 8), (16, 1, 2, 4, 8), (17, 1, 1, 0, 8),
+    (-3, 0, 0, 0, 2), (-3, 0, 2, 0, 2), (-2, 0, 0, 2, 4), (-2, 0, 2, 2, 4),
+    (0, 0, 0, 4, 6), (0, 0, 2, 4, 6), (2, 0, 0, 6, 8), (2, 0, 2, 6, 8),
+    (3, 0, 1, 0, 8), (12, 1, 0, 0, 4), (12, 1, 2, 0, 4), (16, 1, 0, 4, 8), (16, 1, 2, 4, 8), (17, 1, 1, 0, 8),
 )
 DRAIN_ON_VECTOR = ()
 ON_SCALAR = (((0, 2), (1, 2)), ((0, 3), (0, 1)), ((0, 0), (1, 0)), ((0, 3),))
@@ -50,42 +51,42 @@ def tile_mixerblock_pa_kernel(tc, p, mix_w, mix_b, decay, out_w, out_b, x, out):
 
         const = pool("const", 1)
         big_pool = pool("big", 2)
-        p_raw_pool = pool("p_raw", 1)
         p_grouped_pool = pool("p_grouped", 2)
-        left_pool = pool("left_rows", 3)
+        quarter_pool = pool("quarter", 4)
         rows_pool = pool("m_rows", 3)
-        grouped_pool = pool("m_grouped", 3)
-        m_pool = pool("m_words", 3)
+        grouped_pool = pool("m_grouped", 2)
+        m_pool = pool("m_words", 2)
         c_pool = pool("c_rows", 2)
-        x_pool = pool("x_stage", 4)
-        y_pool = pool("y_stage", 3)
+        c_words_pool = pool("c_words", 2)
+        x_pool = pool("x_stage", 3)
+        y_pool = pool("y_stage", 2)
         psum_m = stack.enter_context(tc.psum_pool(name="psum_m", bufs=3))
         psum_mix = stack.enter_context(tc.psum_pool(name="psum_mix", bufs=2))
         psum_misc = stack.enter_context(tc.psum_pool(name="psum_misc", bufs=3))
 
-        p_raw, p_grouped, w_raw, w_grouped, left_rows, m_rows, blocks = {}, {}, {}, {}, {}, {}, {}
+        p_raw, p_grouped, w_raw, w_grouped, m_rows, c_words, c_scales = {}, {}, {}, {}, {}, {}, {}
         m_grouped, m_words, m_scales, mixed, c_rows, c_grouped = {}, {}, {}, {}, {}, {}
         projected, y_turned, turned_back, x_raw = {}, {}, {}, {}
 
         p_words = const.tile([P, 2 * PAIRS, 2 * B * HD], U32, align_bytes=64)
         p_scales = const.tile([P, 2 * PAIRS, 2 * B * HD], U8, align_bytes=64)
-        c_words = const.tile([P, GROUPS, SWEEPS, N_TILE], U32, align_bytes=64)
-        c_scales = const.tile([P, GROUPS, SWEEPS, N_TILE], U8, align_bytes=64)
         w_words = const.tile([P, GROUPS, E], U32, align_bytes=64)
         w_scales = const.tile([P, GROUPS, E], U8, align_bytes=64)
+        left_rows = const.tile([P, 2, PAIRS, 2, 2, 256], F32)
         variants = const.tile([P, 3, PAIRS, 2 * B * HD], U32, align_bytes=64)
 
         def load_p(c):
-            p_raw[c] = p_raw_pool.tile([P, 2, B * PAIRS, PACK * HD], BF16, name="p_raw")
+            for odd in range(2):
+                p_raw[(c, odd)] = big_pool.tile([P, B * PAIRS, PACK * HD], BF16, name="p_raw", tag="big", align_bytes=64)
             steps = slice(c * K_PASS, (c + 1) * K_PASS)
             heads = p.rearrange("b (r h) t f -> h (b r) t f", h=2)
             nc.sync.dma_start(
-                out=p_raw[c][:, 0, :, :], in_=heads[0][:, steps, :].rearrange("n (q j) f -> q n (j f)", j=PACK)
+                out=p_raw[(c, 0)][:], in_=heads[0][:, steps, :].rearrange("n (q j) f -> q n (j f)", j=PACK)
             )
             source = heads[1][:, steps, :].rearrange("n (a r j) f -> a r n (j f)", a=BLOCKS, j=PACK)
             for a in range(BLOCKS):
                 rows = slice(32 * (3 - a), 32 * (4 - a))
-                nc.sync.dma_start(out=p_raw[c][rows, 1, :, :], in_=source[a])
+                nc.sync.dma_start(out=p_raw[(c, 1)][rows, :, :], in_=source[a])
 
         def regroup_p(part, odd, engine_copy):
             c, pair = divmod(part, PAIRS)
@@ -95,7 +96,7 @@ def tile_mixerblock_pa_kernel(tc, p, mix_w, mix_b, decay, out_w, out_b, x, out):
                 )
             engine_copy(
                 out=p_grouped[part][:, odd, :, :, :],
-                in_=p_raw[c][:, odd, :, :]
+                in_=p_raw[(c, odd)][:]
                 .rearrange("q (b r) v -> q b r v", b=B)[:, :, pair, :]
                 .rearrange("q b (j f) -> q b f j", j=PACK),
             )
@@ -118,41 +119,47 @@ def tile_mixerblock_pa_kernel(tc, p, mix_w, mix_b, decay, out_w, out_b, x, out):
                     in_=p_words[rows, c * PAIRS + pairs.start : c * PAIRS + pairs.stop, p_cols(odd)].bitcast(I32),
                 )
 
-        def load_out_w(g):
-            w_raw[g] = big_pool.tile([P, PACK, E], BF16, name="w_raw", tag="big", align_bytes=64)
+        def load_out_w(piece):
+            g, n_half = divmod(piece, 2)
+            w_raw[piece] = quarter_pool.tile([P, PACK, N_TILE], BF16, name="w_raw", tag="quarter", align_bytes=64)
             nc.sync.dma_start(
-                out=w_raw[g][:],
-                in_=out_w[g * K_PASS : (g + 1) * K_PASS, :].rearrange("(q j) n -> q j n", j=PACK),
+                out=w_raw[piece][:],
+                in_=out_w[g * K_PASS : (g + 1) * K_PASS, n_half * N_TILE : (n_half + 1) * N_TILE].rearrange(
+                    "(q j) n -> q j n", j=PACK
+                ),
             )
 
-        def regroup_out_w(g, engine_copy):
-            w_grouped[g] = rows_pool.tile([P, E, PACK], BF16, name="w_grouped", tag="m_rows", align_bytes=64)
+        def regroup_out_w(piece, engine_copy):
+            w_grouped[piece] = quarter_pool.tile(
+                [P, N_TILE, PACK], BF16, name="w_grouped", tag="quarter", align_bytes=64
+            )
             engine_copy(
-                out=w_grouped[g][:].rearrange("q (c i) j -> q c j i", i=4),
-                in_=w_raw[g][:].rearrange("q j (c i) -> q c j i", i=4),
+                out=w_grouped[piece][:].rearrange("q (c i) j -> q c j i", i=4),
+                in_=w_raw[piece][:].rearrange("q j (c i) -> q c j i", i=4),
             )
 
-        def quantise_out_w(g):
+        def quantise_out_w(piece):
+            g, n_half = divmod(piece, 2)
+            cols = slice(n_half * N_TILE, (n_half + 1) * N_TILE)
             nc.vector.quantize_mx(
-                out=w_words[:, g, :].bitcast(FP8X4),
-                scales=w_scales[:, g, :],
-                in_=w_grouped[g][:].rearrange("q n j -> q (n j)"),
+                out=w_words[:, g, cols].bitcast(FP8X4),
+                scales=w_scales[:, g, cols],
+                in_=w_grouped[piece][:].rearrange("q n j -> q (n j)"),
             )
 
         def place_of(step):
             return step // PAIRS // 2, step // PAIRS % 2, step % PAIRS
 
-        def load_left(step):
-            if not 0 <= step < STEPS:
-                return
-            c, half, pair = place_of(step)
-            width = 2 * K_PASS * (c + 1)
-            tile = left_pool.tile([P, 2 * T], F32, name="left_rows", tag="left_rows")
-            nc.sync.dma_start(
-                out=tile[:, 0:width],
-                in_=parked[step // PAIRS].rearrange("n v -> (n v)")[pair * width : (pair + 1) * width].partition_broadcast(P),
-            )
-            left_rows[step] = tile[:, 0:width].rearrange("p (h u v) -> p h u v", h=2, u=2)
+        def load_left(c, first, last, odds=(0, 1), ks=range(P // COPIES)):
+            copies = parked[c].rearrange("t v -> (t v)").rearrange("(n h r v) -> h n r v", n=COPIES, h=2, v=256)
+            for odd in odds:
+                for k in ks:
+                    nc.sync.dma_start(
+                        out=left_rows[k : P : P // COPIES, odd, first:last, :, 1 - c if odd else c, :].rearrange(
+                            "n r u v -> n (r u) v"
+                        ),
+                        in_=copies[odd][:, 2 * first : 2 * last, :],
+                    )
 
         def make_m(step):
             if not 0 <= step < STEPS:
@@ -169,7 +176,7 @@ def tile_mixerblock_pa_kernel(tc, p, mix_w, mix_b, decay, out_w, out_b, x, out):
             def scale_left(odd, chunk, dst, first, last):
                 h = 2 * pair + odd
                 i = c * BLOCKS + chunk
-                src = left_rows[step][:, odd, :, first:last]
+                src = left_rows[:, odd, pair, :, :, :].rearrange("p u c v -> p u (c v)")[:, :, first:last]
                 scale = right[:, h, i : i + 1]
                 if (odd, chunk) in ON_SCALAR[step // PAIRS]:
                     nc.scalar.activation(out=dst, in_=src, func=ACT.Copy, scale=scale)
@@ -180,10 +187,10 @@ def tile_mixerblock_pa_kernel(tc, p, mix_w, mix_b, decay, out_w, out_b, x, out):
                 edge = HD * (row + 1)
                 if c == 0 and row < 3:
                     scale_left(0, row, part(row, 0, edge), 0, edge)
-                    scale_left(1, 2 - row, part(row, edge, 256), edge, 256)
+                    scale_left(1, 2 - row, part(row, edge, 256), 256 + edge, 512)
                 elif c == 0:
                     scale_left(0, 3, part(3, 0, 256), 0, 256)
-                    scale_left(1, 3, part(3, 256, 512), 0, 256)
+                    scale_left(1, 3, part(3, 256, 512), 256, 512)
                 elif row < 3:
                     scale_left(0, row, part(row, 0, 256 + edge), 0, 256 + edge)
                     scale_left(1, 2 - row, part(row, 256 + edge, 768), edge, 512)
@@ -324,8 +331,8 @@ def tile_mixerblock_pa_kernel(tc, p, mix_w, mix_b, decay, out_w, out_b, x, out):
             if not 0 <= turn < SWEEPS * GROUPS:
                 return
             rows = c_rows[divmod(turn, GROUPS)]
-            c_grouped[turn] = p_grouped_pool.tile(
-                [P, N_TILE, PACK], BF16, name="c_grouped", tag="c_grouped", align_bytes=64
+            c_grouped[turn] = quarter_pool.tile(
+                [P, N_TILE, PACK], BF16, name="c_grouped", tag="quarter", align_bytes=64
             )
             out_words = c_grouped[turn][:].rearrange("q s j -> q (s j)").bitcast(F32)
             for b in range(B):
@@ -345,9 +352,12 @@ def tile_mixerblock_pa_kernel(tc, p, mix_w, mix_b, decay, out_w, out_b, x, out):
             if not 0 <= turn < SWEEPS * GROUPS:
                 return
             sweep, g = divmod(turn, GROUPS)
+            if g == 0:
+                c_words[sweep] = c_words_pool.tile([P, GROUPS, N_TILE], U32, name="c_words", align_bytes=64)
+                c_scales[sweep] = c_words_pool.tile([P, GROUPS, N_TILE], U8, name="c_scales", align_bytes=64)
             nc.vector.quantize_mx(
-                out=c_words[:, g, sweep, :].bitcast(FP8X4),
-                scales=c_scales[:, g, sweep, :],
+                out=c_words[sweep][:, g, :].bitcast(FP8X4),
+                scales=c_scales[sweep][:, g, :],
                 in_=c_grouped[turn][:].rearrange("q s j -> q (s j)"),
             )
 
@@ -362,8 +372,8 @@ def tile_mixerblock_pa_kernel(tc, p, mix_w, mix_b, decay, out_w, out_b, x, out):
                     out=projected[item][:],
                     lhsT=w_words[:, g, cols].bitcast(FP8X4),
                     lhsT_scale=w_scales[:, g, cols],
-                    rhs=c_words[:, g, sweep, :].bitcast(FP8X4),
-                    rhs_scale=c_scales[:, g, sweep, :],
+                    rhs=c_words[sweep][:, g, :].bitcast(FP8X4),
+                    rhs_scale=c_scales[sweep][:, g, :],
                     start=(g == 0),
                     stop=(g == GROUPS - 1),
                 )
@@ -424,108 +434,123 @@ def tile_mixerblock_pa_kernel(tc, p, mix_w, mix_b, decay, out_w, out_b, x, out):
             nc.vector.memset(warm[:], 1.0)
             nc.scalar.activation(out=warm[:], in_=warm[:], func=ACT.Ln)
 
-            own_decay = const.tile([H, 1], BF16)
-            nc.sync.dma_start(out=own_decay[:], in_=decay.rearrange("(h o) -> h o", o=1))
             decay_rows = const.tile([P, H], BF16)
             nc.sync.dma_start(out=decay_rows[:], in_=decay.partition_broadcast(P))
-            mix_w_rows = const.tile([H, T], BF16)
-            nc.sync.dma_start(out=mix_w_rows[:], in_=mix_w[:, :])
-            load_p(0)
-            load_out_w(0)
+            mix_w_rows = quarter_pool.tile([P, T], BF16, name="mix_w_rows", tag="quarter", align_bytes=64)
+            nc.gpsimd.memset(mix_w_rows[:].bitcast(I32), 0)
+            nc.sync.dma_start(out=mix_w_rows[0:H, :], in_=mix_w[:, :])
             w_rows = const.tile([P, P], BF16)
             nc.sync.dma_start(out=w_rows[:], in_=mix_w.rearrange("h (a q) -> (h a) q", q=P))
+            load_p(0)
+            load_out_w(0)
             b_rows = const.tile([P, P], BF16)
             nc.sync.dma_start(out=b_rows[:], in_=mix_b.rearrange("h (a q) -> (h a) q", q=P))
-            load_out_w(1)
+            out_b_rows = const.tile([P, P], BF16)
+            nc.vector.memset(out_b_rows[:], 0.0)
+            nc.sync.dma_start(out=out_b_rows[0 : E // P, :], in_=out_b.rearrange("(i q) -> i q", q=P))
 
-            left_work = [left_pool.tile([P, 2 * T], F32, name="left_work", tag="left_rows") for n in range(3)]
-            t_int = left_work[0][0:H, T : 2 * T].bitcast(I32)
-            t_row = left_work[0][0:H, 0:T]
-            factor = left_work[1][0:H, 0:T]
-            places = (left_work[1][0:H, T : 2 * T], left_work[2][0:H, 0:T])
-            left_parts = [
-                [place[:, odd * 512 : (odd + 1) * 512].rearrange("h (u v) -> h u v", u=2) for odd in range(2)]
-                for place in places
+            work = [
+                rows_pool.tile([P, M_ROWS // 2], F32, name="work", tag="m_rows", align_bytes=64) for n in range(2)
             ]
-            nc.gpsimd.iota(t_int, pattern=[[1, T]], base=0, channel_multiplier=0)
-            head_int = const.tile([H, 1], I32)
-            nc.gpsimd.iota(head_int[:], pattern=[[0, 1]], base=0, channel_multiplier=1)
-            s_int = const.tile([P, CHUNKS], I32)
-            nc.gpsimd.iota(s_int[:], pattern=[[P, CHUNKS]], base=0, channel_multiplier=1)
-            t_in_block_int = const.tile([P, 2, HD // 2, 2], I32)
-            nc.gpsimd.iota(t_in_block_int[:], pattern=[[2, 2], [PACK, HD // 2], [1, 2]], base=0, channel_multiplier=0)
+            t_int = work[0][:, T : 2 * T].bitcast(I32)
+            t_row = work[0][:, 0:T]
+            factor = work[1][:, 0:T]
+            left_parts = [work[1][:, T + c * K_PASS : T + (c + 1) * K_PASS] for c in range(2)]
+            reversed_part = work[1][:, 2 * T : 2 * T + 256]
             identity_f32 = const.tile([P, P], F32)
             make_identity(nc, identity_f32[:])
             identity_bf16 = const.tile([P, P], BF16)
             make_identity(nc, identity_bf16[:])
+            nc.gpsimd.iota(t_int, pattern=[[1, T]], base=0, channel_multiplier=0)
+            s_int = const.tile([P, CHUNKS], I32)
+            nc.gpsimd.iota(s_int[:], pattern=[[P, CHUNKS]], base=0, channel_multiplier=1)
+            t_in_block_int = const.tile([P, 2, HD // 2, 2], I32)
+            nc.gpsimd.iota(t_in_block_int[:], pattern=[[2, 2], [PACK, HD // 2], [1, 2]], base=0, channel_multiplier=0)
             nc.gpsimd.memset(variants[:].rearrange("q v r n -> q (v r n)").bitcast(I32), 0)
 
-            own_clipped = const.tile([H, 1], F32)
-            nc.vector.tensor_scalar(
-                out=own_clipped[:], in0=own_decay[:], scalar1=0.9, scalar2=1.0, op0=ALU.max, op1=ALU.min
+            own_head = const.tile([P, 2, PAIRS], F32)
+            nc.vector.tensor_reduce(
+                out=own_head[:].rearrange("q h r -> q (h r)"),
+                in_=identity_f32[:].rearrange("q (n h) -> q h n", h=H),
+                op=ALU.add,
+                axis=AX.X,
             )
-            own_log = const.tile([H, 1], F32)
-            nc.scalar.activation(out=own_log[:], in_=own_clipped[:], func=ACT.Ln)
+            early_head, late_head, even_head, odd_head = (
+                const.tile([P, 1], F32, name=name) for name in ("early_head", "late_head", "even_head", "odd_head")
+            )
+            for dst, heads in (
+                (early_head, own_head[:, :, 0 : PAIRS // 2]),
+                (late_head, own_head[:, :, PAIRS // 2 : PAIRS]),
+                (even_head, own_head[:, 0:1, :]),
+                (odd_head, own_head[:, 1:2, :]),
+            ):
+                nc.vector.tensor_reduce(out=dst[:], in_=heads, op=ALU.add, axis=AX.XY)
+            nc.vector.tensor_copy(out=t_row, in_=t_int)
+            spread = const.tile([P, P], BF16)
+            nc.vector.tensor_copy(
+                out=spread[:].rearrange("k (n h r) -> k n h r", h=2, r=PAIRS),
+                in_=identity_bf16[:, 0:H].rearrange("k (r h) -> k h r", h=2).unsqueeze(1).to_broadcast([P, P // H, 2, PAIRS]),
+            )
+
             d_clipped = const.tile([P, H], F32)
             nc.vector.tensor_scalar(
                 out=d_clipped[:], in0=decay_rows[:], scalar1=0.9, scalar2=1.0, op0=ALU.max, op1=ALU.min
             )
             log_d = const.tile([P, H], F32)
             nc.scalar.activation(out=log_d[:], in_=d_clipped[:], func=ACT.Ln)
-
-            nc.vector.tensor_copy(out=t_row, in_=t_int)
-            own_rate = const.tile([H, 1], F32)
+            own_logs = const.tile([P, 2, PAIRS], F32)
+            nc.vector.tensor_tensor(
+                out=own_logs[:],
+                in0=log_d[:].rearrange("q (r h) -> q h r", h=2),
+                in1=own_head[:],
+                op=ALU.mult,
+            )
+            own_log = const.tile([P, 1], F32)
+            nc.vector.tensor_reduce(out=own_log[:], in_=own_logs[:], op=ALU.add, axis=AX.XY)
+            own_rate = const.tile([P, 1], F32)
             nc.vector.tensor_scalar(out=own_rate[:], in0=own_log[:], scalar1=-0.5, scalar2=None, op0=ALU.mult)
-            nc.scalar.activation(out=t_row, in_=t_row, func=ACT.Exp, scale=own_rate[:, 0:1])
-            late_head = const.tile([H, 1], F32)
-            nc.vector.tensor_scalar(
-                out=late_head[:], in0=head_int[:], scalar1=float(HALF_H), scalar2=None, op0=ALU.is_ge
-            )
-            early_head = const.tile([H, 1], F32)
-            nc.vector.tensor_scalar(
-                out=early_head[:], in0=head_int[:], scalar1=float(HALF_H), scalar2=None, op0=ALU.is_lt
-            )
-            nc.vector.tensor_scalar(
-                out=factor,
-                in0=mix_w_rows[:],
-                scalar1=late_head[:, 0:1],
-                scalar2=early_head[:, 0:1],
-                op0=ALU.mult,
-                op1=ALU.add,
-            )
-            parked = [out[n % 2, T - PAIRS : T, :] for n in range(2)]
-            parked += [out[n % 2, T - PAIRS - H : T - PAIRS, :] for n in range(2)]
 
-            def park(sweep, queue):
-                for odd in range(2):
-                    heads = slice(odd, H, 2)
-                    if sweep < 2:
-                        rows = parked[sweep].rearrange("r (h u v) -> h r u v", h=2, u=2)
-                        queue.dma_start(out=rows[odd], in_=left_parts[0][odd][heads, :, :])
-                    else:
-                        rows = parked[sweep].rearrange("(r h) (u c v) -> h c r u v", h=2, u=2, c=2)
-                        for c in range(2):
-                            place = 1 - c if odd else c
-                            queue.dma_start(out=rows[odd][place], in_=left_parts[c][odd][heads, :, :])
+            parked = [out[B - 1, T // 2 + 256 * c : T // 2 + 256 * (c + 1), :] for c in range(2)]
 
-            for c in range(2):
-                for odd in range(2):
-                    for u in range(2):
-                        dst = left_parts[c][odd][:, u, :]
-                        views = [
-                            source[:, c * K_PASS : (c + 1) * K_PASS].rearrange(
-                                "h (a r u e) -> h u a r e", a=4, u=2, e=2
-                            )[:, u, :: (-1 if odd else 1), :, :]
-                            for source in (t_row, factor)
-                        ]
-                        nc.vector.tensor_tensor(
-                            out=dst.rearrange("h (a r e) -> h a r e", a=4, e=2),
-                            in0=views[0],
-                            in1=views[1],
-                            op=ALU.mult,
-                        )
-                if c == 0:
-                    park(0, nc.scalar)
+            def prepare_left(c):
+                steps = slice(c * K_PASS, (c + 1) * K_PASS)
+                own_w = psum_misc.tile([P, K_PASS], F32, name="own_w", tag="misc")
+                nc.tensor.matmul(out=own_w[:], lhsT=spread[:], rhs=mix_w_rows[:, steps], start=True, stop=True)
+                nc.vector.tensor_scalar(
+                    out=factor[:, steps],
+                    in0=own_w[:],
+                    scalar1=late_head[:, 0:1],
+                    scalar2=early_head[:, 0:1],
+                    op0=ALU.mult,
+                    op1=ALU.add,
+                )
+                nc.scalar.activation(out=t_row[:, steps], in_=t_row[:, steps], func=ACT.Exp, scale=own_rate[:, 0:1])
+                nc.vector.tensor_tensor(out=t_row[:, steps], in0=t_row[:, steps], in1=factor[:, steps], op=ALU.mult)
+                views = t_row[:, steps].rearrange("q (a r u e) -> q u a r e", a=4, u=2, e=2)
+                for u in range(2):
+                    nc.vector.tensor_scalar(
+                        out=reversed_part.rearrange("q (a r e) -> q a r e", a=4, e=2),
+                        in0=views[:, u, ::-1, :, :],
+                        scalar1=odd_head[:, 0:1],
+                        scalar2=None,
+                        op0=ALU.mult,
+                    )
+                    nc.vector.scalar_tensor_tensor(
+                        out=left_parts[c][:, 256 * u : 256 * (u + 1)].rearrange("q (a r e) -> q a r e", a=4, e=2),
+                        in0=views[:, u, :, :, :],
+                        scalar=even_head[:, 0:1],
+                        in1=reversed_part.rearrange("q (a r e) -> q a r e", a=4, e=2),
+                        op0=ALU.mult,
+                        op1=ALU.add,
+                    )
+                copies = parked[c].rearrange("t v -> (t v)").rearrange("(n q v) -> n q v", q=P, v=K_PASS)
+                for n in range(COPIES * H // P):
+                    (nc.scalar if c == 0 else nc.sync).dma_start(out=copies[n], in_=left_parts[c])
+
+            prepare_left(0)
+            load_left(0, 0, 2)
+            load_out_w(1)
+            load_left(0, 2, PAIRS)
 
             s_index = const.tile([P, CHUNKS], F32)
             nc.vector.tensor_copy(out=s_index[:], in_=s_int[:])
@@ -543,10 +568,6 @@ def tile_mixerblock_pa_kernel(tc, p, mix_w, mix_b, decay, out_w, out_b, x, out):
             )
             right = const.tile([P, H, CHUNKS], F32)
             nc.scalar.activation(out=right[:], in_=exponent[:], func=ACT.Exp, scale=0.5)
-            load_left(0)
-            for sweep in range(1, SWEEPS):
-                park(sweep, nc.sync)
-            load_left(1)
 
             t_in_block = const.tile([P, 2, HD], F32)
             nc.vector.tensor_copy(out=t_in_block[:], in_=t_in_block_int[:].rearrange("q u r e -> q u (r e)"))
@@ -573,17 +594,16 @@ def tile_mixerblock_pa_kernel(tc, p, mix_w, mix_b, decay, out_w, out_b, x, out):
                     in_=turned[:, :, sweep // 2, :, sweep % 2].unsqueeze(3).to_broadcast([P, H, 2, B]),
                 )
 
-            regroup_p(0, 0, nc.vector.tensor_copy)
-            regroup_p(0, 1, nc.vector.tensor_copy)
-            quantise_p(0)
+            for part in range(4):
+                if part < 3:
+                    regroup_p(part, 0, nc.vector.tensor_copy)
+                    regroup_p(part, 1, nc.scalar.copy)
+                if part > 0:
+                    quantise_p(part - 1)
             regroup_out_w(0, nc.vector.tensor_copy)
             quantise_out_w(0)
-            regroup_out_w(1, nc.scalar.copy)
             last_turn = -1
 
-            out_b_rows = const.tile([P, P], BF16)
-            nc.gpsimd.memset(out_b_rows[:], 0.0)
-            nc.sync.dma_start(out=out_b_rows[0 : E // P, :], in_=out_b.rearrange("(i q) -> i q", q=P))
             out_b_turned = psum_misc.tile([P, P], BF16, name="out_b_turned", tag="misc")
             nc.tensor.transpose(out=out_b_turned[:], in_=out_b_rows[:], identity=identity_bf16[:])
             out_b_column = const.tile([P, E // P], F32)
@@ -592,14 +612,15 @@ def tile_mixerblock_pa_kernel(tc, p, mix_w, mix_b, decay, out_w, out_b, x, out):
             for step in range(-3, STEPS + 17):
                 item = step - 11
                 turn = (step - 5) // 4 if step % 4 == 1 else -1
-                load_left(step + 5)
-                if step == 4:
+                if step == 2:
                     load_p(1)
                 load_x(item - 3)
                 make_m(step + 3)
                 mask_m(step + 2)
-                part = step + 4 if step < 4 else step
-                if step < 4 or 8 <= step < 16:
+                if step in range(8):
+                    load_left(1, 0, PAIRS, (step % 2,), (step // 2,))
+                part = step + 6 if step < 2 else step + 3
+                if step < 2 or 5 <= step < 13:
                     regroup_p(part, 0, nc.vector.tensor_copy)
                     regroup_p(part, 1, nc.scalar.copy)
                 transpose_m(step + 1)
@@ -607,8 +628,18 @@ def tile_mixerblock_pa_kernel(tc, p, mix_w, mix_b, decay, out_w, out_b, x, out):
                 turn_back(item - 5)
                 quantise_m(step)
                 if step == -2:
+                    regroup_out_w(1, nc.scalar.copy)
+                    load_out_w(2)
+                if step == -1:
                     quantise_out_w(1)
-                if -3 < step <= 4 or 8 < step <= 16:
+                    load_out_w(3)
+                if step == -3:
+                    prepare_left(1)
+                if step in (1, 3):
+                    regroup_out_w(2 + step // 2, nc.vector.tensor_copy)
+                if step in (2, 4):
+                    quantise_out_w(1 + step // 2)
+                if -3 < step <= 2 or 5 < step <= 13:
                     quantise_p(last_part)
                 last_part = part
                 quantise_c(last_turn)

@@ -27,7 +27,8 @@ SWEEPS = 4
 STEPS = SWEEPS * PAIRS
 GROUPS = E // K_PASS
 GROUP_PAIRS = PAIRS // GROUPS
-ITEMS = SWEEPS * (E // P)
+ITEMS = (SWEEPS - 1) * (E // P)
+LAST_ITEMS = E // P
 COPIES = 32
 MAX_BLOCKS = 7
 ROW_WIDTH = ((256, 512), (768, 1024))
@@ -58,15 +59,14 @@ def tile_mixerblock_pa_kernel(tc, p, mix_w, mix_b, decay, out_w, out_b, x, out):
         m_pool = pool("m_words", 2)
         c_pool = pool("c_rows", 2)
         c_words_pool = pool("c_words", 2)
-        x_pool = pool("x_stage", 3)
-        y_pool = pool("y_stage", 2)
+        x_pool = pool("x_stage", 4)
         psum_m = stack.enter_context(tc.psum_pool(name="psum_m", bufs=3))
         psum_mix = stack.enter_context(tc.psum_pool(name="psum_mix", bufs=2))
         psum_misc = stack.enter_context(tc.psum_pool(name="psum_misc", bufs=3))
 
         p_raw, p_grouped, w_raw, w_grouped, m_rows, c_words, c_scales = {}, {}, {}, {}, {}, {}, {}
         m_grouped, m_words, m_scales, mixed, c_rows, c_grouped = {}, {}, {}, {}, {}, {}
-        projected, y_turned, turned_back, x_raw = {}, {}, {}, {}
+        projected, y_turned, turned_back, x_raw, y, last_y = {}, {}, {}, {}, {}, {}
 
         p_words = const.tile([P, 2 * PAIRS, 2 * B * HD], U32, align_bytes=64)
         p_scales = const.tile([P, 2 * PAIRS, 2 * B * HD], U8, align_bytes=64)
@@ -230,18 +230,20 @@ def tile_mixerblock_pa_kernel(tc, p, mix_w, mix_b, decay, out_w, out_b, x, out):
                 found += [(name, 3, 3, 256 * n) for n, name in enumerate(names)]
             return found
 
-        def transpose_m(step):
+        def transpose_m(step, first_part):
             if not 0 <= step < STEPS:
                 return
             c, half, pair = place_of(step)
             width = ROW_WIDTH[c][half]
             found = block_list(c, half)
             words = m_rows[step][:].bitcast(F32)
-            m_grouped[step] = grouped_pool.tile(
-                [P, MAX_BLOCKS * P, PACK], BF16, name="m_grouped", align_bytes=64
-            )
+            if first_part:
+                m_grouped[step] = grouped_pool.tile(
+                    [P, MAX_BLOCKS * P, PACK], BF16, name="m_grouped", align_bytes=64
+                )
             out_words = m_grouped[step][:].rearrange("q s j -> q (s j)").bitcast(F32)
-            for n in range(0, len(found), 2):
+            middle = (len(found) + 1) // 4 * 2
+            for n in range(0, middle, 2) if first_part else range(middle, len(found), 2):
                 count = min(2, len(found) - n)
                 bank = psum_m.tile([P, 2, 2, P], F32, name="m_psum", tag="m_psum")
                 for i in range(count):
@@ -278,12 +280,28 @@ def tile_mixerblock_pa_kernel(tc, p, mix_w, mix_b, decay, out_w, out_b, x, out):
                     )
                     first += count
 
+        def keep_warm(step):
+            if not 0 <= step < STEPS:
+                return
+            if step not in mixed:
+                mixed[step] = psum_mix.tile([P, 2, 2, B * HD], F32, name="mixed", tag="mixed")
+            if step >= PAIRS:
+                nc.tensor.matmul_mx(
+                    out=mixed[step][:].rearrange("p h n v -> p (h n v)"),
+                    lhsT=w_words[:, 0, 0:P].bitcast(FP8X4),
+                    lhsT_scale=w_scales[:, 0, 0:P],
+                    rhs=w_words[:, 0, 0:N_TILE].bitcast(FP8X4),
+                    rhs_scale=w_scales[:, 0, 0:N_TILE],
+                    start=True,
+                    stop=True,
+                )
+
         def multiply(step):
             if not 0 <= step < STEPS:
                 return
             c, half, pair = place_of(step)
             slots = {(what, chunk): n for n, (what, chunk, row, first) in enumerate(block_list(c, half))}
-            mixed[step] = psum_mix.tile([P, 2, 2, B * HD], F32, name="mixed")
+            keep_warm(step)
             for odd in range(2):
                 for n in range(2):
                     chunk = half + 2 * n
@@ -348,17 +366,18 @@ def tile_mixerblock_pa_kernel(tc, p, mix_w, mix_b, decay, out_w, out_b, x, out):
                     in_=turned[:].rearrange("q n u s -> q n s u"),
                 )
 
-        def quantise_c(turn):
+        def quantise_c(turn, batches):
             if not 0 <= turn < SWEEPS * GROUPS:
                 return
             sweep, g = divmod(turn, GROUPS)
             if g == 0:
                 c_words[sweep] = c_words_pool.tile([P, GROUPS, N_TILE], U32, name="c_words", align_bytes=64)
                 c_scales[sweep] = c_words_pool.tile([P, GROUPS, N_TILE], U8, name="c_scales", align_bytes=64)
+            cols = slice(batches.start * 2 * P, batches.stop * 2 * P)
             nc.vector.quantize_mx(
-                out=c_words[sweep][:, g, :].bitcast(FP8X4),
-                scales=c_scales[sweep][:, g, :],
-                in_=c_grouped[turn][:].rearrange("q s j -> q (s j)"),
+                out=c_words[sweep][:, g, cols].bitcast(FP8X4),
+                scales=c_scales[sweep][:, g, cols],
+                in_=c_grouped[turn][:, cols, :].rearrange("q s j -> q (s j)"),
             )
 
         def project(item):
@@ -366,7 +385,8 @@ def tile_mixerblock_pa_kernel(tc, p, mix_w, mix_b, decay, out_w, out_b, x, out):
                 return
             sweep, n_block = divmod(item, E // P)
             cols = slice(n_block * P, (n_block + 1) * P)
-            projected[item] = psum_misc.tile([P, N_TILE], F32, name="projected", tag="misc")
+            bank, tag = (psum_misc, "misc") if item < 21 else (psum_mix, "mixed") if item < 23 else (psum_m, "m_psum")
+            projected[item] = bank.tile([P, N_TILE], F32, name="projected", tag=tag)
             for g in range(GROUPS):
                 nc.tensor.matmul_mx(
                     out=projected[item][:],
@@ -403,7 +423,7 @@ def tile_mixerblock_pa_kernel(tc, p, mix_w, mix_b, decay, out_w, out_b, x, out):
             if not 0 <= item < ITEMS or item % 2:
                 return
             b, rows, cols = rows_and_cols(item)
-            x_raw[item] = x_pool.tile([P, 2, N_TILE], BF16, name="x_raw")
+            x_raw[item] = x_pool.tile([P, 2, N_TILE], BF16, name="x_raw", tag="x_raw")
             nc.sync.dma_start(
                 out=x_raw[item][:],
                 in_=x[b, rows.start : rows.start + 3 * P, cols].rearrange("(n s) v -> s n v", s=P)[:, 0:3:2, :],
@@ -424,10 +444,72 @@ def tile_mixerblock_pa_kernel(tc, p, mix_w, mix_b, decay, out_w, out_b, x, out):
         def add_x_and_store(item):
             if not 0 <= item < ITEMS:
                 return
-            b, rows, cols = rows_and_cols(item)
-            y = y_pool.tile([P, N_TILE], F32)
-            nc.vector.tensor_tensor(out=y[:], in0=turned_back[item][:], in1=x_raw[item - item % 2][:, item % 2, :], op=ALU.add)
-            nc.sync.dma_start(out=out[b, rows, cols], in_=y[:])
+            b, rows, cols = rows_and_cols(item - item % 2)
+            if item % 2 == 0:
+                y[item] = quarter_pool.tile([P, 2, N_TILE], F32, name="y", tag="quarter", align_bytes=64)
+            both = y[item - item % 2]
+            nc.vector.tensor_tensor(
+                out=both[:, item % 2, :], in0=turned_back[item][:], in1=x_raw[item - item % 2][:, item % 2, :], op=ALU.add
+            )
+            if item % 2:
+                nc.sync.dma_start(
+                    out=out[b, rows.start : rows.start + 3 * P, cols].rearrange("(n s) v -> s n v", s=P)[:, 0:3:2, :],
+                    in_=both[:],
+                )
+
+        def last_rows_and_cols(k):
+            b, n_half, n = k // 4, k // 2 % 2, k % 2
+            chunk = BLOCKS + 1 + 2 * n
+            return b, slice(chunk * P, (chunk + 1) * P), slice(n_half * N_TILE, (n_half + 1) * N_TILE)
+
+        def load_last_x(k):
+            b, rows, cols = last_rows_and_cols(k)
+            x_raw[ITEMS + k] = x_pool.tile([P, 2, N_TILE], BF16, name="x_raw", tag="x_raw")
+            nc.sync.dma_start(
+                out=x_raw[ITEMS + k][:],
+                in_=x[b, rows.start : rows.start + 3 * P, cols].rearrange("(n s) v -> s n v", s=P)[:, 0:3:2, :],
+            )
+
+        def residual(k):
+            return left_rows[:, 0, k // 2, :, :, :].rearrange("p u c v -> p (u c v)").rearrange(
+                "p (n v) -> p n v", n=2
+            )
+
+        def out_b_everywhere():
+            return left_rows[:, 1, 0, 0, :, :].rearrange("p c v -> p (c v)").bitcast(BF16)
+
+        def add_out_b_to_x(k):
+            cols = last_rows_and_cols(k)[2]
+            nc.vector.tensor_tensor(
+                out=residual(k),
+                in0=x_raw[ITEMS + k][:],
+                in1=out_b_everywhere()[:, cols].unsqueeze(1).to_broadcast([P, 2, N_TILE]),
+                op=ALU.add,
+            )
+
+        def project_last(k):
+            b, rows, cols = last_rows_and_cols(k)
+            first = (2 * b + k % 2) * P
+            bank, tag = (psum_mix, "mixed") if k % 4 < 2 else (psum_m, "m_psum")
+            projected[ITEMS + k] = bank.tile([P, N_TILE], F32, name="projected", tag=tag)
+            for g in range(GROUPS):
+                nc.tensor.matmul_mx(
+                    out=projected[ITEMS + k][:],
+                    lhsT=c_words[SWEEPS - 1][:, g, first : first + P].bitcast(FP8X4),
+                    lhsT_scale=c_scales[SWEEPS - 1][:, g, first : first + P],
+                    rhs=w_words[:, g, cols].bitcast(FP8X4),
+                    rhs_scale=w_scales[:, g, cols],
+                    start=(g == 0),
+                    stop=(g == GROUPS - 1),
+                )
+
+        def finish_last(k):
+            b, rows, cols = last_rows_and_cols(k)
+            if k % 2 == 0:
+                last_y[k] = quarter_pool.tile([P, 2, N_TILE], F32, name="last_y", tag="quarter", align_bytes=64)
+            dst = last_y[k - k % 2][:, k % 2, :]
+            nc.vector.tensor_tensor(out=dst, in0=projected[ITEMS + k][:], in1=residual(k)[:, k % 2, :], op=ALU.add)
+            nc.sync.dma_start(out=out[b, rows, cols], in_=dst)
 
         with tc.manual_schedule():
             warm = const.tile([P, 1], F32)
@@ -444,24 +526,23 @@ def tile_mixerblock_pa_kernel(tc, p, mix_w, mix_b, decay, out_w, out_b, x, out):
             load_p(0)
             load_out_w(0)
             b_rows = const.tile([P, P], BF16)
-            nc.sync.dma_start(out=b_rows[:], in_=mix_b.rearrange("h (a q) -> (h a) q", q=P))
             out_b_rows = const.tile([P, P], BF16)
             nc.vector.memset(out_b_rows[:], 0.0)
-            nc.sync.dma_start(out=out_b_rows[0 : E // P, :], in_=out_b.rearrange("(i q) -> i q", q=P))
 
             work = [
                 rows_pool.tile([P, M_ROWS // 2], F32, name="work", tag="m_rows", align_bytes=64) for n in range(2)
             ]
-            t_int = work[0][:, T : 2 * T].bitcast(I32)
-            t_row = work[0][:, 0:T]
-            factor = work[1][:, 0:T]
-            left_parts = [work[1][:, T + c * K_PASS : T + (c + 1) * K_PASS] for c in range(2)]
-            reversed_part = work[1][:, 2 * T : 2 * T + 256]
+            late_work = [x_pool.tile([P, K_PASS], F32, name="late_work", tag="x_raw") for n in range(4)]
+            t_int = work[0][:, 0:T].bitcast(I32)
+            t_row = (work[0][:, T : T + K_PASS], late_work[0][:])
+            factor = (work[1][:, 0:K_PASS], late_work[1][:])
+            left_parts = (work[1][:, K_PASS:T], late_work[2][:])
+            reversed_part = (work[1][:, T : T + 256], late_work[3][:, 0:256])
             identity_f32 = const.tile([P, P], F32)
             make_identity(nc, identity_f32[:])
+            nc.gpsimd.iota(t_int, pattern=[[1, T]], base=0, channel_multiplier=0)
             identity_bf16 = const.tile([P, P], BF16)
             make_identity(nc, identity_bf16[:])
-            nc.gpsimd.iota(t_int, pattern=[[1, T]], base=0, channel_multiplier=0)
             s_int = const.tile([P, CHUNKS], I32)
             nc.gpsimd.iota(s_int[:], pattern=[[P, CHUNKS]], base=0, channel_multiplier=1)
             t_in_block_int = const.tile([P, 2, HD // 2, 2], I32)
@@ -485,13 +566,6 @@ def tile_mixerblock_pa_kernel(tc, p, mix_w, mix_b, decay, out_w, out_b, x, out):
                 (odd_head, own_head[:, 1:2, :]),
             ):
                 nc.vector.tensor_reduce(out=dst[:], in_=heads, op=ALU.add, axis=AX.XY)
-            nc.vector.tensor_copy(out=t_row, in_=t_int)
-            spread = const.tile([P, P], BF16)
-            nc.vector.tensor_copy(
-                out=spread[:].rearrange("k (n h r) -> k n h r", h=2, r=PAIRS),
-                in_=identity_bf16[:, 0:H].rearrange("k (r h) -> k h r", h=2).unsqueeze(1).to_broadcast([P, P // H, 2, PAIRS]),
-            )
-
             d_clipped = const.tile([P, H], F32)
             nc.vector.tensor_scalar(
                 out=d_clipped[:], in0=decay_rows[:], scalar1=0.9, scalar2=1.0, op0=ALU.max, op1=ALU.min
@@ -509,6 +583,13 @@ def tile_mixerblock_pa_kernel(tc, p, mix_w, mix_b, decay, out_w, out_b, x, out):
             nc.vector.tensor_reduce(out=own_log[:], in_=own_logs[:], op=ALU.add, axis=AX.XY)
             own_rate = const.tile([P, 1], F32)
             nc.vector.tensor_scalar(out=own_rate[:], in0=own_log[:], scalar1=-0.5, scalar2=None, op0=ALU.mult)
+            for c in range(2):
+                nc.vector.tensor_copy(out=t_row[c], in_=t_int[:, c * K_PASS : (c + 1) * K_PASS])
+            spread = const.tile([P, P], BF16)
+            nc.vector.tensor_copy(
+                out=spread[:].rearrange("k (n h r) -> k n h r", h=2, r=PAIRS),
+                in_=identity_bf16[:, 0:H].rearrange("k (r h) -> k h r", h=2).unsqueeze(1).to_broadcast([P, P // H, 2, PAIRS]),
+            )
 
             parked = [out[B - 1, T // 2 + 256 * c : T // 2 + 256 * (c + 1), :] for c in range(2)]
 
@@ -517,19 +598,19 @@ def tile_mixerblock_pa_kernel(tc, p, mix_w, mix_b, decay, out_w, out_b, x, out):
                 own_w = psum_misc.tile([P, K_PASS], F32, name="own_w", tag="misc")
                 nc.tensor.matmul(out=own_w[:], lhsT=spread[:], rhs=mix_w_rows[:, steps], start=True, stop=True)
                 nc.vector.tensor_scalar(
-                    out=factor[:, steps],
+                    out=factor[c],
                     in0=own_w[:],
                     scalar1=late_head[:, 0:1],
                     scalar2=early_head[:, 0:1],
                     op0=ALU.mult,
                     op1=ALU.add,
                 )
-                nc.scalar.activation(out=t_row[:, steps], in_=t_row[:, steps], func=ACT.Exp, scale=own_rate[:, 0:1])
-                nc.vector.tensor_tensor(out=t_row[:, steps], in0=t_row[:, steps], in1=factor[:, steps], op=ALU.mult)
-                views = t_row[:, steps].rearrange("q (a r u e) -> q u a r e", a=4, u=2, e=2)
+                nc.scalar.activation(out=t_row[c], in_=t_row[c], func=ACT.Exp, scale=own_rate[:, 0:1])
+                nc.vector.tensor_tensor(out=t_row[c], in0=t_row[c], in1=factor[c], op=ALU.mult)
+                views = t_row[c].rearrange("q (a r u e) -> q u a r e", a=4, u=2, e=2)
                 for u in range(2):
                     nc.vector.tensor_scalar(
-                        out=reversed_part.rearrange("q (a r e) -> q a r e", a=4, e=2),
+                        out=reversed_part[c].rearrange("q (a r e) -> q a r e", a=4, e=2),
                         in0=views[:, u, ::-1, :, :],
                         scalar1=odd_head[:, 0:1],
                         scalar2=None,
@@ -539,16 +620,18 @@ def tile_mixerblock_pa_kernel(tc, p, mix_w, mix_b, decay, out_w, out_b, x, out):
                         out=left_parts[c][:, 256 * u : 256 * (u + 1)].rearrange("q (a r e) -> q a r e", a=4, e=2),
                         in0=views[:, u, :, :, :],
                         scalar=even_head[:, 0:1],
-                        in1=reversed_part.rearrange("q (a r e) -> q a r e", a=4, e=2),
+                        in1=reversed_part[c].rearrange("q (a r e) -> q a r e", a=4, e=2),
                         op0=ALU.mult,
                         op1=ALU.add,
                     )
                 copies = parked[c].rearrange("t v -> (t v)").rearrange("(n q v) -> n q v", q=P, v=K_PASS)
                 for n in range(COPIES * H // P):
-                    (nc.scalar if c == 0 else nc.sync).dma_start(out=copies[n], in_=left_parts[c])
+                    nc.sync.dma_start(out=copies[n], in_=left_parts[c])
 
             prepare_left(0)
             load_left(0, 0, 2)
+            nc.sync.dma_start(out=b_rows[:], in_=mix_b.rearrange("h (a q) -> (h a) q", q=P))
+            nc.sync.dma_start(out=out_b_rows[0 : E // P, :], in_=out_b.rearrange("(i q) -> i q", q=P))
             load_out_w(1)
             load_left(0, 2, PAIRS)
 
@@ -556,8 +639,6 @@ def tile_mixerblock_pa_kernel(tc, p, mix_w, mix_b, decay, out_w, out_b, x, out):
             nc.vector.tensor_copy(out=s_index[:], in_=s_int[:])
             w_turned = psum_misc.tile([P, P], BF16, name="w_turned", tag="misc")
             nc.tensor.transpose(out=w_turned[:], in_=w_rows[:], identity=identity_bf16[:])
-            b_turned = psum_misc.tile([P, P], BF16, name="b_turned", tag="misc")
-            nc.tensor.transpose(out=b_turned[:], in_=b_rows[:], identity=identity_bf16[:])
 
             exponent = const.tile([P, H, CHUNKS], F32)
             nc.vector.tensor_tensor(
@@ -586,14 +667,6 @@ def tile_mixerblock_pa_kernel(tc, p, mix_w, mix_b, decay, out_w, out_b, x, out):
             nc.vector.tensor_tensor(
                 out=right[:, 0:HALF_H, :], in0=right[:, 0:HALF_H, :], in1=w_by_s[:, 0:HALF_H, :], op=ALU.mult
             )
-            bias_by_s = const.tile([P, H, SWEEPS, 2 * B], F32)
-            turned = b_turned[:].rearrange("q (h c n e) -> q h c n e", h=H, c=2, n=2)
-            for sweep in range(SWEEPS):
-                nc.vector.tensor_copy(
-                    out=bias_by_s[:, :, sweep, :].rearrange("q h (n b) -> q h n b", b=B),
-                    in_=turned[:, :, sweep // 2, :, sweep % 2].unsqueeze(3).to_broadcast([P, H, 2, B]),
-                )
-
             for part in range(4):
                 if part < 3:
                     regroup_p(part, 0, nc.vector.tensor_copy)
@@ -604,28 +677,54 @@ def tile_mixerblock_pa_kernel(tc, p, mix_w, mix_b, decay, out_w, out_b, x, out):
             quantise_out_w(0)
             last_turn = -1
 
-            out_b_turned = psum_misc.tile([P, P], BF16, name="out_b_turned", tag="misc")
-            nc.tensor.transpose(out=out_b_turned[:], in_=out_b_rows[:], identity=identity_bf16[:])
+            bias_by_s = const.tile([P, H, SWEEPS, 2 * B], F32)
             out_b_column = const.tile([P, E // P], F32)
-            nc.vector.tensor_copy(out=out_b_column[:], in_=out_b_turned[:, 0 : E // P])
 
-            for step in range(-3, STEPS + 17):
-                item = step - 11
+            def turn_biases():
+                b_turned = psum_misc.tile([P, P], BF16, name="b_turned", tag="misc")
+                nc.tensor.transpose(out=b_turned[:], in_=b_rows[:], identity=identity_bf16[:])
+                turned = b_turned[:].rearrange("q (h c n e) -> q h c n e", h=H, c=2, n=2)
+                for sweep in range(SWEEPS):
+                    nc.vector.tensor_copy(
+                        out=bias_by_s[:, :, sweep, :].rearrange("q h (n b) -> q h n b", b=B),
+                        in_=turned[:, :, sweep // 2, :, sweep % 2].unsqueeze(3).to_broadcast([P, H, 2, B]),
+                    )
+                out_b_turned = psum_misc.tile([P, P], BF16, name="out_b_turned", tag="misc")
+                nc.tensor.transpose(out=out_b_turned[:], in_=out_b_rows[:], identity=identity_bf16[:])
+                nc.vector.tensor_copy(out=out_b_column[:], in_=out_b_turned[:, 0 : E // P])
+
+            project_at = [min(item, 20) + 11 + (item > 20) + (item > 22) for item in range(ITEMS)]
+            turn_at = [item + 16 if item < 17 else (31 + (item - 14) // 2 + (item > 19)) for item in range(ITEMS)]
+            for step in range(-3, STEPS + 8):
                 turn = (step - 5) // 4 if step % 4 == 1 else -1
+                if step in range(3, 11):
+                    load_left(1, 0, PAIRS, ((step - 3) % 2,), ((step - 3) // 2,))
                 if step == 2:
                     load_p(1)
-                load_x(item - 3)
+                for item in range(ITEMS):
+                    if turn_at[item] == step + 2:
+                        load_x(item)
+                if step == 25:
+                    nc.sync.dma_start(out=out_b_everywhere(), in_=out_b.partition_broadcast(P))
+                if 26 <= step < 30:
+                    load_last_x(2 * (step - 26))
                 make_m(step + 3)
                 mask_m(step + 2)
-                if step in range(8):
-                    load_left(1, 0, PAIRS, (step % 2,), (step // 2,))
                 part = step + 6 if step < 2 else step + 3
                 if step < 2 or 5 <= step < 13:
                     regroup_p(part, 0, nc.vector.tensor_copy)
                     regroup_p(part, 1, nc.scalar.copy)
-                transpose_m(step + 1)
+                transpose_m(step + 1, True)
+                if step < STEPS:
+                    for item in range(ITEMS):
+                        if project_at[item] == step:
+                            project(item)
+                keep_warm(step)
+                transpose_m(step + 1, False)
                 transpose_c(turn)
-                turn_back(item - 5)
+                for item in range(ITEMS):
+                    if turn_at[item] == step:
+                        turn_back(item)
                 quantise_m(step)
                 if step == -2:
                     regroup_out_w(1, nc.scalar.copy)
@@ -633,7 +732,9 @@ def tile_mixerblock_pa_kernel(tc, p, mix_w, mix_b, decay, out_w, out_b, x, out):
                 if step == -1:
                     quantise_out_w(1)
                     load_out_w(3)
-                if step == -3:
+                if step == -1:
+                    turn_biases()
+                if step == 0:
                     prepare_left(1)
                 if step in (1, 3):
                     regroup_out_w(2 + step // 2, nc.vector.tensor_copy)
@@ -642,13 +743,30 @@ def tile_mixerblock_pa_kernel(tc, p, mix_w, mix_b, decay, out_w, out_b, x, out):
                 if -3 < step <= 2 or 5 < step <= 13:
                     quantise_p(last_part)
                 last_part = part
-                quantise_c(last_turn)
-                last_turn = turn
+                quantise_c(last_turn, slice(0, 2))
+                last_turn = turn if turn < SWEEPS * GROUPS - 1 else -1
+                if turn == SWEEPS * GROUPS - 1:
+                    quantise_c(turn, slice(0, 1))
+                    quantise_c(turn, slice(1, 2))
                 add_bias(step - 1)
                 multiply(step)
                 for when, c, v, first, last in VARIANT_COPIES:
                     if when == step:
                         copy_variants(c, v, slice(first, last))
-                project(item)
-                add_out_b(item - 1)
-                add_x_and_store(item - 6)
+                for item in range(ITEMS):
+                    if project_at[item] == step >= STEPS:
+                        project(item)
+                if STEPS + 2 <= step < STEPS + 6:
+                    project_last(2 * (step - STEPS - 2))
+                    project_last(2 * (step - STEPS - 2) + 1)
+                for item in range(ITEMS):
+                    if project_at[item] + 1 == step:
+                        add_out_b(item)
+                for item in range(ITEMS):
+                    if turn_at[item] + 1 == step:
+                        add_x_and_store(item)
+                if 28 <= step < 32:
+                    add_out_b_to_x(2 * (step - 28))
+                if STEPS + 3 <= step < STEPS + 7:
+                    finish_last(2 * (step - STEPS - 3))
+                    finish_last(2 * (step - STEPS - 3) + 1)

@@ -39,7 +39,8 @@ VARIANT_COPIES = (
     (3, 0, 1, 0, 8), (12, 1, 0, 0, 4), (12, 1, 2, 0, 4), (16, 1, 0, 4, 8), (16, 1, 2, 4, 8), (17, 1, 1, 0, 8),
 )
 DRAIN_ON_VECTOR = ()
-ON_SCALAR = (((0, 2), (1, 2)), ((0, 3), (0, 1)), ((0, 0), (1, 0)), ((0, 3),))
+ON_SCALAR = (((), ()), ((), ((0, 3),)), (((0, 0),), ((0, 0),)), ((), ((0, 1),)))
+BIAS_ON_SCALAR = ((0, 1), (1,), (0, 1), (0, 1))
 
 FLOPS = 2 * B * H * HD * (K_PASS * N_TILE + T * N_TILE) + 2 * B * T * E * E
 
@@ -178,7 +179,7 @@ def tile_mixerblock_pa_kernel(tc, p, mix_w, mix_b, decay, out_w, out_b, x, out):
                 i = c * BLOCKS + chunk
                 src = left_rows[:, odd, pair, :, :, :].rearrange("p u c v -> p u (c v)")[:, :, first:last]
                 scale = right[:, h, i : i + 1]
-                if (odd, chunk) in ON_SCALAR[step // PAIRS]:
+                if (odd, chunk) in ON_SCALAR[step // PAIRS][pair // GROUP_PAIRS]:
                     nc.scalar.activation(out=dst, in_=src, func=ACT.Copy, scale=scale)
                 else:
                     nc.vector.tensor_scalar(out=dst, in0=src, scalar1=scale, scalar2=None, op0=ALU.mult)
@@ -280,28 +281,12 @@ def tile_mixerblock_pa_kernel(tc, p, mix_w, mix_b, decay, out_w, out_b, x, out):
                     )
                     first += count
 
-        def keep_warm(step):
-            if not 0 <= step < STEPS:
-                return
-            if step not in mixed:
-                mixed[step] = psum_mix.tile([P, 2, 2, B * HD], F32, name="mixed", tag="mixed")
-            if step >= PAIRS:
-                nc.tensor.matmul_mx(
-                    out=mixed[step][:].rearrange("p h n v -> p (h n v)"),
-                    lhsT=w_words[:, 0, 0:P].bitcast(FP8X4),
-                    lhsT_scale=w_scales[:, 0, 0:P],
-                    rhs=w_words[:, 0, 0:N_TILE].bitcast(FP8X4),
-                    rhs_scale=w_scales[:, 0, 0:N_TILE],
-                    start=True,
-                    stop=True,
-                )
-
         def multiply(step):
             if not 0 <= step < STEPS:
                 return
             c, half, pair = place_of(step)
             slots = {(what, chunk): n for n, (what, chunk, row, first) in enumerate(block_list(c, half))}
-            keep_warm(step)
+            mixed[step] = psum_mix.tile([P, 2, 2, B * HD], F32, name="mixed", tag="mixed")
             for odd in range(2):
                 for n in range(2):
                     chunk = half + 2 * n
@@ -336,14 +321,26 @@ def tile_mixerblock_pa_kernel(tc, p, mix_w, mix_b, decay, out_w, out_b, x, out):
             if pair_in_group == 0:
                 c_rows[where] = c_pool.tile([P, 2, B, K_PASS], BF16, name="c_rows")
             first = 2 * HD * pair_in_group
-            nc.vector.tensor_tensor(
-                out=c_rows[where][:, :, :, first : first + 2 * HD].rearrange("p n b (h f) -> p h (n b) f", h=2),
-                in0=mixed[step][:].rearrange("p h n (b f) -> p h (n b) f", b=B),
-                in1=bias_by_s[:, 2 * pair : 2 * pair + 2, step // PAIRS, :]
-                .unsqueeze(3)
-                .to_broadcast([P, 2, 2 * B, HD]),
-                op=ALU.add,
-            )
+            on_scalar = BIAS_ON_SCALAR[step // PAIRS]
+            for odd in on_scalar:
+                for n in range(2):
+                    nc.scalar.activation(
+                        out=c_rows[where][:, n, :, first + odd * HD : first + (odd + 1) * HD],
+                        in_=mixed[step][:, odd, n, :].rearrange("p (b f) -> p b f", b=B),
+                        func=ACT.Identity,
+                        bias=bias_by_s[:, 2 * pair + odd, step // PAIRS, 2 * n : 2 * n + 1],
+                    )
+            heads = slice(0, 2 - len(on_scalar))
+            count = heads.stop
+            if count:
+                nc.vector.tensor_tensor(
+                    out=c_rows[where][:, :, :, first : first + count * HD].rearrange("p n b (h f) -> p h (n b) f", h=count),
+                    in0=mixed[step][:, heads, :, :].rearrange("p h n (b f) -> p h (n b) f", b=B),
+                    in1=bias_by_s[:, 2 * pair : 2 * pair + count, step // PAIRS, :]
+                    .unsqueeze(3)
+                    .to_broadcast([P, count, 2 * B, HD]),
+                    op=ALU.add,
+                )
 
         def transpose_c(turn):
             if not 0 <= turn < SWEEPS * GROUPS:
@@ -524,7 +521,6 @@ def tile_mixerblock_pa_kernel(tc, p, mix_w, mix_b, decay, out_w, out_b, x, out):
             w_rows = const.tile([P, P], BF16)
             nc.sync.dma_start(out=w_rows[:], in_=mix_w.rearrange("h (a q) -> (h a) q", q=P))
             load_p(0)
-            load_out_w(0)
             b_rows = const.tile([P, P], BF16)
             out_b_rows = const.tile([P, P], BF16)
             nc.vector.memset(out_b_rows[:], 0.0)
@@ -545,6 +541,9 @@ def tile_mixerblock_pa_kernel(tc, p, mix_w, mix_b, decay, out_w, out_b, x, out):
             make_identity(nc, identity_bf16[:])
             s_int = const.tile([P, CHUNKS], I32)
             nc.gpsimd.iota(s_int[:], pattern=[[P, CHUNKS]], base=0, channel_multiplier=1)
+            position_int = const.tile([P, 2, 4], I32)
+            nc.gpsimd.iota(position_int[:, 0, :], pattern=[[2, 2], [256, 2]], base=0, channel_multiplier=2)
+            nc.gpsimd.iota(position_int[:, 1, :], pattern=[[2, 2], [-256, 2]], base=384, channel_multiplier=2)
             t_in_block_int = const.tile([P, 2, HD // 2, 2], I32)
             nc.gpsimd.iota(t_in_block_int[:], pattern=[[2, 2], [PACK, HD // 2], [1, 2]], base=0, channel_multiplier=0)
             nc.gpsimd.memset(variants[:].rearrange("q v r n -> q (v r n)").bitcast(I32), 0)
@@ -566,12 +565,48 @@ def tile_mixerblock_pa_kernel(tc, p, mix_w, mix_b, decay, out_w, out_b, x, out):
                 (odd_head, own_head[:, 1:2, :]),
             ):
                 nc.vector.tensor_reduce(out=dst[:], in_=heads, op=ALU.add, axis=AX.XY)
+            odd_value, late_block, both_values = (
+                const.tile([P, 1], F32, name=name) for name in ("odd_value", "late_block", "both_values")
+            )
+            for dst, cols in ((odd_value, identity_f32[:, 1:P:2]), (late_block, identity_f32[:, HD:P])):
+                nc.vector.tensor_reduce(out=dst[:], in_=cols, op=ALU.add, axis=AX.X)
+            nc.vector.scalar_tensor_tensor(
+                out=both_values[:], in0=late_block[:], scalar=256.0, in1=odd_value[:], op0=ALU.mult, op1=ALU.add
+            )
+            position = const.tile([P, 2, 4], F32)
+            for odd, less in ((0, odd_value), (1, both_values)):
+                nc.vector.tensor_scalar(
+                    out=position[:, odd, :], in0=position_int[:, odd, :], scalar1=less[:, 0:1], scalar2=None, op0=ALU.subtract
+                )
             d_clipped = const.tile([P, H], F32)
             nc.vector.tensor_scalar(
                 out=d_clipped[:], in0=decay_rows[:], scalar1=0.9, scalar2=1.0, op0=ALU.max, op1=ALU.min
             )
             log_d = const.tile([P, H], F32)
             nc.scalar.activation(out=log_d[:], in_=d_clipped[:], func=ACT.Ln)
+            left_columns = const.tile([P, PAIRS // 2, 2, 4], F32)
+            nc.vector.tensor_tensor(
+                out=left_columns[:],
+                in0=position[:].unsqueeze(1).to_broadcast([P, PAIRS // 2, 2, 4]),
+                in1=log_d[:, 0:HALF_H].rearrange("q (r h) -> q r h", h=2).unsqueeze(3).to_broadcast([P, PAIRS // 2, 2, 4]),
+                op=ALU.mult,
+            )
+            nc.scalar.activation(out=left_columns[:], in_=left_columns[:], func=ACT.Exp, scale=-0.5)
+
+            def spread_left(pair):
+                for odd in range(2):
+                    bank = psum_m.tile([P, 4, P], F32, name="left_spread", tag="m_psum")
+                    for k in range(4):
+                        nc.tensor.transpose(
+                            out=bank[:, k, :],
+                            in_=left_columns[:, pair, odd, k : k + 1].to_broadcast([P, P]),
+                            identity=identity_f32[:],
+                        )
+                    (nc.scalar.copy if odd or pair > 1 else nc.vector.tensor_copy)(
+                        out=left_rows[:, odd, pair, :, odd, :],
+                        in_=bank[:].rearrange("p (u i) n -> p u (i n)", u=2),
+                    )
+
             own_logs = const.tile([P, 2, PAIRS], F32)
             nc.vector.tensor_tensor(
                 out=own_logs[:],
@@ -605,7 +640,6 @@ def tile_mixerblock_pa_kernel(tc, p, mix_w, mix_b, decay, out_w, out_b, x, out):
                     op0=ALU.mult,
                     op1=ALU.add,
                 )
-                nc.scalar.activation(out=t_row[c], in_=t_row[c], func=ACT.Exp, scale=own_rate[:, 0:1])
                 nc.vector.tensor_tensor(out=t_row[c], in0=t_row[c], in1=factor[c], op=ALU.mult)
                 views = t_row[c].rearrange("q (a r u e) -> q u a r e", a=4, u=2, e=2)
                 for u in range(2):
@@ -628,12 +662,13 @@ def tile_mixerblock_pa_kernel(tc, p, mix_w, mix_b, decay, out_w, out_b, x, out):
                 for n in range(COPIES * H // P):
                     nc.sync.dma_start(out=copies[n], in_=left_parts[c])
 
+            for c in range(2):
+                nc.scalar.activation(out=t_row[c], in_=t_row[c], func=ACT.Exp, scale=own_rate[:, 0:1])
             prepare_left(0)
-            load_left(0, 0, 2)
             nc.sync.dma_start(out=b_rows[:], in_=mix_b.rearrange("h (a q) -> (h a) q", q=P))
             nc.sync.dma_start(out=out_b_rows[0 : E // P, :], in_=out_b.rearrange("(i q) -> i q", q=P))
-            load_out_w(1)
-            load_left(0, 2, PAIRS)
+            load_left(0, PAIRS // 2, PAIRS)
+            load_out_w(0)
 
             s_index = const.tile([P, CHUNKS], F32)
             nc.vector.tensor_copy(out=s_index[:], in_=s_int[:])
@@ -662,6 +697,8 @@ def tile_mixerblock_pa_kernel(tc, p, mix_w, mix_b, decay, out_w, out_b, x, out):
                     op0=ALU.is_le,
                 )
 
+            for pair in range(2):
+                spread_left(pair)
             w_by_s = const.tile([P, H, CHUNKS], F32)
             nc.vector.tensor_copy(out=w_by_s[:].rearrange("q h i -> q (h i)"), in_=w_turned[:])
             nc.vector.tensor_tensor(
@@ -673,8 +710,6 @@ def tile_mixerblock_pa_kernel(tc, p, mix_w, mix_b, decay, out_w, out_b, x, out):
                     regroup_p(part, 1, nc.scalar.copy)
                 if part > 0:
                     quantise_p(part - 1)
-            regroup_out_w(0, nc.vector.tensor_copy)
-            quantise_out_w(0)
             last_turn = -1
 
             bias_by_s = const.tile([P, H, SWEEPS, 2 * B], F32)
@@ -697,8 +732,8 @@ def tile_mixerblock_pa_kernel(tc, p, mix_w, mix_b, decay, out_w, out_b, x, out):
             turn_at = [item + 16 if item < 17 else (31 + (item - 14) // 2 + (item > 19)) for item in range(ITEMS)]
             for step in range(-3, STEPS + 8):
                 turn = (step - 5) // 4 if step % 4 == 1 else -1
-                if step in range(3, 11):
-                    load_left(1, 0, PAIRS, ((step - 3) % 2,), ((step - 3) // 2,))
+                if step in range(5, 9):
+                    load_left(1, 0, PAIRS, ks=(step - 5,))
                 if step == 2:
                     load_p(1)
                 for item in range(ITEMS):
@@ -710,6 +745,12 @@ def tile_mixerblock_pa_kernel(tc, p, mix_w, mix_b, decay, out_w, out_b, x, out):
                     load_last_x(2 * (step - 26))
                 make_m(step + 3)
                 mask_m(step + 2)
+                for item in range(ITEMS):
+                    if project_at[item] + 1 == step:
+                        add_out_b(item)
+                for item in range(ITEMS):
+                    if turn_at[item] + 1 == step:
+                        add_x_and_store(item)
                 part = step + 6 if step < 2 else step + 3
                 if step < 2 or 5 <= step < 13:
                     regroup_p(part, 0, nc.vector.tensor_copy)
@@ -719,27 +760,26 @@ def tile_mixerblock_pa_kernel(tc, p, mix_w, mix_b, decay, out_w, out_b, x, out):
                     for item in range(ITEMS):
                         if project_at[item] == step:
                             project(item)
-                keep_warm(step)
                 transpose_m(step + 1, False)
                 transpose_c(turn)
                 for item in range(ITEMS):
                     if turn_at[item] == step:
                         turn_back(item)
                 quantise_m(step)
-                if step == -2:
-                    regroup_out_w(1, nc.scalar.copy)
-                    load_out_w(2)
-                if step == -1:
-                    quantise_out_w(1)
-                    load_out_w(3)
+                if step == -3:
+                    for pair in range(2, PAIRS // 2):
+                        spread_left(pair)
                 if step == -1:
                     turn_biases()
-                if step == 0:
+                    load_out_w(1)
+                if step == 3:
                     prepare_left(1)
-                if step in (1, 3):
-                    regroup_out_w(2 + step // 2, nc.vector.tensor_copy)
-                if step in (2, 4):
-                    quantise_out_w(1 + step // 2)
+                if step in (0, 2, 4, 6):
+                    regroup_out_w(step // 2, nc.scalar.copy if step < 4 else nc.vector.tensor_copy)
+                if step in (1, 3, 5, 7):
+                    quantise_out_w(step // 2)
+                    if step < 5:
+                        load_out_w(2 + step // 2)
                 if -3 < step <= 2 or 5 < step <= 13:
                     quantise_p(last_part)
                 last_part = part
@@ -759,12 +799,6 @@ def tile_mixerblock_pa_kernel(tc, p, mix_w, mix_b, decay, out_w, out_b, x, out):
                 if STEPS + 2 <= step < STEPS + 6:
                     project_last(2 * (step - STEPS - 2))
                     project_last(2 * (step - STEPS - 2) + 1)
-                for item in range(ITEMS):
-                    if project_at[item] + 1 == step:
-                        add_out_b(item)
-                for item in range(ITEMS):
-                    if turn_at[item] + 1 == step:
-                        add_x_and_store(item)
                 if 28 <= step < 32:
                     add_out_b_to_x(2 * (step - 28))
                 if STEPS + 3 <= step < STEPS + 7:

@@ -281,12 +281,27 @@ def tile_mixerblock_pa_kernel(tc, p, mix_w, mix_b, decay, out_w, out_b, x, out):
                     )
                     first += count
 
+        def keep_warm(step):
+            if not 0 <= step < STEPS:
+                return
+            if step not in mixed:
+                mixed[step] = psum_mix.tile([P, 2, 2, B * HD], F32, name="mixed", tag="mixed")
+            nc.tensor.matmul_mx(
+                out=mixed[step][:].rearrange("p h n v -> p (h n v)"),
+                lhsT=p_words[:, 0, 0:P].bitcast(FP8X4),
+                lhsT_scale=p_scales[:, 0, 0:P],
+                rhs=p_words[:, 0:2, :].rearrange("q r n -> q (r n)").bitcast(FP8X4),
+                rhs_scale=p_scales[:, 0:2, :].rearrange("q r n -> q (r n)"),
+                start=True,
+                stop=True,
+            )
+
         def multiply(step):
             if not 0 <= step < STEPS:
                 return
             c, half, pair = place_of(step)
             slots = {(what, chunk): n for n, (what, chunk, row, first) in enumerate(block_list(c, half))}
-            mixed[step] = psum_mix.tile([P, 2, 2, B * HD], F32, name="mixed", tag="mixed")
+            keep_warm(step)
             for odd in range(2):
                 for n in range(2):
                     chunk = half + 2 * n
@@ -760,6 +775,7 @@ def tile_mixerblock_pa_kernel(tc, p, mix_w, mix_b, decay, out_w, out_b, x, out):
                     for item in range(ITEMS):
                         if project_at[item] == step:
                             project(item)
+                keep_warm(step)
                 transpose_m(step + 1, False)
                 transpose_c(turn)
                 for item in range(ITEMS):

@@ -31,6 +31,7 @@ ITEMS = (SWEEPS - 1) * (E // P)
 LAST_ITEMS = E // P
 COPIES = 32
 MAX_BLOCKS = 7
+ONES = 32
 ROW_WIDTH = ((256, 512), (768, 1024))
 M_ROWS = 4672
 VARIANT_COPIES = (
@@ -39,8 +40,8 @@ VARIANT_COPIES = (
     (3, 0, 1, 0, 8), (12, 1, 0, 0, 4), (12, 1, 2, 0, 4), (16, 1, 0, 4, 8), (16, 1, 2, 4, 8), (17, 1, 1, 0, 8),
 )
 DRAIN_ON_VECTOR = ()
-ON_SCALAR = (((), ()), ((), ((0, 3),)), (((0, 0),), ((0, 0),)), ((), ((0, 1),)))
-BIAS_ON_SCALAR = ((0, 1), (1,), (0, 1), (0, 1))
+ON_SCALAR = (((), ()), (((0, 3),), ((0, 3),)), (((0, 0),), ((0, 0),)), ((), ((0, 1),)))
+BIAS_ON_SCALAR = ((0, 1), (), (0, 1), (0, 1))
 
 FLOPS = 2 * B * H * HD * (K_PASS * N_TILE + T * N_TILE) + 2 * B * T * E * E
 
@@ -91,12 +92,12 @@ def tile_mixerblock_pa_kernel(tc, p, mix_w, mix_b, decay, out_w, out_b, x, out):
 
         def regroup_p(part, odd, engine_copy):
             c, pair = divmod(part, PAIRS)
-            if odd == 0:
-                p_grouped[part] = p_grouped_pool.tile(
-                    [P, 2, B, HD, PACK], BF16, name="p_grouped", tag="p_grouped", align_bytes=64
+            if odd == 0 and part % 2 == 0:
+                p_grouped[part // 2] = p_grouped_pool.tile(
+                    [P, 2, 2, B, HD, PACK], BF16, name="p_grouped", tag="p_grouped", align_bytes=64
                 )
             engine_copy(
-                out=p_grouped[part][:, odd, :, :, :],
+                out=p_grouped[part // 2][:, part % 2, odd, :, :, :],
                 in_=p_raw[(c, odd)][:]
                 .rearrange("q (b r) v -> q b r v", b=B)[:, :, pair, :]
                 .rearrange("q b (j f) -> q b f j", j=PACK),
@@ -104,9 +105,9 @@ def tile_mixerblock_pa_kernel(tc, p, mix_w, mix_b, decay, out_w, out_b, x, out):
 
         def quantise_p(part):
             nc.vector.quantize_mx(
-                out=p_words[:, part, :].bitcast(FP8X4),
-                scales=p_scales[:, part, :],
-                in_=p_grouped[part][:].rearrange("q h b f j -> q (h b f j)"),
+                out=p_words[:, part : part + 2, :].rearrange("q r n -> q (r n)").bitcast(FP8X4),
+                scales=p_scales[:, part : part + 2, :].rearrange("q r n -> q (r n)"),
+                in_=p_grouped[part // 2][:].rearrange("q r h b f j -> q (r h b f j)"),
             )
 
         def p_cols(odd):
@@ -152,7 +153,7 @@ def tile_mixerblock_pa_kernel(tc, p, mix_w, mix_b, decay, out_w, out_b, x, out):
             return step // PAIRS // 2, step // PAIRS % 2, step % PAIRS
 
         def load_left(c, first, last, odds=(0, 1), ks=range(P // COPIES)):
-            copies = parked[c].rearrange("t v -> (t v)").rearrange("(n h r v) -> h n r v", n=COPIES, h=2, v=256)
+            copies = parked[c].rearrange("t v -> (t v)").rearrange("(h n r v) -> h n r v", n=COPIES, h=2, v=256)
             for odd in odds:
                 for k in ks:
                     nc.sync.dma_start(
@@ -231,6 +232,17 @@ def tile_mixerblock_pa_kernel(tc, p, mix_w, mix_b, decay, out_w, out_b, x, out):
                 found += [(name, 3, 3, 256 * n) for n, name in enumerate(names)]
             return found
 
+        def keep_warm(bank):
+            nc.tensor.matmul_mx(
+                out=bank,
+                lhsT=p_words[:, 0, 0:P].bitcast(FP8X4),
+                lhsT_scale=p_scales[:, 0, 0:P],
+                rhs=p_words[:, 0:2, :].rearrange("q r n -> q (r n)").bitcast(FP8X4),
+                rhs_scale=p_scales[:, 0:2, :].rearrange("q r n -> q (r n)"),
+                start=True,
+                stop=True,
+            )
+
         def transpose_m(step, first_part):
             if not 0 <= step < STEPS:
                 return
@@ -247,6 +259,8 @@ def tile_mixerblock_pa_kernel(tc, p, mix_w, mix_b, decay, out_w, out_b, x, out):
             for n in range(0, middle, 2) if first_part else range(middle, len(found), 2):
                 count = min(2, len(found) - n)
                 bank = psum_m.tile([P, 2, 2, P], F32, name="m_psum", tag="m_psum")
+                if n == middle:
+                    keep_warm(bank[:].rearrange("q i u s -> q (i u s)"))
                 for i in range(count):
                     what, chunk, row, first = found[n + i]
                     for u in range(2):
@@ -281,27 +295,13 @@ def tile_mixerblock_pa_kernel(tc, p, mix_w, mix_b, decay, out_w, out_b, x, out):
                     )
                     first += count
 
-        def keep_warm(step):
-            if not 0 <= step < STEPS:
-                return
-            if step not in mixed:
-                mixed[step] = psum_mix.tile([P, 2, 2, B * HD], F32, name="mixed", tag="mixed")
-            nc.tensor.matmul_mx(
-                out=mixed[step][:].rearrange("p h n v -> p (h n v)"),
-                lhsT=p_words[:, 0, 0:P].bitcast(FP8X4),
-                lhsT_scale=p_scales[:, 0, 0:P],
-                rhs=p_words[:, 0:2, :].rearrange("q r n -> q (r n)").bitcast(FP8X4),
-                rhs_scale=p_scales[:, 0:2, :].rearrange("q r n -> q (r n)"),
-                start=True,
-                stop=True,
-            )
-
         def multiply(step):
             if not 0 <= step < STEPS:
                 return
             c, half, pair = place_of(step)
             slots = {(what, chunk): n for n, (what, chunk, row, first) in enumerate(block_list(c, half))}
-            keep_warm(step)
+            mixed[step] = psum_mix.tile([P, 2, 2, B * HD], F32, name="mixed", tag="mixed")
+            keep_warm(mixed[step][:].rearrange("p h n v -> p (h n v)"))
             for odd in range(2):
                 for n in range(2):
                     chunk = half + 2 * n
@@ -336,6 +336,7 @@ def tile_mixerblock_pa_kernel(tc, p, mix_w, mix_b, decay, out_w, out_b, x, out):
             if pair_in_group == 0:
                 c_rows[where] = c_pool.tile([P, 2, B, K_PASS], BF16, name="c_rows")
             first = 2 * HD * pair_in_group
+            chunk = c * BLOCKS + half
             on_scalar = BIAS_ON_SCALAR[step // PAIRS]
             for odd in on_scalar:
                 for n in range(2):
@@ -343,19 +344,19 @@ def tile_mixerblock_pa_kernel(tc, p, mix_w, mix_b, decay, out_w, out_b, x, out):
                         out=c_rows[where][:, n, :, first + odd * HD : first + (odd + 1) * HD],
                         in_=mixed[step][:, odd, n, :].rearrange("p (b f) -> p b f", b=B),
                         func=ACT.Identity,
-                        bias=bias_by_s[:, 2 * pair + odd, step // PAIRS, 2 * n : 2 * n + 1],
+                        bias=bias_by_s[:, 2 * pair + odd, chunk + 2 * n : chunk + 2 * n + 1],
                     )
-            heads = slice(0, 2 - len(on_scalar))
-            count = heads.stop
-            if count:
-                nc.vector.tensor_tensor(
-                    out=c_rows[where][:, :, :, first : first + count * HD].rearrange("p n b (h f) -> p h (n b) f", h=count),
-                    in0=mixed[step][:, heads, :, :].rearrange("p h n (b f) -> p h (n b) f", b=B),
-                    in1=bias_by_s[:, 2 * pair : 2 * pair + count, step // PAIRS, :]
-                    .unsqueeze(3)
-                    .to_broadcast([P, count, 2 * B, HD]),
-                    op=ALU.add,
-                )
+            for odd in range(2):
+                if odd not in on_scalar:
+                    nc.vector.tensor_tensor(
+                        out=c_rows[where][:, :, :, first + odd * HD : first + (odd + 1) * HD],
+                        in0=mixed[step][:, odd, :, :].rearrange("p n (b f) -> p n b f", b=B),
+                        in1=bias_by_s[:, 2 * pair + odd, chunk : chunk + 3 : 2]
+                        .unsqueeze(2)
+                        .unsqueeze(3)
+                        .to_broadcast([P, 2, B, HD]),
+                        op=ALU.add,
+                    )
 
         def transpose_c(turn):
             if not 0 <= turn < SWEEPS * GROUPS:
@@ -531,7 +532,8 @@ def tile_mixerblock_pa_kernel(tc, p, mix_w, mix_b, decay, out_w, out_b, x, out):
             decay_rows = const.tile([P, H], BF16)
             nc.sync.dma_start(out=decay_rows[:], in_=decay.partition_broadcast(P))
             mix_w_rows = quarter_pool.tile([P, T], BF16, name="mix_w_rows", tag="quarter", align_bytes=64)
-            nc.gpsimd.memset(mix_w_rows[:].bitcast(I32), 0)
+            nc.vector.memset(mix_w_rows[:].bitcast(I32), 0)
+            nc.vector.memset(mix_w_rows[ONES : ONES + 32, :], 1.0)
             nc.sync.dma_start(out=mix_w_rows[0:H, :], in_=mix_w[:, :])
             w_rows = const.tile([P, P], BF16)
             nc.sync.dma_start(out=w_rows[:], in_=mix_w.rearrange("h (a q) -> (h a) q", q=P))
@@ -540,86 +542,81 @@ def tile_mixerblock_pa_kernel(tc, p, mix_w, mix_b, decay, out_w, out_b, x, out):
             out_b_rows = const.tile([P, P], BF16)
             nc.vector.memset(out_b_rows[:], 0.0)
 
-            work = [
-                rows_pool.tile([P, M_ROWS // 2], F32, name="work", tag="m_rows", align_bytes=64) for n in range(2)
-            ]
-            late_work = [x_pool.tile([P, K_PASS], F32, name="late_work", tag="x_raw") for n in range(4)]
-            t_int = work[0][:, 0:T].bitcast(I32)
-            t_row = (work[0][:, T : T + K_PASS], late_work[0][:])
-            factor = (work[1][:, 0:K_PASS], late_work[1][:])
-            left_parts = (work[1][:, K_PASS:T], late_work[2][:])
-            reversed_part = (work[1][:, T : T + 256], late_work[3][:, 0:256])
+            def iota(dst, pattern, base, channel_multiplier):
+                nc.gpsimd.iota(
+                    dst,
+                    pattern=pattern,
+                    base=base,
+                    channel_multiplier=channel_multiplier,
+                    allow_small_or_imprecise_dtypes=True,
+                )
+
             identity_f32 = const.tile([P, P], F32)
             make_identity(nc, identity_f32[:])
-            nc.gpsimd.iota(t_int, pattern=[[1, T]], base=0, channel_multiplier=0)
+            t_column = const.tile([P, PACK], F32)
+            iota(t_column[:], [[1, PACK]], 0, PACK)
+            t_row = x_pool.tile([P, K_PASS], F32, name="t_row", tag="x_raw")
+            iota(t_row[0 : P // 2, :], [[2, 2], [P, BLOCKS], [PACK, HD // 2], [1, 2]], 0, 0)
+            iota(t_row[P // 2 : P, :], [[2, 2], [-P, BLOCKS], [PACK, HD // 2], [1, 2]], K_PASS - P, 0)
+            s_index = const.tile([P, CHUNKS], F32)
+            iota(s_index[:], [[P, CHUNKS]], 0, 1)
+            t_in_block = const.tile([P, 2, HD], F32)
+            iota(t_in_block[:].rearrange("q u (r e) -> q u r e", e=2), [[2, 2], [PACK, HD // 2], [1, 2]], 0, 0)
             identity_bf16 = const.tile([P, P], BF16)
             make_identity(nc, identity_bf16[:])
-            s_int = const.tile([P, CHUNKS], I32)
-            nc.gpsimd.iota(s_int[:], pattern=[[P, CHUNKS]], base=0, channel_multiplier=1)
-            position_int = const.tile([P, 2, 4], I32)
-            nc.gpsimd.iota(position_int[:, 0, :], pattern=[[2, 2], [256, 2]], base=0, channel_multiplier=2)
-            nc.gpsimd.iota(position_int[:, 1, :], pattern=[[2, 2], [-256, 2]], base=384, channel_multiplier=2)
-            t_in_block_int = const.tile([P, 2, HD // 2, 2], I32)
-            nc.gpsimd.iota(t_in_block_int[:], pattern=[[2, 2], [PACK, HD // 2], [1, 2]], base=0, channel_multiplier=0)
+            spread = const.tile([P, 2, P], BF16)
+            nc.gpsimd.memset(spread[:], 0.0)
+            for odd in range(2):
+                own = spread[:, odd, odd * HD : (odd + 1) * HD].rearrange("k (n r) -> k n r", r=PAIRS)
+                nc.gpsimd.tensor_copy(
+                    out=own[:, :, PAIRS // 2 : PAIRS],
+                    in_=identity_bf16[:, HALF_H + odd : H : 2].unsqueeze(1).to_broadcast([P, PAIRS, PAIRS // 2]),
+                )
+                nc.gpsimd.tensor_copy(
+                    out=own[:, :, 0 : PAIRS // 2],
+                    in_=identity_bf16[:, ONES : ONES + 1].unsqueeze(2).to_broadcast([P, PAIRS, PAIRS // 2]),
+                )
             nc.gpsimd.memset(variants[:].rearrange("q v r n -> q (v r n)").bitcast(I32), 0)
 
             own_head = const.tile([P, 2, PAIRS], F32)
             nc.vector.tensor_reduce(
-                out=own_head[:].rearrange("q h r -> q (h r)"),
-                in_=identity_f32[:].rearrange("q (n h) -> q h n", h=H),
+                out=own_head[:],
+                in_=identity_f32[:].rearrange("q (h n r) -> q h r n", h=2, r=PAIRS),
                 op=ALU.add,
                 axis=AX.X,
             )
-            early_head, late_head, even_head, odd_head = (
-                const.tile([P, 1], F32, name=name) for name in ("early_head", "late_head", "even_head", "odd_head")
+            reversed_identity = const.tile([P, P], F32)
+            nc.vector.tensor_copy(
+                out=reversed_identity[:].rearrange("q (a r) -> q a r", a=BLOCKS),
+                in_=identity_f32[:].rearrange("q (a r) -> q a r", a=BLOCKS)[:, ::-1, :],
             )
-            for dst, heads in (
-                (early_head, own_head[:, :, 0 : PAIRS // 2]),
-                (late_head, own_head[:, :, PAIRS // 2 : PAIRS]),
-                (even_head, own_head[:, 0:1, :]),
-                (odd_head, own_head[:, 1:2, :]),
-            ):
-                nc.vector.tensor_reduce(out=dst[:], in_=heads, op=ALU.add, axis=AX.XY)
-            odd_value, late_block, both_values = (
-                const.tile([P, 1], F32, name=name) for name in ("odd_value", "late_block", "both_values")
-            )
-            for dst, cols in ((odd_value, identity_f32[:, 1:P:2]), (late_block, identity_f32[:, HD:P])):
-                nc.vector.tensor_reduce(out=dst[:], in_=cols, op=ALU.add, axis=AX.X)
-            nc.vector.scalar_tensor_tensor(
-                out=both_values[:], in0=late_block[:], scalar=256.0, in1=odd_value[:], op0=ALU.mult, op1=ALU.add
-            )
-            position = const.tile([P, 2, 4], F32)
-            for odd, less in ((0, odd_value), (1, both_values)):
-                nc.vector.tensor_scalar(
-                    out=position[:, odd, :], in0=position_int[:, odd, :], scalar1=less[:, 0:1], scalar2=None, op0=ALU.subtract
-                )
             d_clipped = const.tile([P, H], F32)
             nc.vector.tensor_scalar(
                 out=d_clipped[:], in0=decay_rows[:], scalar1=0.9, scalar2=1.0, op0=ALU.max, op1=ALU.min
             )
             log_d = const.tile([P, H], F32)
             nc.scalar.activation(out=log_d[:], in_=d_clipped[:], func=ACT.Ln)
-            left_columns = const.tile([P, PAIRS // 2, 2, 4], F32)
+            left_columns = const.tile([P, PAIRS // 2, 2, PACK], F32)
             nc.vector.tensor_tensor(
                 out=left_columns[:],
-                in0=position[:].unsqueeze(1).to_broadcast([P, PAIRS // 2, 2, 4]),
-                in1=log_d[:, 0:HALF_H].rearrange("q (r h) -> q r h", h=2).unsqueeze(3).to_broadcast([P, PAIRS // 2, 2, 4]),
+                in0=t_column[:].unsqueeze(1).unsqueeze(1).to_broadcast([P, PAIRS // 2, 2, PACK]),
+                in1=log_d[:, 0:HALF_H].rearrange("q (r h) -> q r h", h=2).unsqueeze(3).to_broadcast([P, PAIRS // 2, 2, PACK]),
                 op=ALU.mult,
             )
             nc.scalar.activation(out=left_columns[:], in_=left_columns[:], func=ACT.Exp, scale=-0.5)
 
             def spread_left(pair):
                 for odd in range(2):
-                    bank = psum_m.tile([P, 4, P], F32, name="left_spread", tag="m_psum")
-                    for k in range(4):
+                    bank = psum_m.tile([P, PACK, P], F32, name="left_spread", tag="m_psum")
+                    for k in range(PACK):
                         nc.tensor.transpose(
                             out=bank[:, k, :],
                             in_=left_columns[:, pair, odd, k : k + 1].to_broadcast([P, P]),
-                            identity=identity_f32[:],
+                            identity=reversed_identity[:] if odd else identity_f32[:],
                         )
                     (nc.scalar.copy if odd or pair > 1 else nc.vector.tensor_copy)(
-                        out=left_rows[:, odd, pair, :, odd, :],
-                        in_=bank[:].rearrange("p (u i) n -> p u (i n)", u=2),
+                        out=left_rows[:, odd, pair, :, odd, :].rearrange("p u (m e) -> p u m e", e=2),
+                        in_=bank[:].rearrange("p (u e) m -> p u m e", u=2),
                     )
 
             own_logs = const.tile([P, 2, PAIRS], F32)
@@ -631,114 +628,95 @@ def tile_mixerblock_pa_kernel(tc, p, mix_w, mix_b, decay, out_w, out_b, x, out):
             )
             own_log = const.tile([P, 1], F32)
             nc.vector.tensor_reduce(out=own_log[:], in_=own_logs[:], op=ALU.add, axis=AX.XY)
-            own_rate = const.tile([P, 1], F32)
-            nc.vector.tensor_scalar(out=own_rate[:], in0=own_log[:], scalar1=-0.5, scalar2=None, op0=ALU.mult)
-            for c in range(2):
-                nc.vector.tensor_copy(out=t_row[c], in_=t_int[:, c * K_PASS : (c + 1) * K_PASS])
-            spread = const.tile([P, P], BF16)
-            nc.vector.tensor_copy(
-                out=spread[:].rearrange("k (n h r) -> k n h r", h=2, r=PAIRS),
-                in_=identity_bf16[:, 0:H].rearrange("k (r h) -> k h r", h=2).unsqueeze(1).to_broadcast([P, P // H, 2, PAIRS]),
+            own_rate = const.tile([P, 2], F32)
+            for k in range(2):
+                nc.vector.tensor_scalar(
+                    out=own_rate[:, k : k + 1],
+                    in0=own_log[:],
+                    scalar1=-0.5 * K_PASS**k,
+                    scalar2=None,
+                    op0=ALU.mult,
+                )
+
+            left_parts = [x_pool.tile([P, K_PASS], F32, name="left_parts", tag="x_raw") for c in range(2)]
+            parked = [out[B - 1, T // 2 + 256 * c : T // 2 + 256 * (c + 1), :] for c in range(2)]
+            nc.scalar.activation(out=left_parts[0][:], in_=t_row[:], func=ACT.Exp, scale=own_rate[:, 0:1])
+            nc.scalar.activation(
+                out=left_parts[1][:], in_=t_row[:], func=ACT.Exp, scale=own_rate[:, 0:1], bias=own_rate[:, 1:2]
             )
 
-            parked = [out[B - 1, T // 2 + 256 * c : T // 2 + 256 * (c + 1), :] for c in range(2)]
-
             def prepare_left(c):
-                steps = slice(c * K_PASS, (c + 1) * K_PASS)
                 own_w = psum_misc.tile([P, K_PASS], F32, name="own_w", tag="misc")
-                nc.tensor.matmul(out=own_w[:], lhsT=spread[:], rhs=mix_w_rows[:, steps], start=True, stop=True)
-                nc.vector.tensor_scalar(
-                    out=factor[c],
-                    in0=own_w[:],
-                    scalar1=late_head[:, 0:1],
-                    scalar2=early_head[:, 0:1],
-                    op0=ALU.mult,
-                    op1=ALU.add,
+                weights = mix_w_rows[:, c * K_PASS : (c + 1) * K_PASS]
+                nc.tensor.matmul(
+                    out=own_w[:].rearrange("q (u n e) -> q u n e", u=2, e=2),
+                    lhsT=spread[:, 0, :],
+                    rhs=weights.rearrange("k (n u e) -> k u n e", u=2, e=2),
+                    start=True,
+                    stop=False,
                 )
-                nc.vector.tensor_tensor(out=t_row[c], in0=t_row[c], in1=factor[c], op=ALU.mult)
-                views = t_row[c].rearrange("q (a r u e) -> q u a r e", a=4, u=2, e=2)
-                for u in range(2):
-                    nc.vector.tensor_scalar(
-                        out=reversed_part[c].rearrange("q (a r e) -> q a r e", a=4, e=2),
-                        in0=views[:, u, ::-1, :, :],
-                        scalar1=odd_head[:, 0:1],
-                        scalar2=None,
-                        op0=ALU.mult,
+                for a in range(BLOCKS):
+                    nc.tensor.matmul(
+                        out=own_w[:].rearrange("q (u a r e) -> q a u r e", u=2, a=BLOCKS, e=2)[:, BLOCKS - 1 - a],
+                        lhsT=spread[:, 1, :],
+                        rhs=weights.rearrange("k (a r u e) -> k a u r e", a=BLOCKS, u=2, e=2)[:, a],
+                        start=False,
+                        stop=(a == BLOCKS - 1),
                     )
-                    nc.vector.scalar_tensor_tensor(
-                        out=left_parts[c][:, 256 * u : 256 * (u + 1)].rearrange("q (a r e) -> q a r e", a=4, e=2),
-                        in0=views[:, u, :, :, :],
-                        scalar=even_head[:, 0:1],
-                        in1=reversed_part[c].rearrange("q (a r e) -> q a r e", a=4, e=2),
-                        op0=ALU.mult,
-                        op1=ALU.add,
-                    )
-                copies = parked[c].rearrange("t v -> (t v)").rearrange("(n q v) -> n q v", q=P, v=K_PASS)
-                for n in range(COPIES * H // P):
-                    nc.sync.dma_start(out=copies[n], in_=left_parts[c])
+                nc.vector.tensor_tensor(out=left_parts[c][:], in0=own_w[:], in1=left_parts[c][:], op=ALU.mult)
+                copies = parked[c].rearrange("t v -> (t v)").rearrange("(h n q v) -> h n q v", h=2, q=HD, v=K_PASS)
+                for n in range(COPIES * PAIRS // HD):
+                    for odd in range(2):
+                        nc.sync.dma_start(out=copies[odd, n], in_=left_parts[c][odd * HD : (odd + 1) * HD, :])
 
-            for c in range(2):
-                nc.scalar.activation(out=t_row[c], in_=t_row[c], func=ACT.Exp, scale=own_rate[:, 0:1])
-            prepare_left(0)
             nc.sync.dma_start(out=b_rows[:], in_=mix_b.rearrange("h (a q) -> (h a) q", q=P))
             nc.sync.dma_start(out=out_b_rows[0 : E // P, :], in_=out_b.rearrange("(i q) -> i q", q=P))
-            load_left(0, PAIRS // 2, PAIRS)
             load_out_w(0)
 
-            s_index = const.tile([P, CHUNKS], F32)
-            nc.vector.tensor_copy(out=s_index[:], in_=s_int[:])
-            w_turned = psum_misc.tile([P, P], BF16, name="w_turned", tag="misc")
-            nc.tensor.transpose(out=w_turned[:], in_=w_rows[:], identity=identity_bf16[:])
-
-            exponent = const.tile([P, H, CHUNKS], F32)
+            right = const.tile([P, H, CHUNKS], F32)
             nc.vector.tensor_tensor(
-                out=exponent[:],
+                out=right[:],
                 in0=s_index[:].unsqueeze(1).to_broadcast([P, H, CHUNKS]),
                 in1=log_d[:].unsqueeze(2).to_broadcast([P, H, CHUNKS]),
                 op=ALU.mult,
             )
-            right = const.tile([P, H, CHUNKS], F32)
-            nc.scalar.activation(out=right[:], in_=exponent[:], func=ACT.Exp, scale=0.5)
+            nc.scalar.activation(out=right[:], in_=right[:], func=ACT.Exp, scale=0.5)
 
-            t_in_block = const.tile([P, 2, HD], F32)
-            nc.vector.tensor_copy(out=t_in_block[:], in_=t_in_block_int[:].rearrange("q u r e -> q u (r e)"))
             triangles = const.tile([P, 2, 2 * HD], BF16)
-            for n in range(2):
-                nc.vector.tensor_scalar(
-                    out=triangles[:, :, n * HD : (n + 1) * HD],
-                    in0=t_in_block[:],
-                    scalar1=s_index[:, 0:1],
-                    scalar2=None,
-                    op0=ALU.is_le,
-                )
+            nc.vector.tensor_scalar(
+                out=triangles[:].rearrange("q u (n v) -> q u n v", n=2),
+                in0=t_in_block[:].unsqueeze(2).to_broadcast([P, 2, 2, HD]),
+                scalar1=s_index[:, 0:1],
+                scalar2=None,
+                op0=ALU.is_le,
+            )
 
             for pair in range(2):
                 spread_left(pair)
-            w_by_s = const.tile([P, H, CHUNKS], F32)
-            nc.vector.tensor_copy(out=w_by_s[:].rearrange("q h i -> q (h i)"), in_=w_turned[:])
-            nc.vector.tensor_tensor(
-                out=right[:, 0:HALF_H, :], in0=right[:, 0:HALF_H, :], in1=w_by_s[:, 0:HALF_H, :], op=ALU.mult
+            w_turned = psum_misc.tile([P, H, CHUNKS], BF16, name="w_turned", tag="misc")
+            nc.tensor.transpose(
+                out=w_turned[:].rearrange("q h i -> q (h i)"), in_=w_rows[:], identity=identity_bf16[:]
             )
+
+            nc.vector.tensor_tensor(
+                out=right[:, 0:HALF_H, :], in0=right[:, 0:HALF_H, :], in1=w_turned[:, 0:HALF_H, :], op=ALU.mult
+            )
+            prepare_left(0)
             for part in range(4):
-                if part < 3:
-                    regroup_p(part, 0, nc.vector.tensor_copy)
-                    regroup_p(part, 1, nc.scalar.copy)
-                if part > 0:
-                    quantise_p(part - 1)
+                regroup_p(part, 0, nc.vector.tensor_copy)
+                regroup_p(part, 1, nc.scalar.copy)
+                if part == 2:
+                    quantise_p(0)
+            quantise_p(2)
             last_turn = -1
 
-            bias_by_s = const.tile([P, H, SWEEPS, 2 * B], F32)
+            bias_by_s = const.tile([P, H, CHUNKS], F32)
             out_b_column = const.tile([P, E // P], F32)
 
             def turn_biases():
                 b_turned = psum_misc.tile([P, P], BF16, name="b_turned", tag="misc")
                 nc.tensor.transpose(out=b_turned[:], in_=b_rows[:], identity=identity_bf16[:])
-                turned = b_turned[:].rearrange("q (h c n e) -> q h c n e", h=H, c=2, n=2)
-                for sweep in range(SWEEPS):
-                    nc.vector.tensor_copy(
-                        out=bias_by_s[:, :, sweep, :].rearrange("q h (n b) -> q h n b", b=B),
-                        in_=turned[:, :, sweep // 2, :, sweep % 2].unsqueeze(3).to_broadcast([P, H, 2, B]),
-                    )
+                nc.vector.tensor_copy(out=bias_by_s[:].rearrange("q h i -> q (h i)"), in_=b_turned[:])
                 out_b_turned = psum_misc.tile([P, P], BF16, name="out_b_turned", tag="misc")
                 nc.tensor.transpose(out=out_b_turned[:], in_=out_b_rows[:], identity=identity_bf16[:])
                 nc.vector.tensor_copy(out=out_b_column[:], in_=out_b_turned[:, 0 : E // P])
@@ -766,8 +744,8 @@ def tile_mixerblock_pa_kernel(tc, p, mix_w, mix_b, decay, out_w, out_b, x, out):
                 for item in range(ITEMS):
                     if turn_at[item] + 1 == step:
                         add_x_and_store(item)
-                part = step + 6 if step < 2 else step + 3
-                if step < 2 or 5 <= step < 13:
+                part = step + 7 if step < 1 else step + 3
+                if step < 1 or 5 <= step < 13:
                     regroup_p(part, 0, nc.vector.tensor_copy)
                     regroup_p(part, 1, nc.scalar.copy)
                 transpose_m(step + 1, True)
@@ -775,7 +753,6 @@ def tile_mixerblock_pa_kernel(tc, p, mix_w, mix_b, decay, out_w, out_b, x, out):
                     for item in range(ITEMS):
                         if project_at[item] == step:
                             project(item)
-                keep_warm(step)
                 transpose_m(step + 1, False)
                 transpose_c(turn)
                 for item in range(ITEMS):
@@ -785,6 +762,7 @@ def tile_mixerblock_pa_kernel(tc, p, mix_w, mix_b, decay, out_w, out_b, x, out):
                 if step == -3:
                     for pair in range(2, PAIRS // 2):
                         spread_left(pair)
+                    load_left(0, PAIRS // 2, PAIRS)
                 if step == -1:
                     turn_biases()
                     load_out_w(1)
@@ -796,8 +774,8 @@ def tile_mixerblock_pa_kernel(tc, p, mix_w, mix_b, decay, out_w, out_b, x, out):
                     quantise_out_w(step // 2)
                     if step < 5:
                         load_out_w(2 + step // 2)
-                if -3 < step <= 2 or 5 < step <= 13:
-                    quantise_p(last_part)
+                if (-3 < step <= 1 or 5 < step <= 13) and last_part % 2 == 1:
+                    quantise_p(last_part - 1)
                 last_part = part
                 quantise_c(last_turn, slice(0, 2))
                 last_turn = turn if turn < SWEEPS * GROUPS - 1 else -1

@@ -40,7 +40,7 @@ VARIANT_COPIES = (
     (3, 0, 1, 0, 8), (12, 1, 0, 0, 4), (12, 1, 2, 0, 4), (16, 1, 0, 4, 8), (16, 1, 2, 4, 8), (17, 1, 1, 0, 8),
 )
 DRAIN_ON_VECTOR = ()
-ON_SCALAR = (((), ()), (((0, 3),), ((0, 3),)), (((0, 0),), ((0, 0),)), ((), ((0, 1),)))
+ON_SCALAR = (((), ()), ((), ((0, 3),)), (((0, 0),), ((0, 0),)), ((), ()))
 BIAS_ON_SCALAR = ((0, 1), (), (0, 1), (0, 1))
 
 FLOPS = 2 * B * H * HD * (K_PASS * N_TILE + T * N_TILE) + 2 * B * T * E * E
@@ -152,16 +152,13 @@ def tile_mixerblock_pa_kernel(tc, p, mix_w, mix_b, decay, out_w, out_b, x, out):
         def place_of(step):
             return step // PAIRS // 2, step // PAIRS % 2, step % PAIRS
 
-        def load_left(c, first, last, odds=(0, 1), ks=range(P // COPIES)):
-            copies = parked[c].rearrange("t v -> (t v)").rearrange("(h n r v) -> h n r v", n=COPIES, h=2, v=256)
-            for odd in odds:
-                for k in ks:
-                    nc.sync.dma_start(
-                        out=left_rows[k : P : P // COPIES, odd, first:last, :, 1 - c if odd else c, :].rearrange(
-                            "n r u v -> n (r u) v"
-                        ),
-                        in_=copies[odd][:, 2 * first : 2 * last, :],
-                    )
+        def load_left(k):
+            copies = parked.rearrange("(h n r v) -> h n r v", n=COPIES, h=2, v=256)
+            for odd in range(2):
+                nc.sync.dma_start(
+                    out=left_rows[k : P : P // COPIES, odd, :, :, 1 - odd, :].rearrange("n r u v -> n (r u) v"),
+                    in_=copies[odd],
+                )
 
         def make_m(step):
             if not 0 <= step < STEPS:
@@ -259,7 +256,7 @@ def tile_mixerblock_pa_kernel(tc, p, mix_w, mix_b, decay, out_w, out_b, x, out):
             for n in range(0, middle, 2) if first_part else range(middle, len(found), 2):
                 count = min(2, len(found) - n)
                 bank = psum_m.tile([P, 2, 2, P], F32, name="m_psum", tag="m_psum")
-                if n == middle:
+                if n == middle and step < 11:
                     keep_warm(bank[:].rearrange("q i u s -> q (i u s)"))
                 for i in range(count):
                     what, chunk, row, first = found[n + i]
@@ -555,15 +552,16 @@ def tile_mixerblock_pa_kernel(tc, p, mix_w, mix_b, decay, out_w, out_b, x, out):
             make_identity(nc, identity_f32[:])
             t_column = const.tile([P, PACK], F32)
             iota(t_column[:], [[1, PACK]], 0, PACK)
-            t_row = x_pool.tile([P, K_PASS], F32, name="t_row", tag="x_raw")
-            iota(t_row[0 : P // 2, :], [[2, 2], [P, BLOCKS], [PACK, HD // 2], [1, 2]], 0, 0)
-            iota(t_row[P // 2 : P, :], [[2, 2], [-P, BLOCKS], [PACK, HD // 2], [1, 2]], K_PASS - P, 0)
+            identity_bf16 = const.tile([P, P], BF16)
+            make_identity(nc, identity_bf16[:])
             s_index = const.tile([P, CHUNKS], F32)
             iota(s_index[:], [[P, CHUNKS]], 0, 1)
             t_in_block = const.tile([P, 2, HD], F32)
             iota(t_in_block[:].rearrange("q u (r e) -> q u r e", e=2), [[2, 2], [PACK, HD // 2], [1, 2]], 0, 0)
-            identity_bf16 = const.tile([P, P], BF16)
-            make_identity(nc, identity_bf16[:])
+            nc.gpsimd.memset(variants[:].rearrange("q v r n -> q (v r n)").bitcast(I32), 0)
+            t_row = x_pool.tile([P, K_PASS], F32, name="t_row", tag="x_raw")
+            iota(t_row[0 : P // 2, :], [[2, 2], [P, BLOCKS], [PACK, HD // 2], [1, 2]], K_PASS, 0)
+            iota(t_row[P // 2 : P, :], [[2, 2], [-P, BLOCKS], [PACK, HD // 2], [1, 2]], T - P, 0)
             spread = const.tile([P, 2, P], BF16)
             nc.gpsimd.memset(spread[:], 0.0)
             for odd in range(2):
@@ -576,15 +574,7 @@ def tile_mixerblock_pa_kernel(tc, p, mix_w, mix_b, decay, out_w, out_b, x, out):
                     out=own[:, :, 0 : PAIRS // 2],
                     in_=identity_bf16[:, ONES : ONES + 1].unsqueeze(2).to_broadcast([P, PAIRS, PAIRS // 2]),
                 )
-            nc.gpsimd.memset(variants[:].rearrange("q v r n -> q (v r n)").bitcast(I32), 0)
 
-            own_head = const.tile([P, 2, PAIRS], F32)
-            nc.vector.tensor_reduce(
-                out=own_head[:],
-                in_=identity_f32[:].rearrange("q (h n r) -> q h r n", h=2, r=PAIRS),
-                op=ALU.add,
-                axis=AX.X,
-            )
             reversed_identity = const.tile([P, P], F32)
             nc.vector.tensor_copy(
                 out=reversed_identity[:].rearrange("q (a r) -> q a r", a=BLOCKS),
@@ -596,18 +586,18 @@ def tile_mixerblock_pa_kernel(tc, p, mix_w, mix_b, decay, out_w, out_b, x, out):
             )
             log_d = const.tile([P, H], F32)
             nc.scalar.activation(out=log_d[:], in_=d_clipped[:], func=ACT.Ln)
-            left_columns = const.tile([P, PAIRS // 2, 2, PACK], F32)
+            left_columns = const.tile([P, PAIRS, 2, PACK], F32)
             nc.vector.tensor_tensor(
-                out=left_columns[:],
-                in0=t_column[:].unsqueeze(1).unsqueeze(1).to_broadcast([P, PAIRS // 2, 2, PACK]),
-                in1=log_d[:, 0:HALF_H].rearrange("q (r h) -> q r h", h=2).unsqueeze(3).to_broadcast([P, PAIRS // 2, 2, PACK]),
+                out=left_columns[:].rearrange("m r h k -> m (r h) k"),
+                in0=t_column[:].unsqueeze(1).to_broadcast([P, H, PACK]),
+                in1=log_d[:].unsqueeze(2).to_broadcast([P, H, PACK]),
                 op=ALU.mult,
             )
             nc.scalar.activation(out=left_columns[:], in_=left_columns[:], func=ACT.Exp, scale=-0.5)
 
             def spread_left(pair):
                 for odd in range(2):
-                    bank = psum_m.tile([P, PACK, P], F32, name="left_spread", tag="m_psum")
+                    bank = psum_misc.tile([P, PACK, P], F32, name="left_spread", tag="misc")
                     for k in range(PACK):
                         nc.tensor.transpose(
                             out=bank[:, k, :],
@@ -618,56 +608,6 @@ def tile_mixerblock_pa_kernel(tc, p, mix_w, mix_b, decay, out_w, out_b, x, out):
                         out=left_rows[:, odd, pair, :, odd, :].rearrange("p u (m e) -> p u m e", e=2),
                         in_=bank[:].rearrange("p (u e) m -> p u m e", u=2),
                     )
-
-            own_logs = const.tile([P, 2, PAIRS], F32)
-            nc.vector.tensor_tensor(
-                out=own_logs[:],
-                in0=log_d[:].rearrange("q (r h) -> q h r", h=2),
-                in1=own_head[:],
-                op=ALU.mult,
-            )
-            own_log = const.tile([P, 1], F32)
-            nc.vector.tensor_reduce(out=own_log[:], in_=own_logs[:], op=ALU.add, axis=AX.XY)
-            own_rate = const.tile([P, 2], F32)
-            for k in range(2):
-                nc.vector.tensor_scalar(
-                    out=own_rate[:, k : k + 1],
-                    in0=own_log[:],
-                    scalar1=-0.5 * K_PASS**k,
-                    scalar2=None,
-                    op0=ALU.mult,
-                )
-
-            left_parts = [x_pool.tile([P, K_PASS], F32, name="left_parts", tag="x_raw") for c in range(2)]
-            parked = [out[B - 1, T // 2 + 256 * c : T // 2 + 256 * (c + 1), :] for c in range(2)]
-            nc.scalar.activation(out=left_parts[0][:], in_=t_row[:], func=ACT.Exp, scale=own_rate[:, 0:1])
-            nc.scalar.activation(
-                out=left_parts[1][:], in_=t_row[:], func=ACT.Exp, scale=own_rate[:, 0:1], bias=own_rate[:, 1:2]
-            )
-
-            def prepare_left(c):
-                own_w = psum_misc.tile([P, K_PASS], F32, name="own_w", tag="misc")
-                weights = mix_w_rows[:, c * K_PASS : (c + 1) * K_PASS]
-                nc.tensor.matmul(
-                    out=own_w[:].rearrange("q (u n e) -> q u n e", u=2, e=2),
-                    lhsT=spread[:, 0, :],
-                    rhs=weights.rearrange("k (n u e) -> k u n e", u=2, e=2),
-                    start=True,
-                    stop=False,
-                )
-                for a in range(BLOCKS):
-                    nc.tensor.matmul(
-                        out=own_w[:].rearrange("q (u a r e) -> q a u r e", u=2, a=BLOCKS, e=2)[:, BLOCKS - 1 - a],
-                        lhsT=spread[:, 1, :],
-                        rhs=weights.rearrange("k (a r u e) -> k a u r e", a=BLOCKS, u=2, e=2)[:, a],
-                        start=False,
-                        stop=(a == BLOCKS - 1),
-                    )
-                nc.vector.tensor_tensor(out=left_parts[c][:], in0=own_w[:], in1=left_parts[c][:], op=ALU.mult)
-                copies = parked[c].rearrange("t v -> (t v)").rearrange("(h n q v) -> h n q v", h=2, q=HD, v=K_PASS)
-                for n in range(COPIES * PAIRS // HD):
-                    for odd in range(2):
-                        nc.sync.dma_start(out=copies[odd, n], in_=left_parts[c][odd * HD : (odd + 1) * HD, :])
 
             nc.sync.dma_start(out=b_rows[:], in_=mix_b.rearrange("h (a q) -> (h a) q", q=P))
             nc.sync.dma_start(out=out_b_rows[0 : E // P, :], in_=out_b.rearrange("(i q) -> i q", q=P))
@@ -691,6 +631,11 @@ def tile_mixerblock_pa_kernel(tc, p, mix_w, mix_b, decay, out_w, out_b, x, out):
                 op0=ALU.is_le,
             )
 
+            w_columns = psum_mix.tile([P, PACK, P], BF16, name="w_columns", tag="mixed")
+            for k in range(PACK):
+                nc.tensor.transpose(
+                    out=w_columns[:, k, :], in_=mix_w_rows[:, k:K_PASS:PACK], identity=identity_bf16[:]
+                )
             for pair in range(2):
                 spread_left(pair)
             w_turned = psum_misc.tile([P, H, CHUNKS], BF16, name="w_turned", tag="misc")
@@ -701,7 +646,61 @@ def tile_mixerblock_pa_kernel(tc, p, mix_w, mix_b, decay, out_w, out_b, x, out):
             nc.vector.tensor_tensor(
                 out=right[:, 0:HALF_H, :], in0=right[:, 0:HALF_H, :], in1=w_turned[:, 0:HALF_H, :], op=ALU.mult
             )
-            prepare_left(0)
+            late_columns = left_columns[:, PAIRS // 2 : PAIRS, :, :]
+            nc.vector.tensor_tensor(
+                out=late_columns,
+                in0=late_columns,
+                in1=w_columns[:, :, HALF_H:H].rearrange("m k (r h) -> m r h k", h=2),
+                op=ALU.mult,
+            )
+            parked = out[B - 1, T // 2 : T // 2 + 256, :].rearrange("t v -> (t v)")
+
+            def decay_left():
+                own_head = const.tile([P, 2, PAIRS], F32)
+                nc.vector.tensor_reduce(
+                    out=own_head[:],
+                    in_=identity_f32[:].rearrange("q (h n r) -> q h r n", h=2, r=PAIRS),
+                    op=ALU.add,
+                    axis=AX.X,
+                )
+                own_logs = const.tile([P, 2, PAIRS], F32)
+                nc.vector.tensor_tensor(
+                    out=own_logs[:],
+                    in0=log_d[:].rearrange("q (r h) -> q h r", h=2),
+                    in1=own_head[:],
+                    op=ALU.mult,
+                )
+                own_log = const.tile([P, 1], F32)
+                nc.vector.tensor_reduce(out=own_log[:], in_=own_logs[:], op=ALU.add, axis=AX.XY)
+                own_rate = const.tile([P, 1], F32)
+                nc.vector.tensor_scalar(out=own_rate[:], in0=own_log[:], scalar1=-0.5, scalar2=None, op0=ALU.mult)
+                nc.scalar.activation(out=t_row[:], in_=t_row[:], func=ACT.Exp, scale=own_rate[:, 0:1])
+
+            def prepare_left():
+                own_w = psum_misc.tile([P, K_PASS], F32, name="own_w", tag="misc")
+                weights = mix_w_rows[:, K_PASS:T]
+                nc.tensor.matmul(
+                    out=own_w[:].rearrange("q (u n e) -> q u n e", u=2, e=2),
+                    lhsT=spread[:, 0, :],
+                    rhs=weights.rearrange("k (n u e) -> k u n e", u=2, e=2),
+                    start=True,
+                    stop=False,
+                )
+                for a in range(BLOCKS):
+                    nc.tensor.matmul(
+                        out=own_w[:].rearrange("q (u a r e) -> q a u r e", u=2, a=BLOCKS, e=2)[:, BLOCKS - 1 - a],
+                        lhsT=spread[:, 1, :],
+                        rhs=weights.rearrange("k (a r u e) -> k a u r e", a=BLOCKS, u=2, e=2)[:, a],
+                        start=False,
+                        stop=(a == BLOCKS - 1),
+                    )
+                left_parts = x_pool.tile([P, K_PASS], F32, name="left_parts", tag="x_raw")
+                nc.vector.tensor_tensor(out=left_parts[:], in0=own_w[:], in1=t_row[:], op=ALU.mult)
+                copies = parked.rearrange("(h n q v) -> h n q v", h=2, q=HD, v=K_PASS)
+                for n in range(COPIES * PAIRS // HD):
+                    for odd in range(2):
+                        nc.sync.dma_start(out=copies[odd, n], in_=left_parts[odd * HD : (odd + 1) * HD, :])
+
             for part in range(4):
                 regroup_p(part, 0, nc.vector.tensor_copy)
                 regroup_p(part, 1, nc.scalar.copy)
@@ -726,7 +725,7 @@ def tile_mixerblock_pa_kernel(tc, p, mix_w, mix_b, decay, out_w, out_b, x, out):
             for step in range(-3, STEPS + 8):
                 turn = (step - 5) // 4 if step % 4 == 1 else -1
                 if step in range(5, 9):
-                    load_left(1, 0, PAIRS, ks=(step - 5,))
+                    load_left(step - 5)
                 if step == 2:
                     load_p(1)
                 for item in range(ITEMS):
@@ -736,8 +735,9 @@ def tile_mixerblock_pa_kernel(tc, p, mix_w, mix_b, decay, out_w, out_b, x, out):
                     nc.sync.dma_start(out=out_b_everywhere(), in_=out_b.partition_broadcast(P))
                 if 26 <= step < 30:
                     load_last_x(2 * (step - 26))
-                make_m(step + 3)
+                quantise_m(step)
                 mask_m(step + 2)
+                make_m(step + 3)
                 for item in range(ITEMS):
                     if project_at[item] + 1 == step:
                         add_out_b(item)
@@ -758,18 +758,18 @@ def tile_mixerblock_pa_kernel(tc, p, mix_w, mix_b, decay, out_w, out_b, x, out):
                 for item in range(ITEMS):
                     if turn_at[item] == step:
                         turn_back(item)
-                quantise_m(step)
-                if step == -3:
-                    for pair in range(2, PAIRS // 2):
-                        spread_left(pair)
-                    load_left(0, PAIRS // 2, PAIRS)
-                if step == -1:
+                if step + 5 in range(2, PAIRS):
+                    spread_left(step + 5)
+                if step == 0:
                     turn_biases()
+                if step == 1:
+                    decay_left()
+                if step == -1:
                     load_out_w(1)
                 if step == 3:
-                    prepare_left(1)
+                    prepare_left()
                 if step in (0, 2, 4, 6):
-                    regroup_out_w(step // 2, nc.scalar.copy if step < 4 else nc.vector.tensor_copy)
+                    regroup_out_w(step // 2, nc.vector.tensor_copy)
                 if step in (1, 3, 5, 7):
                     quantise_out_w(step // 2)
                     if step < 5:

@@ -40,7 +40,7 @@ VARIANT_COPIES = (
     (3, 0, 1, 0, 8), (12, 1, 0, 0, 4), (12, 1, 2, 0, 4), (16, 1, 0, 4, 8), (16, 1, 2, 4, 8), (17, 1, 1, 0, 8),
 )
 DRAIN_ON_VECTOR = ()
-ON_SCALAR = (((), ()), ((), ((0, 3),)), (((0, 0),), ((0, 0),)), ((), ()))
+ON_SCALAR = (((), ()), ((), ((0, 3),)), (((0, 0),), ((0, 0),)), ((), ((0, 1),)))
 BIAS_ON_SCALAR = ((0, 1), (), (0, 1), (0, 1))
 
 FLOPS = 2 * B * H * HD * (K_PASS * N_TILE + T * N_TILE) + 2 * B * T * E * E
@@ -701,14 +701,6 @@ def tile_mixerblock_pa_kernel(tc, p, mix_w, mix_b, decay, out_w, out_b, x, out):
                     for odd in range(2):
                         nc.sync.dma_start(out=copies[odd, n], in_=left_parts[odd * HD : (odd + 1) * HD, :])
 
-            for part in range(4):
-                regroup_p(part, 0, nc.vector.tensor_copy)
-                regroup_p(part, 1, nc.scalar.copy)
-                if part == 2:
-                    quantise_p(0)
-            quantise_p(2)
-            last_turn = -1
-
             bias_by_s = const.tile([P, H, CHUNKS], F32)
             out_b_column = const.tile([P, E // P], F32)
 
@@ -720,13 +712,22 @@ def tile_mixerblock_pa_kernel(tc, p, mix_w, mix_b, decay, out_w, out_b, x, out):
                 nc.tensor.transpose(out=out_b_turned[:], in_=out_b_rows[:], identity=identity_bf16[:])
                 nc.vector.tensor_copy(out=out_b_column[:], in_=out_b_turned[:, 0 : E // P])
 
+            for part in range(4):
+                regroup_p(part, 0, nc.vector.tensor_copy)
+                regroup_p(part, 1, nc.scalar.copy)
+                if part == 2:
+                    quantise_p(0)
+                    turn_biases()
+            quantise_p(2)
+            last_turn = -1
+
             project_at = [min(item, 20) + 11 + (item > 20) + (item > 22) for item in range(ITEMS)]
             turn_at = [item + 16 if item < 17 else (31 + (item - 14) // 2 + (item > 19)) for item in range(ITEMS)]
             for step in range(-3, STEPS + 8):
                 turn = (step - 5) // 4 if step % 4 == 1 else -1
                 if step in range(5, 9):
                     load_left(step - 5)
-                if step == 2:
+                if step == 1:
                     load_p(1)
                 for item in range(ITEMS):
                     if turn_at[item] == step + 2:
@@ -744,8 +745,8 @@ def tile_mixerblock_pa_kernel(tc, p, mix_w, mix_b, decay, out_w, out_b, x, out):
                 for item in range(ITEMS):
                     if turn_at[item] + 1 == step:
                         add_x_and_store(item)
-                part = step + 7 if step < 1 else step + 3
-                if step < 1 or 5 <= step < 13:
+                part = step + 7 if step < 1 else step + 4
+                if step < 1 or 4 <= step < 12:
                     regroup_p(part, 0, nc.vector.tensor_copy)
                     regroup_p(part, 1, nc.scalar.copy)
                 transpose_m(step + 1, True)
@@ -760,8 +761,6 @@ def tile_mixerblock_pa_kernel(tc, p, mix_w, mix_b, decay, out_w, out_b, x, out):
                         turn_back(item)
                 if step + 5 in range(2, PAIRS):
                     spread_left(step + 5)
-                if step == 0:
-                    turn_biases()
                 if step == 1:
                     decay_left()
                 if step == -1:
@@ -769,12 +768,12 @@ def tile_mixerblock_pa_kernel(tc, p, mix_w, mix_b, decay, out_w, out_b, x, out):
                 if step == 3:
                     prepare_left()
                 if step in (0, 2, 4, 6):
-                    regroup_out_w(step // 2, nc.vector.tensor_copy)
+                    regroup_out_w(step // 2, nc.scalar.copy if step == 6 else nc.vector.tensor_copy)
                 if step in (1, 3, 5, 7):
                     quantise_out_w(step // 2)
                     if step < 5:
                         load_out_w(2 + step // 2)
-                if (-3 < step <= 1 or 5 < step <= 13) and last_part % 2 == 1:
+                if (-3 < step <= 1 or 4 < step <= 12) and last_part % 2 == 1:
                     quantise_p(last_part - 1)
                 last_part = part
                 quantise_c(last_turn, slice(0, 2))

from contextlib import ExitStack

import concourse.mybir as mybir
from concourse.masks import make_identity

F32 = mybir.dt.float32
BF16 = mybir.dt.bfloat16
I32 = mybir.dt.int32
U32 = mybir.dt.uint32
U8 = mybir.dt.uint8
FP8X4 = mybir.dt.float8_e4m3fn_x4
ALU = mybir.AluOpType
ACT = mybir.ActivationFunctionType
AX = mybir.AxisListType

P = 128
PACK = 4
K_PASS = P * PACK
B, H, T, HD = 2, 16, 1024, 64
E = H * HD
HALF_H = H // 2
CHUNKS = T // P
PAIRS = H // 2
N_TILE = 512
BLOCKS = K_PASS // P
SWEEPS = 4
STEPS = SWEEPS * PAIRS
GROUPS = E // K_PASS
GROUP_PAIRS = PAIRS // GROUPS
ITEMS = (SWEEPS - 1) * (E // P)
LAST_ITEMS = E // P
COPIES = 32
MAX_BLOCKS = 7
ONES = 32
ROW_WIDTH = ((256, 512), (768, 1024))
M_ROWS = 4672
VARIANT_COPIES = (
    (-3, 0, 0, 0, 2), (-3, 0, 2, 0, 2), (-2, 0, 0, 2, 4), (-2, 0, 2, 2, 4),
    (0, 0, 0, 4, 6), (0, 0, 2, 4, 6), (2, 0, 0, 6, 8), (2, 0, 2, 6, 8),
    (3, 0, 1, 0, 8), (12, 1, 0, 0, 4), (12, 1, 2, 0, 4), (16, 1, 0, 4, 8), (16, 1, 2, 4, 8), (17, 1, 1, 0, 8),
)
DRAIN_ON_VECTOR = ()
ON_SCALAR = (((), ()), ((), ((0, 3),)), (((0, 0),), ((0, 0),)), ((), ((0, 1),)))
BIAS_ON_SCALAR = ((0, 1), (), (0, 1), (0, 1))

FLOPS = 2 * B * H * HD * (K_PASS * N_TILE + T * N_TILE) + 2 * B * T * E * E


def tile_mixerblock_pa_kernel(tc, p, mix_w, mix_b, decay, out_w, out_b, x, out):
    nc = tc.nc
    with ExitStack() as stack:
        def pool(name, bufs):
            return stack.enter_context(tc.tile_pool(name=name, bufs=bufs))

        const = pool("const", 1)
        big_pool = pool("big", 2)
        p_grouped_pool = pool("p_grouped", 2)
        quarter_pool = pool("quarter", 4)
        rows_pool = pool("m_rows", 3)
        grouped_pool = pool("m_grouped", 2)
        m_pool = pool("m_words", 2)
        c_pool = pool("c_rows", 2)
        c_words_pool = pool("c_words", 2)
        x_pool = pool("x_stage", 4)
        psum_m = stack.enter_context(tc.psum_pool(name="psum_m", bufs=3))
        psum_mix = stack.enter_context(tc.psum_pool(name="psum_mix", bufs=2))
        psum_misc = stack.enter_context(tc.psum_pool(name="psum_misc", bufs=3))

        p_raw, p_grouped, w_raw, w_grouped, m_rows, c_words, c_scales = {}, {}, {}, {}, {}, {}, {}
        m_grouped, m_words, m_scales, mixed, c_rows, c_grouped = {}, {}, {}, {}, {}, {}
        projected, y_turned, turned_back, x_raw, y, last_y = {}, {}, {}, {}, {}, {}

        p_words = const.tile([P, 2 * PAIRS, 2 * B * HD], U32, align_bytes=64)
        p_scales = const.tile([P, 2 * PAIRS, 2 * B * HD], U8, align_bytes=64)
        w_words = const.tile([P, GROUPS, E], U32, align_bytes=64)
        w_scales = const.tile([P, GROUPS, E], U8, align_bytes=64)
        left_rows = const.tile([P, 2, PAIRS, 2, 2, 256], F32)
        variants = const.tile([P, 3, PAIRS, 2 * B * HD], U32, align_bytes=64)

        def load_p(c):
            for odd in range(2):
                p_raw[(c, odd)] = big_pool.tile([P, B * PAIRS, PACK * HD], BF16, name="p_raw", tag="big", align_bytes=64)
            steps = slice(c * K_PASS, (c + 1) * K_PASS)
            heads = p.rearrange("b (r h) t f -> h (b r) t f", h=2)
            nc.sync.dma_start(
                out=p_raw[(c, 0)][:], in_=heads[0][:, steps, :].rearrange("n (q j) f -> q n (j f)", j=PACK)
            )
            source = heads[1][:, steps, :].rearrange("n (a r j) f -> a r n (j f)", a=BLOCKS, j=PACK)
            for a in range(BLOCKS):
                rows = slice(32 * (3 - a), 32 * (4 - a))
                nc.sync.dma_start(out=p_raw[(c, 1)][rows, :, :], in_=source[a])

        def regroup_p(part, odd, engine_copy):
            c, pair = divmod(part, PAIRS)
            if odd == 0 and part % 2 == 0:
                p_grouped[part // 2] = p_grouped_pool.tile(
                    [P, 2, 2, B, HD, PACK], BF16, name="p_grouped", tag="p_grouped", align_bytes=64
                )
            engine_copy(
                out=p_grouped[part // 2][:, part % 2, odd, :, :, :],
                in_=p_raw[(c, odd)][:]
                .rearrange("q (b r) v -> q b r v", b=B)[:, :, pair, :]
                .rearrange("q b (j f) -> q b f j", j=PACK),
            )

        def quantise_p(part):
            nc.vector.quantize_mx(
                out=p_words[:, part : part + 2, :].rearrange("q r n -> q (r n)").bitcast(FP8X4),
                scales=p_scales[:, part : part + 2, :].rearrange("q r n -> q (r n)"),
                in_=p_grouped[part // 2][:].rearrange("q r h b f j -> q (r h b f j)"),
            )

        def p_cols(odd):
            return slice(odd * B * HD, (odd + 1) * B * HD)

        def copy_variants(c, v, pairs):
            for odd in range(2):
                rows = slice(32 * (v + 1), P) if odd else slice(0, 32 * (v + 1))
                nc.sync.dma_start(
                    out=variants[rows, v, pairs, p_cols(odd)].bitcast(I32),
                    in_=p_words[rows, c * PAIRS + pairs.start : c * PAIRS + pairs.stop, p_cols(odd)].bitcast(I32),
                )

        def load_out_w(piece):
            g, n_half = divmod(piece, 2)
            w_raw[piece] = quarter_pool.tile([P, PACK, N_TILE], BF16, name="w_raw", tag="quarter", align_bytes=64)
            nc.sync.dma_start(
                out=w_raw[piece][:],
                in_=out_w[g * K_PASS : (g + 1) * K_PASS, n_half * N_TILE : (n_half + 1) * N_TILE].rearrange(
                    "(q j) n -> q j n", j=PACK
                ),
            )

        def regroup_out_w(piece, engine_copy):
            w_grouped[piece] = quarter_pool.tile(
                [P, N_TILE, PACK], BF16, name="w_grouped", tag="quarter", align_bytes=64
            )
            engine_copy(
                out=w_grouped[piece][:].rearrange("q (c i) j -> q c j i", i=4),
                in_=w_raw[piece][:].rearrange("q j (c i) -> q c j i", i=4),
            )

        def quantise_out_w(piece):
            g, n_half = divmod(piece, 2)
            cols = slice(n_half * N_TILE, (n_half + 1) * N_TILE)
            nc.vector.quantize_mx(
                out=w_words[:, g, cols].bitcast(FP8X4),
                scales=w_scales[:, g, cols],
                in_=w_grouped[piece][:].rearrange("q n j -> q (n j)"),
            )

        def place_of(step):
            return step // PAIRS // 2, step // PAIRS % 2, step % PAIRS

        def load_left(k):
            copies = parked.rearrange("(h n r v) -> h n r v", n=COPIES, h=2, v=256)
            for odd in range(2):
                nc.sync.dma_start(
                    out=left_rows[k : P : P // COPIES, odd, :, :, 1 - odd, :].rearrange("n r u v -> n (r u) v"),
                    in_=copies[odd],
                )

        def make_m(step):
            if not 0 <= step < STEPS:
                return
            c, half, pair = place_of(step)
            tile = rows_pool.tile([P, M_ROWS], BF16, name="m_rows", tag="m_rows", align_bytes=64)
            m_rows[step] = tile
            width = ROW_WIDTH[c][half]

            def part(row, first, last):
                base = row // 2 * 2 * width
                return tile[:, base : base + 2 * width].rearrange("p (u v) -> p u v", u=2)[:, :, first:last]

            def scale_left(odd, chunk, dst, first, last):
                h = 2 * pair + odd
                i = c * BLOCKS + chunk
                src = left_rows[:, odd, pair, :, :, :].rearrange("p u c v -> p u (c v)")[:, :, first:last]
                scale = right[:, h, i : i + 1]
                if (odd, chunk) in ON_SCALAR[step // PAIRS][pair // GROUP_PAIRS]:
                    nc.scalar.activation(out=dst, in_=src, func=ACT.Copy, scale=scale)
                else:
                    nc.vector.tensor_scalar(out=dst, in0=src, scalar1=scale, scalar2=None, op0=ALU.mult)

            for row in (half, half + 2):
                edge = HD * (row + 1)
                if c == 0 and row < 3:
                    scale_left(0, row, part(row, 0, edge), 0, edge)
                    scale_left(1, 2 - row, part(row, edge, 256), 256 + edge, 512)
                elif c == 0:
                    scale_left(0, 3, part(3, 0, 256), 0, 256)
                    scale_left(1, 3, part(3, 256, 512), 256, 512)
                elif row < 3:
                    scale_left(0, row, part(row, 0, 256 + edge), 0, 256 + edge)
                    scale_left(1, 2 - row, part(row, 256 + edge, 768), edge, 512)
                else:
                    scale_left(0, 3, part(3, 0, 512), 0, 512)
                    scale_left(1, 3, part(3, 512, 1024), 0, 512)

        def mask_m(step):
            if not 0 <= step < STEPS:
                return
            c, half, pair = place_of(step)
            width = ROW_WIDTH[c][half]
            first = 256 * c + half * HD
            pieces = (
                m_rows[step][:, first : first + 2 * (2 * width + 2 * HD)]
                .rearrange("p (r v) -> p r v", r=2)[:, :, 0 : 2 * width]
                .rearrange("p r (u v) -> p r u v", u=2)[:, :, :, 0 : 2 * HD]
            )
            nc.vector.tensor_tensor(
                out=pieces,
                in0=pieces,
                in1=triangles[:].unsqueeze(1).to_broadcast([P, 2, 2, 2 * HD]),
                op=ALU.mult,
            )

        def block_list(c, half):
            rows = (half,) if half else (0, 2)
            found = []
            for row in rows:
                if c == 1:
                    found.append(("A full", row, row, 0))
                found.append(("X", row, row, 256 * c))
                if c == 1:
                    found.append(("B full", 2 - row, row, 512))
            if half:
                names = ("A full", "A", "B", "B full") if c == 1 else ("A", "B")
                found += [(name, 3, 3, 256 * n) for n, name in enumerate(names)]
            return found

        def keep_warm(bank):
            nc.tensor.matmul_mx(
                out=bank,
                lhsT=p_words[:, 0, 0:P].bitcast(FP8X4),
                lhsT_scale=p_scales[:, 0, 0:P],
                rhs=p_words[:, 0:2, :].rearrange("q r n -> q (r n)").bitcast(FP8X4),
                rhs_scale=p_scales[:, 0:2, :].rearrange("q r n -> q (r n)"),
                start=True,
                stop=True,
            )

        def transpose_m(step, first_part):
            if not 0 <= step < STEPS:
                return
            c, half, pair = place_of(step)
            width = ROW_WIDTH[c][half]
            found = block_list(c, half)
            words = m_rows[step][:].bitcast(F32)
            if first_part:
                m_grouped[step] = grouped_pool.tile(
                    [P, MAX_BLOCKS * P, PACK], BF16, name="m_grouped", align_bytes=64
                )
            out_words = m_grouped[step][:].rearrange("q s j -> q (s j)").bitcast(F32)
            middle = (len(found) + 1) // 4 * 2
            for n in range(0, middle, 2) if first_part else range(middle, len(found), 2):
                count = min(2, len(found) - n)
                bank = psum_m.tile([P, 2, 2, P], F32, name="m_psum", tag="m_psum")
                if n == middle and step < 11:
                    keep_warm(bank[:].rearrange("q i u s -> q (i u s)"))
                for i in range(count):
                    what, chunk, row, first = found[n + i]
                    for u in range(2):
                        start = (row // 2 * 2 * width + u * width + first) // 2
                        nc.tensor.transpose(
                            out=bank[:, i, u, :], in_=words[:, start : start + P], identity=identity_f32[:]
                        )
                drain = nc.vector.tensor_copy if (c, half, n) in DRAIN_ON_VECTOR else nc.scalar.copy
                drain(
                    out=out_words[:, 256 * n : 256 * (n + count)].rearrange(
                        "q (i s u) -> q i s u", i=count, u=2
                    ),
                    in_=bank[:, 0:count, :, :].rearrange("q i u s -> q i s u"),
                )

        def quantise_m(step):
            if not 0 <= step < STEPS:
                return
            c, half, pair = place_of(step)
            found = block_list(c, half)
            m_words[step] = m_pool.tile([P, MAX_BLOCKS * P], U32, name="m_words", align_bytes=64)
            m_scales[step] = m_pool.tile([P, MAX_BLOCKS * P], U8, name="m_scales", align_bytes=64)
            source = m_grouped[step][:].rearrange("q s j -> q (s j)")
            first = 0
            for count in (4, 2, 1):
                if len(found) & count:
                    cols = slice(first * P, (first + count) * P)
                    nc.vector.quantize_mx(
                        out=m_words[step][:, cols].bitcast(FP8X4),
                        scales=m_scales[step][:, cols],
                        in_=source[:, first * K_PASS : (first + count) * K_PASS],
                    )
                    first += count

        def multiply(step):
            if not 0 <= step < STEPS:
                return
            c, half, pair = place_of(step)
            slots = {(what, chunk): n for n, (what, chunk, row, first) in enumerate(block_list(c, half))}
            mixed[step] = psum_mix.tile([P, 2, 2, B * HD], F32, name="mixed", tag="mixed")
            keep_warm(mixed[step][:].rearrange("p h n v -> p (h n v)"))
            for odd in range(2):
                for n in range(2):
                    chunk = half + 2 * n
                    own = "AB"[odd]
                    here = c * PAIRS + pair
                    passes = []
                    if c > 0:
                        passes.append((slots[(own + " full", chunk)], p_words[:, pair, p_cols(odd)], pair))
                    if chunk == 3:
                        passes.append((slots[(own, 3)], p_words[:, here, p_cols(odd)], here))
                    else:
                        v = 2 - chunk if odd else chunk
                        passes.append((slots[("X", v)], variants[:, v, pair, p_cols(odd)], here))
                    for k, (slot, moving, part) in enumerate(passes):
                        cols = slice(slot * P, (slot + 1) * P)
                        nc.tensor.matmul_mx(
                            out=mixed[step][:, odd, n, :],
                            lhsT=m_words[step][:, cols].bitcast(FP8X4),
                            lhsT_scale=m_scales[step][:, cols],
                            rhs=moving.bitcast(FP8X4),
                            rhs_scale=p_scales[:, part, p_cols(odd)],
                            start=(k == 0),
                            stop=(k == len(passes) - 1),
                        )

        def add_bias(step):
            if not 0 <= step < STEPS:
                return
            c, half, pair = place_of(step)
            g, pair_in_group = divmod(pair, GROUP_PAIRS)
            where = (step // PAIRS, g)
            if pair_in_group == 0:
                c_rows[where] = c_pool.tile([P, 2, B, K_PASS], BF16, name="c_rows")
            first = 2 * HD * pair_in_group
            chunk = c * BLOCKS + half
            on_scalar = BIAS_ON_SCALAR[step // PAIRS]
            for odd in on_scalar:
                for n in range(2):
                    nc.scalar.activation(
                        out=c_rows[where][:, n, :, first + odd * HD : first + (odd + 1) * HD],
                        in_=mixed[step][:, odd, n, :].rearrange("p (b f) -> p b f", b=B),
                        func=ACT.Identity,
                        bias=bias_by_s[:, 2 * pair + odd, chunk + 2 * n : chunk + 2 * n + 1],
                    )
            for odd in range(2):
                if odd not in on_scalar:
                    nc.vector.tensor_tensor(
                        out=c_rows[where][:, :, :, first + odd * HD : first + (odd + 1) * HD],
                        in0=mixed[step][:, odd, :, :].rearrange("p n (b f) -> p n b f", b=B),
                        in1=bias_by_s[:, 2 * pair + odd, chunk : chunk + 3 : 2]
                        .unsqueeze(2)
                        .unsqueeze(3)
                        .to_broadcast([P, 2, B, HD]),
                        op=ALU.add,
                    )

        def transpose_c(turn):
            if not 0 <= turn < SWEEPS * GROUPS:
                return
            rows = c_rows[divmod(turn, GROUPS)]
            c_grouped[turn] = quarter_pool.tile(
                [P, N_TILE, PACK], BF16, name="c_grouped", tag="quarter", align_bytes=64
            )
            out_words = c_grouped[turn][:].rearrange("q s j -> q (s j)").bitcast(F32)
            for b in range(B):
                turned = psum_m.tile([P, 2, 2, P], F32, name="c_turned", tag="m_psum")
                for n in range(2):
                    words = rows[:, n, b, :].bitcast(F32)
                    for u in range(2):
                        nc.tensor.transpose(
                            out=turned[:, n, u, :], in_=words[:, u : 2 * P : 2], identity=identity_f32[:]
                        )
                (nc.scalar.copy if b == 0 or turn < SWEEPS * GROUPS - 1 else nc.vector.tensor_copy)(
                    out=out_words[:, b * N_TILE : (b + 1) * N_TILE].rearrange("q (n s u) -> q n s u", n=2, u=2),
                    in_=turned[:].rearrange("q n u s -> q n s u"),
                )

        def quantise_c(turn, batches):
            if not 0 <= turn < SWEEPS * GROUPS:
                return
            sweep, g = divmod(turn, GROUPS)
            if g == 0:
                c_words[sweep] = c_words_pool.tile([P, GROUPS, N_TILE], U32, name="c_words", align_bytes=64)
                c_scales[sweep] = c_words_pool.tile([P, GROUPS, N_TILE], U8, name="c_scales", align_bytes=64)
            cols = slice(batches.start * 2 * P, batches.stop * 2 * P)
            nc.vector.quantize_mx(
                out=c_words[sweep][:, g, cols].bitcast(FP8X4),
                scales=c_scales[sweep][:, g, cols],
                in_=c_grouped[turn][:, cols, :].rearrange("q s j -> q (s j)"),
            )

        def project(item):
            if not 0 <= item < ITEMS:
                return
            sweep, n_block = divmod(item, E // P)
            cols = slice(n_block * P, (n_block + 1) * P)
            bank, tag = (psum_misc, "misc") if item < 21 else (psum_mix, "mixed") if item < 23 else (psum_m, "m_psum")
            projected[item] = bank.tile([P, N_TILE], F32, name="projected", tag=tag)
            for g in range(GROUPS):
                nc.tensor.matmul_mx(
                    out=projected[item][:],
                    lhsT=w_words[:, g, cols].bitcast(FP8X4),
                    lhsT_scale=w_scales[:, g, cols],
                    rhs=c_words[sweep][:, g, :].bitcast(FP8X4),
                    rhs_scale=c_scales[sweep][:, g, :],
                    start=(g == 0),
                    stop=(g == GROUPS - 1),
                )

        def add_out_b(item):
            if not 0 <= item < ITEMS:
                return
            patch, i = divmod(item, 4)
            if i == 0:
                y_turned[patch] = big_pool.tile([P, 4, N_TILE], F32, name="y_turned", tag="big", align_bytes=64)
            n_block = item % (E // P)
            nc.scalar.activation(
                out=y_turned[patch][:, i, :],
                in_=projected[item][:],
                func=ACT.Identity,
                bias=out_b_column[:, n_block : n_block + 1],
            )

        def rows_and_cols(item):
            patch, i = divmod(item, 4)
            sweep, n_half = divmod(patch, 2)
            b, n = divmod(i, 2)
            chunk = sweep // 2 * BLOCKS + sweep % 2 + 2 * n
            return b, slice(chunk * P, (chunk + 1) * P), slice(n_half * N_TILE, (n_half + 1) * N_TILE)

        def load_x(item):
            if not 0 <= item < ITEMS or item % 2:
                return
            b, rows, cols = rows_and_cols(item)
            x_raw[item] = x_pool.tile([P, 2, N_TILE], BF16, name="x_raw", tag="x_raw")
            nc.sync.dma_start(
                out=x_raw[item][:],
                in_=x[b, rows.start : rows.start + 3 * P, cols].rearrange("(n s) v -> s n v", s=P)[:, 0:3:2, :],
            )

        def turn_back(item):
            if not 0 <= item < ITEMS:
                return
            patch, block = divmod(item, 4)
            turned_back[item] = psum_misc.tile([P, N_TILE], F32, name="turned_back", tag="misc")
            for i in range(4):
                nc.tensor.transpose(
                    out=turned_back[item][:, i * P : (i + 1) * P],
                    in_=y_turned[patch][:, i, block * P : (block + 1) * P],
                    identity=identity_f32[:],
                )

        def add_x_and_store(item):
            if not 0 <= item < ITEMS:
                return
            b, rows, cols = rows_and_cols(item - item % 2)
            if item % 2 == 0:
                y[item] = quarter_pool.tile([P, 2, N_TILE], F32, name="y", tag="quarter", align_bytes=64)
            both = y[item - item % 2]
            nc.vector.tensor_tensor(
                out=both[:, item % 2, :], in0=turned_back[item][:], in1=x_raw[item - item % 2][:, item % 2, :], op=ALU.add
            )
            if item % 2:
                nc.sync.dma_start(
                    out=out[b, rows.start : rows.start + 3 * P, cols].rearrange("(n s) v -> s n v", s=P)[:, 0:3:2, :],
                    in_=both[:],
                )

        def last_rows_and_cols(k):
            b, n_half, n = k // 4, k // 2 % 2, k % 2
            chunk = BLOCKS + 1 + 2 * n
            return b, slice(chunk * P, (chunk + 1) * P), slice(n_half * N_TILE, (n_half + 1) * N_TILE)

        def load_last_x(k):
            b, rows, cols = last_rows_and_cols(k)
            x_raw[ITEMS + k] = x_pool.tile([P, 2, N_TILE], BF16, name="x_raw", tag="x_raw")
            nc.sync.dma_start(
                out=x_raw[ITEMS + k][:],
                in_=x[b, rows.start : rows.start + 3 * P, cols].rearrange("(n s) v -> s n v", s=P)[:, 0:3:2, :],
            )

        def residual(k):
            return left_rows[:, 0, k // 2, :, :, :].rearrange("p u c v -> p (u c v)").rearrange(
                "p (n v) -> p n v", n=2
            )

        def out_b_everywhere():
            return left_rows[:, 1, 0, 0, :, :].rearrange("p c v -> p (c v)").bitcast(BF16)

        def add_out_b_to_x(k):
            cols = last_rows_and_cols(k)[2]
            nc.vector.tensor_tensor(
                out=residual(k),
                in0=x_raw[ITEMS + k][:],
                in1=out_b_everywhere()[:, cols].unsqueeze(1).to_broadcast([P, 2, N_TILE]),
                op=ALU.add,
            )

        def project_last(k):
            b, rows, cols = last_rows_and_cols(k)
            first = (2 * b + k % 2) * P
            bank, tag = (psum_mix, "mixed") if k % 4 < 2 else (psum_m, "m_psum")
            projected[ITEMS + k] = bank.tile([P, N_TILE], F32, name="projected", tag=tag)
            for g in range(GROUPS):
                nc.tensor.matmul_mx(
                    out=projected[ITEMS + k][:],
                    lhsT=c_words[SWEEPS - 1][:, g, first : first + P].bitcast(FP8X4),
                    lhsT_scale=c_scales[SWEEPS - 1][:, g, first : first + P],
                    rhs=w_words[:, g, cols].bitcast(FP8X4),
                    rhs_scale=w_scales[:, g, cols],
                    start=(g == 0),
                    stop=(g == GROUPS - 1),
                )

        def finish_last(k):
            b, rows, cols = last_rows_and_cols(k)
            if k % 2 == 0:
                last_y[k] = quarter_pool.tile([P, 2, N_TILE], F32, name="last_y", tag="quarter", align_bytes=64)
            dst = last_y[k - k % 2][:, k % 2, :]
            nc.vector.tensor_tensor(out=dst, in0=projected[ITEMS + k][:], in1=residual(k)[:, k % 2, :], op=ALU.add)
            nc.sync.dma_start(out=out[b, rows, cols], in_=dst)

        with tc.manual_schedule():
            warm = const.tile([P, 1], F32)
            nc.vector.memset(warm[:], 1.0)
            nc.scalar.activation(out=warm[:], in_=warm[:], func=ACT.Ln)

            decay_rows = const.tile([P, H], BF16)
            nc.sync.dma_start(out=decay_rows[:], in_=decay.partition_broadcast(P))
            mix_w_rows = quarter_pool.tile([P, T], BF16, name="mix_w_rows", tag="quarter", align_bytes=64)
            nc.vector.memset(mix_w_rows[:].bitcast(I32), 0)
            nc.vector.memset(mix_w_rows[ONES : ONES + 32, :], 1.0)
            nc.sync.dma_start(out=mix_w_rows[0:H, :], in_=mix_w[:, :])
            w_rows = const.tile([P, P], BF16)
            nc.sync.dma_start(out=w_rows[:], in_=mix_w.rearrange("h (a q) -> (h a) q", q=P))
            load_p(0)
            b_rows = const.tile([P, P], BF16)
            out_b_rows = const.tile([P, P], BF16)
            nc.vector.memset(out_b_rows[:], 0.0)

            def iota(dst, pattern, base, channel_multiplier):
                nc.gpsimd.iota(
                    dst,
                    pattern=pattern,
                    base=base,
                    channel_multiplier=channel_multiplier,
                    allow_small_or_imprecise_dtypes=True,
                )

            identity_f32 = const.tile([P, P], F32)
            make_identity(nc, identity_f32[:])
            t_column = const.tile([P, PACK], F32)
            iota(t_column[:], [[1, PACK]], 0, PACK)
            identity_bf16 = const.tile([P, P], BF16)
            make_identity(nc, identity_bf16[:])
            s_index = const.tile([P, CHUNKS], F32)
            iota(s_index[:], [[P, CHUNKS]], 0, 1)
            t_in_block = const.tile([P, 2, HD], F32)
            iota(t_in_block[:].rearrange("q u (r e) -> q u r e", e=2), [[2, 2], [PACK, HD // 2], [1, 2]], 0, 0)
            nc.gpsimd.memset(variants[:].rearrange("q v r n -> q (v r n)").bitcast(I32), 0)
            t_row = x_pool.tile([P, K_PASS], F32, name="t_row", tag="x_raw")
            iota(t_row[0 : P // 2, :], [[2, 2], [P, BLOCKS], [PACK, HD // 2], [1, 2]], K_PASS, 0)
            iota(t_row[P // 2 : P, :], [[2, 2], [-P, BLOCKS], [PACK, HD // 2], [1, 2]], T - P, 0)
            spread = const.tile([P, 2, P], BF16)
            nc.gpsimd.memset(spread[:], 0.0)
            for odd in range(2):
                own = spread[:, odd, odd * HD : (odd + 1) * HD].rearrange("k (n r) -> k n r", r=PAIRS)
                nc.gpsimd.tensor_copy(
                    out=own[:, :, PAIRS // 2 : PAIRS],
                    in_=identity_bf16[:, HALF_H + odd : H : 2].unsqueeze(1).to_broadcast([P, PAIRS, PAIRS // 2]),
                )
                nc.gpsimd.tensor_copy(
                    out=own[:, :, 0 : PAIRS // 2],
                    in_=identity_bf16[:, ONES : ONES + 1].unsqueeze(2).to_broadcast([P, PAIRS, PAIRS // 2]),
                )

            reversed_identity = const.tile([P, P], F32)
            nc.vector.tensor_copy(
                out=reversed_identity[:].rearrange("q (a r) -> q a r", a=BLOCKS),
                in_=identity_f32[:].rearrange("q (a r) -> q a r", a=BLOCKS)[:, ::-1, :],
            )
            d_clipped = const.tile([P, H], F32)
            nc.vector.tensor_scalar(
                out=d_clipped[:], in0=decay_rows[:], scalar1=0.9, scalar2=1.0, op0=ALU.max, op1=ALU.min
            )
            log_d = const.tile([P, H], F32)
            nc.scalar.activation(out=log_d[:], in_=d_clipped[:], func=ACT.Ln)
            left_columns = const.tile([P, PAIRS, 2, PACK], F32)
            nc.vector.tensor_tensor(
                out=left_columns[:].rearrange("m r h k -> m (r h) k"),
                in0=t_column[:].unsqueeze(1).to_broadcast([P, H, PACK]),
                in1=log_d[:].unsqueeze(2).to_broadcast([P, H, PACK]),
                op=ALU.mult,
            )
            nc.scalar.activation(out=left_columns[:], in_=left_columns[:], func=ACT.Exp, scale=-0.5)

            def spread_left(pair):
                for odd in range(2):
                    bank = psum_misc.tile([P, PACK, P], F32, name="left_spread", tag="misc")
                    for k in range(PACK):
                        nc.tensor.transpose(
                            out=bank[:, k, :],
                            in_=left_columns[:, pair, odd, k : k + 1].to_broadcast([P, P]),
                            identity=reversed_identity[:] if odd else identity_f32[:],
                        )
                    (nc.scalar.copy if odd or pair > 1 else nc.vector.tensor_copy)(
                        out=left_rows[:, odd, pair, :, odd, :].rearrange("p u (m e) -> p u m e", e=2),
                        in_=bank[:].rearrange("p (u e) m -> p u m e", u=2),
                    )

            nc.sync.dma_start(out=b_rows[:], in_=mix_b.rearrange("h (a q) -> (h a) q", q=P))
            nc.sync.dma_start(out=out_b_rows[0 : E // P, :], in_=out_b.rearrange("(i q) -> i q", q=P))
            load_out_w(0)

            right = const.tile([P, H, CHUNKS], F32)
            nc.vector.tensor_tensor(
                out=right[:],
                in0=s_index[:].unsqueeze(1).to_broadcast([P, H, CHUNKS]),
                in1=log_d[:].unsqueeze(2).to_broadcast([P, H, CHUNKS]),
                op=ALU.mult,
            )
            nc.scalar.activation(out=right[:], in_=right[:], func=ACT.Exp, scale=0.5)

            triangles = const.tile([P, 2, 2 * HD], BF16)
            nc.vector.tensor_scalar(
                out=triangles[:].rearrange("q u (n v) -> q u n v", n=2),
                in0=t_in_block[:].unsqueeze(2).to_broadcast([P, 2, 2, HD]),
                scalar1=s_index[:, 0:1],
                scalar2=None,
                op0=ALU.is_le,
            )

            w_columns = psum_mix.tile([P, PACK, P], BF16, name="w_columns", tag="mixed")
            for k in range(PACK):
                nc.tensor.transpose(
                    out=w_columns[:, k, :], in_=mix_w_rows[:, k:K_PASS:PACK], identity=identity_bf16[:]
                )
            for pair in range(2):
                spread_left(pair)
            w_turned = psum_misc.tile([P, H, CHUNKS], BF16, name="w_turned", tag="misc")
            nc.tensor.transpose(
                out=w_turned[:].rearrange("q h i -> q (h i)"), in_=w_rows[:], identity=identity_bf16[:]
            )

            nc.vector.tensor_tensor(
                out=right[:, 0:HALF_H, :], in0=right[:, 0:HALF_H, :], in1=w_turned[:, 0:HALF_H, :], op=ALU.mult
            )
            late_columns = left_columns[:, PAIRS // 2 : PAIRS, :, :]
            nc.vector.tensor_tensor(
                out=late_columns,
                in0=late_columns,
                in1=w_columns[:, :, HALF_H:H].rearrange("m k (r h) -> m r h k", h=2),
                op=ALU.mult,
            )
            parked = out[B - 1, T // 2 : T // 2 + 256, :].rearrange("t v -> (t v)")

            def decay_left():
                own_head = const.tile([P, 2, PAIRS], F32)
                nc.vector.tensor_reduce(
                    out=own_head[:],
                    in_=identity_f32[:].rearrange("q (h n r) -> q h r n", h=2, r=PAIRS),
                    op=ALU.add,
                    axis=AX.X,
                )
                own_logs = const.tile([P, 2, PAIRS], F32)
                nc.vector.tensor_tensor(
                    out=own_logs[:],
                    in0=log_d[:].rearrange("q (r h) -> q h r", h=2),
                    in1=own_head[:],
                    op=ALU.mult,
                )
                own_log = const.tile([P, 1], F32)
                nc.vector.tensor_reduce(out=own_log[:], in_=own_logs[:], op=ALU.add, axis=AX.XY)
                own_rate = const.tile([P, 1], F32)
                nc.vector.tensor_scalar(out=own_rate[:], in0=own_log[:], scalar1=-0.5, scalar2=None, op0=ALU.mult)
                nc.scalar.activation(out=t_row[:], in_=t_row[:], func=ACT.Exp, scale=own_rate[:, 0:1])

            def prepare_left():
                own_w = psum_misc.tile([P, K_PASS], F32, name="own_w", tag="misc")
                weights = mix_w_rows[:, K_PASS:T]
                nc.tensor.matmul(
                    out=own_w[:].rearrange("q (u n e) -> q u n e", u=2, e=2),
                    lhsT=spread[:, 0, :],
                    rhs=weights.rearrange("k (n u e) -> k u n e", u=2, e=2),
                    start=True,
                    stop=False,
                )
                for a in range(BLOCKS):
                    nc.tensor.matmul(
                        out=own_w[:].rearrange("q (u a r e) -> q a u r e", u=2, a=BLOCKS, e=2)[:, BLOCKS - 1 - a],
                        lhsT=spread[:, 1, :],
                        rhs=weights.rearrange("k (a r u e) -> k a u r e", a=BLOCKS, u=2, e=2)[:, a],
                        start=False,
                        stop=(a == BLOCKS - 1),
                    )
                left_parts = x_pool.tile([P, K_PASS], F32, name="left_parts", tag="x_raw")
                nc.vector.tensor_tensor(out=left_parts[:], in0=own_w[:], in1=t_row[:], op=ALU.mult)
                copies = parked.rearrange("(h n q v) -> h n q v", h=2, q=HD, v=K_PASS)
                for n in range(COPIES * PAIRS // HD):
                    for odd in range(2):
                        nc.sync.dma_start(out=copies[odd, n], in_=left_parts[odd * HD : (odd + 1) * HD, :])

            bias_by_s = const.tile([P, H, CHUNKS], F32)
            out_b_column = const.tile([P, E // P], F32)

            def turn_biases():
                b_turned = psum_misc.tile([P, P], BF16, name="b_turned", tag="misc")
                nc.tensor.transpose(out=b_turned[:], in_=b_rows[:], identity=identity_bf16[:])
                nc.vector.tensor_copy(out=bias_by_s[:].rearrange("q h i -> q (h i)"), in_=b_turned[:])
                out_b_turned = psum_misc.tile([P, P], BF16, name="out_b_turned", tag="misc")
                nc.tensor.transpose(out=out_b_turned[:], in_=out_b_rows[:], identity=identity_bf16[:])
                nc.vector.tensor_copy(out=out_b_column[:], in_=out_b_turned[:, 0 : E // P])

            for part in range(4):
                regroup_p(part, 0, nc.vector.tensor_copy)
                regroup_p(part, 1, nc.scalar.copy)
                if part == 2:
                    quantise_p(0)
                    turn_biases()
            quantise_p(2)
            last_turn = -1

            project_at = [min(item, 20) + 11 + (item > 20) + (item > 22) for item in range(ITEMS)]
            turn_at = [item + 16 if item < 17 else (31 + (item - 14) // 2 + (item > 19)) for item in range(ITEMS)]
            for step in range(-3, STEPS + 8):
                turn = (step - 5) // 4 if step % 4 == 1 else -1
                if step in range(5, 9):
                    load_left(step - 5)
                if step == 1:
                    load_p(1)
                for item in range(ITEMS):
                    if turn_at[item] == step + 2:
                        load_x(item)
                if step == 25:
                    nc.sync.dma_start(out=out_b_everywhere(), in_=out_b.partition_broadcast(P))
                if 26 <= step < 30:
                    load_last_x(2 * (step - 26))
                quantise_m(step)
                mask_m(step + 2)
                make_m(step + 3)
                for item in range(ITEMS):
                    if project_at[item] + 1 == step:
                        add_out_b(item)
                for item in range(ITEMS):
                    if turn_at[item] + 1 == step:
                        add_x_and_store(item)
                part = step + 7 if step < 1 else step + 4
                if step < 1 or 4 <= step < 12:
                    regroup_p(part, 0, nc.vector.tensor_copy)
                    regroup_p(part, 1, nc.scalar.copy)
                transpose_m(step + 1, True)
                if step < STEPS:
                    for item in range(ITEMS):
                        if project_at[item] == step:
                            project(item)
                transpose_m(step + 1, False)
                transpose_c(turn)
                for item in range(ITEMS):
                    if turn_at[item] == step:
                        turn_back(item)
                if step + 5 in range(2, PAIRS):
                    spread_left(step + 5)
                if step == 1:
                    decay_left()
                if step == -1:
                    load_out_w(1)
                if step == 3:
                    prepare_left()
                if step in (0, 2, 4, 6):
                    regroup_out_w(step // 2, nc.scalar.copy if step == 6 else nc.vector.tensor_copy)
                if step in (1, 3, 5, 7):
                    quantise_out_w(step // 2)
                    if step < 5:
                        load_out_w(2 + step // 2)
                if (-3 < step <= 1 or 4 < step <= 12) and last_part % 2 == 1:
                    quantise_p(last_part - 1)
                last_part = part
                quantise_c(last_turn, slice(0, 2))
                last_turn = turn if turn < SWEEPS * GROUPS - 1 else -1
                if turn == SWEEPS * GROUPS - 1:
                    quantise_c(turn, slice(0, 1))
                    quantise_c(turn, slice(1, 2))
                add_bias(step - 1)
                multiply(step)
                for when, c, v, first, last in VARIANT_COPIES:
                    if when == step:
                        copy_variants(c, v, slice(first, last))
                for item in range(ITEMS):
                    if project_at[item] == step >= STEPS:
                        project(item)
                if STEPS + 2 <= step < STEPS + 6:
                    project_last(2 * (step - STEPS - 2))
                    project_last(2 * (step - STEPS - 2) + 1)
                if 28 <= step < 32:
                    add_out_b_to_x(2 * (step - 28))
                if STEPS + 3 <= step < STEPS + 7:
                    finish_last(2 * (step - STEPS - 3))
                    finish_last(2 * (step - STEPS - 3) + 1)
